import numpy as np
import ml_dtypes


def mxq(x, axis, fmt="e4m3"):
    dtype, down = {"e4m3": (ml_dtypes.float8_e4m3fn, 7), "e5m2": (ml_dtypes.float8_e5m2, 14)}[fmt]
    v = np.moveaxis(np.asarray(x, np.float32).astype(ml_dtypes.bfloat16).astype(np.float64), axis, -1)
    blocks = v.reshape(v.shape[:-1] + (-1, 32))
    amax = np.abs(blocks).max(-1, keepdims=True)
    byte = np.maximum(np.where(amax > 0, np.frexp(amax)[1] - 1 + 127, 0) - down, 1)
    scale = np.exp2(byte - 127.0)
    codes = (blocks / scale).astype(np.float32).astype(dtype).astype(np.float64)
    return np.moveaxis((codes * scale).reshape(v.shape), -1, axis)


WIDE = False


def mx_kscale(k):
    if not WIDE:
        return np.ones(k)
    levels = np.array([10, -10, 5, -5, 0])
    a = np.random.permutation(np.resize(levels, k // 512 * 4)).reshape(k // 512, 4)
    idx = np.arange(k)
    return np.exp2(a[idx // 512, idx % 128 // 32])


BF16 = ml_dtypes.bfloat16


def bf(x):
    return np.asarray(x, np.float32).astype(BF16)


def f64(x):
    return np.asarray(x).astype(np.float64)


B, NC, APC, D = 4096, 1, 512, 512
H = 2 * D
LN_EPS = 1e-5


def setup_inputs():
    s = mx_kscale(APC)
    t = np.exp2(np.round(np.log2(mx_kscale(H)) / 2))
    return {"tri": bf(np.random.standard_normal((B, APC * NC)) * np.repeat(s, NC)),
            "W1": bf(np.random.standard_normal((NC, APC, H)) / np.sqrt(APC) / s[None, :, None] * t),
            "b1": bf(np.random.standard_normal((NC, H)) * 0.1 * t),
            "W2": bf(np.random.standard_normal((NC, H, D)) / np.sqrt(H) / (t * t)[None, :, None]),
            "b2": bf(np.random.standard_normal((NC, D)) * 0.1),
            "gamma": bf(1.0 + 0.1 * np.random.standard_normal((NC, D))),
            "beta": bf(np.random.standard_normal((NC, D)) * 0.1)}


def reference(tri, W1, b1, W2, b2, gamma, beta):
    tri, W1, b1, W2, b2, gamma, beta = f64(tri), f64(W1), f64(b1), f64(W2), f64(b2), f64(gamma), f64(beta)
    b, n_anchors = tri.shape
    n_comp, apc, _ = W1.shape
    d = W2.shape[2]
    x = np.transpose(tri.reshape(b, apc, n_comp), (2, 0, 1))
    h = (mxq(x, 2, "e4m3") @ mxq(W1, 1, "e4m3")) + b1[:, None, :]
    h = np.square(np.maximum(h, 0.0))
    y = (mxq(h, 2, "e4m3") @ mxq(W2, 1, "e4m3")) + b2[:, None, :]
    mu = np.mean(y, axis=-1, keepdims=True)
    var = np.mean(np.square(y - mu), axis=-1, keepdims=True)
    y = (y - mu) * (1.0 / np.sqrt(var + LN_EPS))
    y = y * gamma[:, None, :] + beta[:, None, :]
    return np.transpose(y, (1, 0, 2)).reshape(b, n_comp * d)

@@ -1,0 +1,243 @@
+from contextlib import ExitStack
+
+import concourse.mybir as mybir
+from concourse.masks import make_identity
+
+F32 = mybir.dt.float32
+BF16 = mybir.dt.bfloat16
+U32 = mybir.dt.uint32
+U8 = mybir.dt.uint8
+FP8X4 = mybir.dt.float8_e4m3fn_x4
+ACT = mybir.ActivationFunctionType
+ALU = mybir.AluOpType
+
+P = 128
+B, K1, H, D = 4096, 512, 1024, 512
+CH = 512
+NCH = B // CH
+BT = CH // P
+LN_EPS = 1e-5
+
+FLOPS = 2 * B * K1 * H + 2 * B * H * D
+
+V_H1 = (1, 3, 5)
+
+
+def tile_patchwork_t_kernel(tc, tri, W1, b1, W2, b2, gamma, beta, out):
+    nc = tc.nc
+    with ExitStack() as ctx:
+        keep = ctx.enter_context(tc.tile_pool(name="keep", bufs=1))
+        tpool = ctx.enter_context(tc.tile_pool(name="tpool", bufs=2))
+        rpool = ctx.enter_context(tc.tile_pool(name="rpool", bufs=3))
+        hpool = ctx.enter_context(tc.tile_pool(name="hpool", bufs=3))
+        cpool = ctx.enter_context(tc.tile_pool(name="cpool", bufs=2))
+        ypool = ctx.enter_context(tc.tile_pool(name="ypool", bufs=2))
+        opool = ctx.enter_context(tc.tile_pool(name="opool", bufs=3))
+        spool = ctx.enter_context(tc.tile_pool(name="spool", bufs=3))
+        ptr = ctx.enter_context(tc.psum_pool(name="ptr", bufs=2))
+        ph = ctx.enter_context(tc.psum_pool(name="ph", bufs=4))
+        py = ctx.enter_context(tc.psum_pool(name="py", bufs=2))
+
+        epst = keep.tile([P, 1], F32, name="epst")
+        nc.vector.memset(epst[:], LN_EPS)
+        warm = keep.tile([P, 1], F32, name="warm")
+        nc.scalar.activation(out=warm[:], in_=epst[:], func=ACT.Sqrt)
+        ident = keep.tile([P, P], F32, name="ident")
+        make_identity(nc, ident[:])
+        ones = keep.tile([P, P], BF16, name="ones")
+        nc.vector.memset(ones[:], 1.0)
+        vec = keep.tile([P, 3 * D], BF16, name="vec")
+        nc.vector.memset(vec[:], 0.0)
+
+        traw = keep.tile([P, NCH, BT * K1], BF16, name="traw")
+
+        def load_tri(c):
+            nc.sync.dma_start(
+                out=traw[:, c, :],
+                in_=tri[c * CH:(c + 1) * CH, :].rearrange("(p t) k -> p (t k)", t=BT),
+            )
+
+        w1v = W1.rearrange("o k h -> (o k) h")
+        w2v = W2.rearrange("o k d -> (o k) d")
+        w1raw = keep.tile([P, 4, H], BF16, name="w1raw")
+        w2raw = keep.tile([P, 2, 4, D], BF16, name="w2raw")
+        b1raw = keep.tile([P, 2, 4], BF16, name="b1raw")
+
+        load_tri(0)
+        for u in range(2):
+            nc.sync.dma_start(
+                out=w1raw[:, 2 * u:2 * u + 2, :],
+                in_=w1v[256 * u:256 * (u + 1), :].rearrange("(q e) h -> q e h", e=2),
+            )
+        nc.scalar.dma_start(out=b1raw[:], in_=b1.rearrange("o (g p t) -> p (o g) t", g=2, t=4))
+        for j, v in enumerate((b2, gamma, beta)):
+            nc.scalar.dma_start(out=vec[0:1, j * D:(j + 1) * D], in_=v)
+        load_tri(1)
+        nc.sync.dma_start(out=w2raw[:], in_=w2v.rearrange("(g p t) d -> p g t d", g=2, t=4))
+        for c in range(2, NCH):
+            load_tri(c)
+
+        b1f = keep.tile([P, 8], F32, name="b1f")
+        nc.vector.tensor_copy(out=b1f[:], in_=b1raw[:].rearrange("p g t -> p (g t)"))
+
+        bc = keep.tile([P, 3, D], F32, name="bc")
+        for j in range(3):
+            pb = py.tile([P, D], F32, name="pb", tag="y")
+            nc.tensor.matmul(out=pb[:], lhsT=ones[:], rhs=vec[:, j * D:(j + 1) * D], start=True, stop=True)
+            nc.scalar.copy(out=bc[:, j, :], in_=pb[:])
+
+        w1g = keep.tile([P, 4 * H], BF16, name="w1g", align_bytes=64)
+        w1c = keep.tile([P, H], U32, name="w1c", align_bytes=64)
+        w1s = keep.tile([P, H], U8, name="w1s", align_bytes=64)
+        w2g = keep.tile([P, 2, D, 4], BF16, name="w2g", align_bytes=64)
+        w2c = keep.tile([P, 2, D], U32, name="w2c", align_bytes=64)
+        w2s = keep.tile([P, 2, D], U8, name="w2s", align_bytes=64)
+
+        def prep_w1():
+            for g in range(2):
+                nc.vector.tensor_copy(
+                    out=w1g[:, g * 2048:(g + 1) * 2048].rearrange("p (t q j) -> p t q j", t=4, q=P, j=4),
+                    in_=w1raw[:, :, g * 512:(g + 1) * 512].rearrange("p j (q t) -> p t q j", t=4),
+                )
+            for g in range(2):
+                nc.vector.quantize_mx(
+                    out=w1c[:, g * 512:(g + 1) * 512].bitcast(FP8X4),
+                    scales=w1s[:, g * 512:(g + 1) * 512],
+                    in_=w1g[:, g * 2048:(g + 1) * 2048],
+                )
+
+        def prep_w2():
+            for g in range(2):
+                nc.vector.tensor_copy(
+                    out=w2g[:, g, :, :],
+                    in_=w2raw[:, g, :, :].rearrange("p t d -> p d t"),
+                )
+            for g in range(2):
+                nc.vector.quantize_mx(
+                    out=w2c[:, g, :].bitcast(FP8X4),
+                    scales=w2s[:, g, :],
+                    in_=w2g[:, g, :, :].rearrange("p d t -> p (d t)"),
+                )
+
+        tq = {}
+        hq = {}
+
+        def stage_t(c):
+            tg = tpool.tile([P, 2 * CH], F32, name="tg", tag="tg", align_bytes=64)
+            words = traw[:, c, :].bitcast(F32)
+            for hf in range(2):
+                trp = ptr.tile([P, 2, 256], F32, name="trp", tag="tr")
+                for j in range(2):
+                    t = 2 * hf + j
+                    for u in range(2):
+                        nc.tensor.transpose(
+                            trp[:, u, j * P:(j + 1) * P],
+                            words[:, t * 256 + u * P:t * 256 + (u + 1) * P],
+                            ident[:],
+                        )
+                nc.scalar.copy(
+                    out=tg[:, hf * 512:(hf + 1) * 512].rearrange("p (w u) -> p w u", u=2),
+                    in_=trp[:].rearrange("p u w -> p w u"),
+                )
+            tcod = tpool.tile([P, CH], U32, name="tcod", tag="tcod", align_bytes=64)
+            tscl = tpool.tile([P, CH], U8, name="tscl", tag="tscl", align_bytes=64)
+            nc.vector.quantize_mx(out=tcod[:].bitcast(FP8X4), scales=tscl[:], in_=tg[:].bitcast(BF16))
+            tq[c] = (tcod, tscl)
+
+        def stage_m1(c):
+            tcod, tscl = tq[c]
+            hcod = cpool.tile([P, 2, CH], U32, name="hcod", tag="hcod", align_bytes=64)
+            hscl = cpool.tile([P, 2, CH], U8, name="hscl", tag="hscl", align_bytes=64)
+            for g in range(2):
+                r = rpool.tile([P, 4, CH], F32, name="r", tag="r")
+                for t in range(4):
+                    m = 4 * g + t
+                    hp = ph.tile([P, CH], F32, name="hp", tag="h")
+                    nc.tensor.matmul_mx(
+                        out=hp[:],
+                        lhsT=w1c[:, m * P:(m + 1) * P].bitcast(FP8X4),
+                        lhsT_scale=w1s[:, m * P:(m + 1) * P],
+                        rhs=tcod[:].bitcast(FP8X4),
+                        rhs_scale=tscl[:],
+                        start=True,
+                        stop=True,
+                    )
+                    if m in V_H1:
+                        nc.vector.tensor_scalar(
+                            out=r[:, t, :], in0=hp[:], scalar1=b1f[:, m:m + 1], scalar2=0.0,
+                            op0=ALU.add, op1=ALU.max,
+                        )
+                    else:
+                        nc.scalar.activation(out=r[:, t, :], in_=hp[:], func=ACT.Relu, bias=b1f[:, m:m + 1], scale=1.0)
+                hb = hpool.tile([P, CH, 4], BF16, name="hb", tag="hb", align_bytes=64)
+                nc.scalar.activation(
+                    out=hb[:].rearrange("p (c i) t -> p c t i", i=4),
+                    in_=r[:].rearrange("p t (c i) -> p c t i", i=4),
+                    func=ACT.Square,
+                )
+                nc.vector.quantize_mx(
+                    out=hcod[:, g, :].bitcast(FP8X4),
+                    scales=hscl[:, g, :],
+                    in_=hb[:].rearrange("p w t -> p (w t)"),
+                )
+            hq[c] = (hcod, hscl)
+
+        def stage_m2(c):
+            hcod, hscl = hq[c]
+            y = ypool.tile([P, BT, D], F32, name="y", tag="y")
+            o = opool.tile([P, BT, D], F32, name="o", tag="o")
+            sums = spool.tile([P, BT], F32, name="sums", tag="sums")
+            negmu = spool.tile([P, BT], F32, name="negmu", tag="negmu")
+            ssq = spool.tile([P, BT], F32, name="ssq", tag="ssq")
+            std = spool.tile([P, BT], F32, name="std", tag="std")
+            rstd = spool.tile([P, BT], F32, name="rstd", tag="rstd")
+            for t in range(BT):
+                yp = py.tile([P, D], F32, name="yp", tag="y")
+                for g in range(2):
+                    nc.tensor.matmul_mx(
+                        out=yp[:],
+                        lhsT=hcod[:, g, t * P:(t + 1) * P].bitcast(FP8X4),
+                        lhsT_scale=hscl[:, g, t * P:(t + 1) * P],
+                        rhs=w2c[:, g, :].bitcast(FP8X4),
+                        rhs_scale=w2s[:, g, :],
+                        start=(g == 0),
+                        stop=(g == 1),
+                    )
+                nc.vector.scalar_tensor_tensor(
+                    out=y[:, t, :], in0=yp[:], scalar=0.0, in1=bc[:, 0, :],
+                    op0=ALU.add, op1=ALU.add, accum_out=sums[:, t:t + 1],
+                )
+            nc.vector.tensor_scalar(out=negmu[:], in0=sums[:], scalar1=-1.0 / D, scalar2=None, op0=ALU.mult)
+            for t in range(BT):
+                junk = spool.tile([P, D], BF16, name="junk", tag="junk")
+                nc.scalar.activation(
+                    out=junk[:], in_=y[:, t, :], func=ACT.Square, bias=negmu[:, t:t + 1], scale=1.0,
+                    accum_out=ssq[:, t:t + 1],
+                )
+            for t in range(BT):
+                nc.vector.scalar_tensor_tensor(
+                    out=o[:, t, :], in0=y[:, t, :], scalar=negmu[:, t:t + 1], in1=bc[:, 1, :],
+                    op0=ALU.add, op1=ALU.mult,
+                )
+            nc.scalar.activation(out=std[:], in_=ssq[:], func=ACT.Sqrt, bias=epst[:, 0:1], scale=1.0 / D)
+            nc.vector.reciprocal(out=rstd[:], in_=std[:])
+            for t in range(BT):
+                nc.vector.scalar_tensor_tensor(
+                    out=o[:, t, :], in0=o[:, t, :], scalar=rstd[:, t:t + 1], in1=bc[:, 2, :],
+                    op0=ALU.mult, op1=ALU.add,
+                )
+            nc.sync.dma_start(
+                out=out[c * CH:(c + 1) * CH, :].rearrange("(p t) d -> p t d", t=BT),
+                in_=o[:],
+            )
+
+        prep_w1()
+        for s in range(NCH + 2):
+            if s < NCH:
+                stage_t(s)
+            if s == 1:
+                prep_w2()
+            if 0 <= s - 1 < NCH:
+                stage_m1(s - 1)
+            if 0 <= s - 2 < NCH:
+                stage_m2(s - 2)

@@ -20,36 +20,52 @@ LN_EPS = 1e-5
 
 FLOPS = 2 * B * K1 * H + 2 * B * H * D
 
-V_H1 = (1, 3, 5)
+GX = 256
 
 
 def tile_patchwork_t_kernel(tc, tri, W1, b1, W2, b2, gamma, beta, out):
     nc = tc.nc
     with ExitStack() as ctx:
         keep = ctx.enter_context(tc.tile_pool(name="keep", bufs=1))
-        tpool = ctx.enter_context(tc.tile_pool(name="tpool", bufs=2))
+        tgpool = ctx.enter_context(tc.tile_pool(name="tgpool", bufs=2))
+        tcpool = ctx.enter_context(tc.tile_pool(name="tcpool", bufs=3))
         rpool = ctx.enter_context(tc.tile_pool(name="rpool", bufs=3))
-        hpool = ctx.enter_context(tc.tile_pool(name="hpool", bufs=3))
+        hpool = ctx.enter_context(tc.tile_pool(name="hpool", bufs=1))
         cpool = ctx.enter_context(tc.tile_pool(name="cpool", bufs=2))
         ypool = ctx.enter_context(tc.tile_pool(name="ypool", bufs=2))
         opool = ctx.enter_context(tc.tile_pool(name="opool", bufs=3))
         spool = ctx.enter_context(tc.tile_pool(name="spool", bufs=3))
-        ptr = ctx.enter_context(tc.psum_pool(name="ptr", bufs=2))
-        ph = ctx.enter_context(tc.psum_pool(name="ph", bufs=4))
+        pgb = ctx.enter_context(tc.psum_pool(name="pgb", bufs=1))
+        ptr = ctx.enter_context(tc.psum_pool(name="ptr", bufs=1))
+        ph = ctx.enter_context(tc.psum_pool(name="ph", bufs=3))
         py = ctx.enter_context(tc.psum_pool(name="py", bufs=2))
 
-        epst = keep.tile([P, 1], F32, name="epst")
-        nc.vector.memset(epst[:], LN_EPS)
-        warm = keep.tile([P, 1], F32, name="warm")
-        nc.scalar.activation(out=warm[:], in_=epst[:], func=ACT.Sqrt)
-        ident = keep.tile([P, P], F32, name="ident")
-        make_identity(nc, ident[:])
-        ones = keep.tile([P, P], BF16, name="ones")
-        nc.vector.memset(ones[:], 1.0)
-        vec = keep.tile([P, 3 * D], BF16, name="vec")
-        nc.vector.memset(vec[:], 0.0)
-
         traw = keep.tile([P, NCH, BT * K1], BF16, name="traw")
+        w1raw = keep.tile([P, 4, H], BF16, name="w1raw")
+        w2raw = keep.tile([P, 2, 4, D], BF16, name="w2raw")
+        b1raw = keep.tile([P, 2, 4], BF16, name="b1raw")
+        b1f = keep.tile([P, 8], F32, name="b1f")
+        vec = keep.tile([P, 3 * D], BF16, name="vec")
+        ones = keep.tile([P, P], BF16, name="ones")
+        ident = keep.tile([P, P], F32, name="ident")
+        epst = keep.tile([P, 1], F32, name="epst")
+        warm = keep.tile([P, 1], F32, name="warm")
+        b2b = keep.tile([P, D], F32, name="b2b")
+        junk = keep.tile([P, D], BF16, name="junk")
+        w1g = keep.tile([P, 4 * H], BF16, name="w1g", align_bytes=64)
+        w1c = keep.tile([P, H], U32, name="w1c", align_bytes=64)
+        w1s = keep.tile([P, H], U8, name="w1s", align_bytes=64)
+        w2g = keep.tile([P, 2, D, 4], BF16, name="w2g", align_bytes=64)
+        w2c = keep.tile([P, 2 * D], U32, name="w2c", align_bytes=64)
+        w2s = keep.tile([P, 2 * D], U8, name="w2s", align_bytes=64)
+        gam = pgb.tile([P, D], F32, name="gam")
+        bet = pgb.tile([P, D], F32, name="bet")
+
+        make_identity(nc, ident[:])
+        ctx.enter_context(tc.manual_schedule())
+
+        w1v = W1.rearrange("o k h -> (o k) h")
+        w2v = W2.rearrange("o k d -> (o k) d")
 
         def load_tri(c):
             nc.sync.dma_start(
@@ -57,187 +73,327 @@ def tile_patchwork_t_kernel(tc, tri, W1, b1, W2, b2, gamma, beta, out):
                 in_=tri[c * CH:(c + 1) * CH, :].rearrange("(p t) k -> p (t k)", t=BT),
             )
 
-        w1v = W1.rearrange("o k h -> (o k) h")
-        w2v = W2.rearrange("o k d -> (o k) d")
-        w1raw = keep.tile([P, 4, H], BF16, name="w1raw")
-        w2raw = keep.tile([P, 2, 4, D], BF16, name="w2raw")
-        b1raw = keep.tile([P, 2, 4], BF16, name="b1raw")
+        def load_w1(g):
+            for u in range(2):
+                nc.sync.dma_start(
+                    out=w1raw[:, 2 * u:2 * u + 2, g * 512:(g + 1) * 512],
+                    in_=w1v[256 * u:256 * (u + 1), g * 512:(g + 1) * 512].rearrange("(q e) h -> q e h", e=2),
+                )
 
-        load_tri(0)
-        for u in range(2):
-            nc.sync.dma_start(
-                out=w1raw[:, 2 * u:2 * u + 2, :],
-                in_=w1v[256 * u:256 * (u + 1), :].rearrange("(q e) h -> q e h", e=2),
+        def regroup_w1(g):
+            nc.vector.tensor_copy(
+                out=w1g[:, g * 2048:(g + 1) * 2048].rearrange("p (t q j) -> p t q j", t=4, q=P, j=4),
+                in_=w1raw[:, :, g * 512:(g + 1) * 512].rearrange("p j (q t) -> p t q j", t=4),
             )
+
+        def quant_w1(g):
+            nc.vector.quantize_mx(
+                out=w1c[:, g * 512:(g + 1) * 512].bitcast(FP8X4),
+                scales=w1s[:, g * 512:(g + 1) * 512],
+                in_=w1g[:, g * 2048:(g + 1) * 2048],
+            )
+
+        def regroup_w2(g):
+            nc.gpsimd.tensor_scalar(
+                out=w2g[:, g, :, :], in0=w2raw[:, g, :, :].rearrange("p t d -> p d t"),
+                scalar1=1.0, scalar2=0.0, op0=ALU.mult, op1=ALU.add,
+            )
+
+        def quant_w2():
+            nc.vector.quantize_mx(
+                out=w2c[:].bitcast(FP8X4), scales=w2s[:], in_=w2g[:].rearrange("p g d t -> p (g d t)"),
+            )
+
+        def spread_vectors():
+            pb = py.tile([P, D], F32, name="pb", tag="y")
+            nc.tensor.matmul(out=pb[:], lhsT=ones[:], rhs=vec[:, 0:D], start=True, stop=True)
+            nc.tensor.matmul(out=gam[:], lhsT=ones[:], rhs=vec[:, D:2 * D], start=True, stop=True)
+            nc.tensor.matmul(out=bet[:], lhsT=ones[:], rhs=vec[:, 2 * D:3 * D], start=True, stop=True)
+            nc.scalar.copy(out=b2b[:], in_=pb[:])
+
+        live = {}
+
+        def ok(c):
+            return 0 <= c < NCH
+
+        def op_t(c, hf):
+            if not ok(c):
+                return
+            words = traw[:, c, :].bitcast(F32)
+            trp = ptr.tile([P, 2, 256], F32, name="trp", tag="tr")
+            live["trp", c, hf] = trp
+            for j in range(2):
+                t = 2 * hf + j
+                for u in range(2):
+                    nc.tensor.transpose(
+                        trp[:, u, j * P:(j + 1) * P],
+                        words[:, t * 256 + u * P:t * 256 + (u + 1) * P],
+                        ident[:],
+                    )
+
+        def op_a(c, hf):
+            if not ok(c):
+                return
+            if hf == 0:
+                live["tg", c] = tgpool.tile([P, 2 * CH], F32, name="tg", tag="tg", align_bytes=64)
+            dst = live["tg", c][:, hf * 512:(hf + 1) * 512].rearrange("p (w u) -> p w u", u=2)
+            src = live["trp", c, hf][:].rearrange("p u w -> p w u")
+            if c == 1:
+                nc.vector.tensor_copy(out=dst, in_=src)
+            else:
+                nc.scalar.copy(out=dst, in_=src)
+
+        def op_qt(c):
+            if not ok(c):
+                return
+            tcod = tcpool.tile([P, CH], U32, name="tcod", tag="tcod", align_bytes=64)
+            tscl = tcpool.tile([P, CH], U8, name="tscl", tag="tscl", align_bytes=64)
+            nc.vector.quantize_mx(out=tcod[:].bitcast(FP8X4), scales=tscl[:], in_=live["tg", c][:].bitcast(BF16))
+            live["tq", c] = (tcod, tscl)
+
+        def op_mm1(c, m):
+            if not ok(c):
+                return
+            tcod, tscl = live["tq", c]
+            hp = ph.tile([P, CH], F32, name="hp", tag="h")
+            live["hp", c, m] = hp
+            nc.tensor.matmul_mx(
+                out=hp[:],
+                lhsT=w1c[:, m * P:(m + 1) * P].bitcast(FP8X4),
+                lhsT_scale=w1s[:, m * P:(m + 1) * P],
+                rhs=tcod[:].bitcast(FP8X4),
+                rhs_scale=tscl[:],
+                start=True,
+                stop=True,
+            )
+
+        def op_h1(c, m):
+            if not ok(c):
+                return
+            g, t = divmod(m, 4)
+            if t == 0:
+                live["r", c, g] = rpool.tile([P, 4, CH], F32, name="r", tag="r")
+            r = live["r", c, g]
+            hp = live["hp", c, m]
+            if c == 0 and g == 1:
+                nc.vector.tensor_scalar(
+                    out=r[:, t, :], in0=hp[:], scalar1=b1f[:, m:m + 1], scalar2=0.0, op0=ALU.add, op1=ALU.max,
+                )
+            else:
+                nc.scalar.activation(out=r[:, t, :], in_=hp[:], func=ACT.Relu, bias=b1f[:, m:m + 1], scale=1.0)
+
+        def square_s(c, g, w0, w1):
+            nc.scalar.activation(
+                out=live["hb", c][:, g, w0:w1, :].rearrange("p (c i) t -> p c t i", i=4),
+                in_=live["r", c, g][:, :, w0:w1].rearrange("p t (c i) -> p c t i", i=4),
+                func=ACT.Square,
+            )
+
+        def square_g(c, g, w0, w1):
+            src = live["r", c, g][:, :, w0:w1].rearrange("p t w -> p w t")
+            nc.gpsimd.tensor_tensor(out=live["hb", c][:, g, w0:w1, :], in0=src, in1=src, op=ALU.mult)
+
+        def op_h2(c, piece):
+            if not ok(c):
+                return
+            if piece == 0:
+                live["hb", c] = hpool.tile([P, 2, CH, 4], BF16, name="hb", tag="hb", align_bytes=64)
+            if c == 0:
+                if piece < 2:
+                    square_s(c, piece, 0, CH)
+            elif piece == 0:
+                square_g(c, 0, 0, CH)
+            elif piece == 1:
+                square_g(c, 1, 0, GX)
+            else:
+                square_s(c, 1, GX, CH)
+
+        def op_qh(c):
+            if not ok(c):
+                return
+            hcod = cpool.tile([P, 2 * CH], U32, name="hcod", tag="hcod", align_bytes=64)
+            hscl = cpool.tile([P, 2 * CH], U8, name="hscl", tag="hscl", align_bytes=64)
+            nc.vector.quantize_mx(
+                out=hcod[:].bitcast(FP8X4), scales=hscl[:], in_=live["hb", c][:].rearrange("p g w t -> p (g w t)"),
+            )
+            live["hq", c] = (hcod, hscl)
+
+        def op_mm2(c, t):
+            if not ok(c):
+                return
+            hcod, hscl = live["hq", c]
+            yp = py.tile([P, D], F32, name="yp", tag="y")
+            live["yp", c, t] = yp
+            for g in range(2):
+                col = g * CH + t * P
+                nc.tensor.matmul_mx(
+                    out=yp[:],
+                    lhsT=hcod[:, col:col + P].bitcast(FP8X4),
+                    lhsT_scale=hscl[:, col:col + P],
+                    rhs=w2c[:, g * D:(g + 1) * D].bitcast(FP8X4),
+                    rhs_scale=w2s[:, g * D:(g + 1) * D],
+                    start=(g == 0),
+                    stop=(g == 1),
+                )
+
+        def op_l1(c, t):
+            if not ok(c):
+                return
+            if t == 0:
+                live["y", c] = ypool.tile([P, BT, D], F32, name="y", tag="y")
+                live["sums", c] = spool.tile([P, BT], F32, name="sums", tag="sums")
+            nc.vector.scalar_tensor_tensor(
+                out=live["y", c][:, t, :], in0=live["yp", c, t][:], scalar=0.0, in1=b2b[:],
+                op0=ALU.add, op1=ALU.add, accum_out=live["sums", c][:, t:t + 1],
+            )
+
+        def op_nm(c):
+            if not ok(c):
+                return
+            live["negmu", c] = spool.tile([P, BT], F32, name="negmu", tag="negmu")
+            nc.vector.tensor_scalar(
+                out=live["negmu", c][:], in0=live["sums", c][:], scalar1=-1.0 / D, scalar2=None, op0=ALU.mult,
+            )
+
+        def op_l2(c, t):
+            if not ok(c):
+                return
+            if t == 0:
+                live["ssq", c] = spool.tile([P, BT], F32, name="ssq", tag="ssq")
+            nc.scalar.activation(
+                out=junk[:], in_=live["y", c][:, t, :], func=ACT.Square, bias=live["negmu", c][:, t:t + 1], scale=1.0,
+                accum_out=live["ssq", c][:, t:t + 1],
+            )
+
+        def op_sq(c):
+            if not ok(c):
+                return
+            live["std", c] = spool.tile([P, BT], F32, name="std", tag="std")
+            nc.scalar.activation(
+                out=live["std", c][:], in_=live["ssq", c][:], func=ACT.Sqrt, bias=epst[:, 0:1], scale=1.0 / D,
+            )
+
+        def op_l3(c, t):
+            if not ok(c):
+                return
+            if t == 0:
+                live["o", c] = opool.tile([P, BT, D], F32, name="o", tag="o")
+            nc.vector.scalar_tensor_tensor(
+                out=live["o", c][:, t, :], in0=live["y", c][:, t, :], scalar=live["negmu", c][:, t:t + 1], in1=gam[:],
+                op0=ALU.add, op1=ALU.mult,
+            )
+
+        def op_rc(c):
+            if not ok(c):
+                return
+            live["rstd", c] = spool.tile([P, BT], F32, name="rstd", tag="rstd")
+            nc.vector.reciprocal(out=live["rstd", c][:], in_=live["std", c][:])
+
+        def op_l4(c, t):
+            if not ok(c):
+                return
+            o = live["o", c]
+            nc.vector.scalar_tensor_tensor(
+                out=o[:, t, :], in0=o[:, t, :], scalar=live["rstd", c][:, t:t + 1], in1=bet[:],
+                op0=ALU.mult, op1=ALU.add,
+            )
+
+        def op_st(c):
+            if not ok(c):
+                return
+            nc.sync.dma_start(
+                out=out[c * CH:(c + 1) * CH, :].rearrange("(p t) d -> p t d", t=BT),
+                in_=live["o", c][:],
+            )
+
+        load_w1(0)
+        load_tri(0)
+        load_w1(1)
+        nc.sync.dma_start(out=w2raw[:], in_=w2v.rearrange("(g p t) d -> p g t d", g=2, t=4))
+        for c in range(1, NCH):
+            load_tri(c)
+        nc.vector.memset(vec[:], 0.0)
         nc.scalar.dma_start(out=b1raw[:], in_=b1.rearrange("o (g p t) -> p (o g) t", g=2, t=4))
         for j, v in enumerate((b2, gamma, beta)):
             nc.scalar.dma_start(out=vec[0:1, j * D:(j + 1) * D], in_=v)
-        load_tri(1)
-        nc.sync.dma_start(out=w2raw[:], in_=w2v.rearrange("(g p t) d -> p g t d", g=2, t=4))
-        for c in range(2, NCH):
-            load_tri(c)
+        nc.vector.memset(epst[:], LN_EPS)
+        nc.vector.memset(ones[:], 1.0)
+        nc.scalar.activation(out=warm[:], in_=epst[:], func=ACT.Sqrt)
 
-        b1f = keep.tile([P, 8], F32, name="b1f")
+        regroup_w1(0)
+        quant_w1(0)
         nc.vector.tensor_copy(out=b1f[:], in_=b1raw[:].rearrange("p g t -> p (g t)"))
+        op_t(0, 0)
+        op_a(0, 0)
+        op_t(0, 1)
+        op_a(0, 1)
+        regroup_w1(1)
+        op_qt(0)
+        quant_w1(1)
+        regroup_w2(0)
+        regroup_w2(1)
+        for m in range(3):
+            op_mm1(0, m)
+        for m in range(5):
+            op_h1(0, m)
+            op_mm1(0, m + 3)
+        for m in range(5, 8):
+            op_h1(0, m)
+        op_h2(0, 0)
+        op_t(1, 0)
+        op_a(1, 0)
+        op_t(1, 1)
+        op_a(1, 1)
+        op_h2(0, 1)
+        op_qt(1)
+        spread_vectors()
+        quant_w2()
+        for m in range(3):
+            op_mm1(1, m)
 
-        bc = keep.tile([P, 3, D], F32, name="bc")
-        for j in range(3):
-            pb = py.tile([P, D], F32, name="pb", tag="y")
-            nc.tensor.matmul(out=pb[:], lhsT=ones[:], rhs=vec[:, j * D:(j + 1) * D], start=True, stop=True)
-            nc.scalar.copy(out=bc[:, j, :], in_=pb[:])
-
-        w1g = keep.tile([P, 4 * H], BF16, name="w1g", align_bytes=64)
-        w1c = keep.tile([P, H], U32, name="w1c", align_bytes=64)
-        w1s = keep.tile([P, H], U8, name="w1s", align_bytes=64)
-        w2g = keep.tile([P, 2, D, 4], BF16, name="w2g", align_bytes=64)
-        w2c = keep.tile([P, 2, D], U32, name="w2c", align_bytes=64)
-        w2s = keep.tile([P, 2, D], U8, name="w2s", align_bytes=64)
-
-        def prep_w1():
-            for g in range(2):
-                nc.vector.tensor_copy(
-                    out=w1g[:, g * 2048:(g + 1) * 2048].rearrange("p (t q j) -> p t q j", t=4, q=P, j=4),
-                    in_=w1raw[:, :, g * 512:(g + 1) * 512].rearrange("p j (q t) -> p t q j", t=4),
-                )
-            for g in range(2):
-                nc.vector.quantize_mx(
-                    out=w1c[:, g * 512:(g + 1) * 512].bitcast(FP8X4),
-                    scales=w1s[:, g * 512:(g + 1) * 512],
-                    in_=w1g[:, g * 2048:(g + 1) * 2048],
-                )
-
-        def prep_w2():
-            for g in range(2):
-                nc.vector.tensor_copy(
-                    out=w2g[:, g, :, :],
-                    in_=w2raw[:, g, :, :].rearrange("p t d -> p d t"),
-                )
-            for g in range(2):
-                nc.vector.quantize_mx(
-                    out=w2c[:, g, :].bitcast(FP8X4),
-                    scales=w2s[:, g, :],
-                    in_=w2g[:, g, :, :].rearrange("p d t -> p (d t)"),
-                )
-
-        tq = {}
-        hq = {}
-
-        def stage_t(c):
-            tg = tpool.tile([P, 2 * CH], F32, name="tg", tag="tg", align_bytes=64)
-            words = traw[:, c, :].bitcast(F32)
-            for hf in range(2):
-                trp = ptr.tile([P, 2, 256], F32, name="trp", tag="tr")
-                for j in range(2):
-                    t = 2 * hf + j
-                    for u in range(2):
-                        nc.tensor.transpose(
-                            trp[:, u, j * P:(j + 1) * P],
-                            words[:, t * 256 + u * P:t * 256 + (u + 1) * P],
-                            ident[:],
-                        )
-                nc.scalar.copy(
-                    out=tg[:, hf * 512:(hf + 1) * 512].rearrange("p (w u) -> p w u", u=2),
-                    in_=trp[:].rearrange("p u w -> p w u"),
-                )
-            tcod = tpool.tile([P, CH], U32, name="tcod", tag="tcod", align_bytes=64)
-            tscl = tpool.tile([P, CH], U8, name="tscl", tag="tscl", align_bytes=64)
-            nc.vector.quantize_mx(out=tcod[:].bitcast(FP8X4), scales=tscl[:], in_=tg[:].bitcast(BF16))
-            tq[c] = (tcod, tscl)
-
-        def stage_m1(c):
-            tcod, tscl = tq[c]
-            hcod = cpool.tile([P, 2, CH], U32, name="hcod", tag="hcod", align_bytes=64)
-            hscl = cpool.tile([P, 2, CH], U8, name="hscl", tag="hscl", align_bytes=64)
-            for g in range(2):
-                r = rpool.tile([P, 4, CH], F32, name="r", tag="r")
-                for t in range(4):
-                    m = 4 * g + t
-                    hp = ph.tile([P, CH], F32, name="hp", tag="h")
-                    nc.tensor.matmul_mx(
-                        out=hp[:],
-                        lhsT=w1c[:, m * P:(m + 1) * P].bitcast(FP8X4),
-                        lhsT_scale=w1s[:, m * P:(m + 1) * P],
-                        rhs=tcod[:].bitcast(FP8X4),
-                        rhs_scale=tscl[:],
-                        start=True,
-                        stop=True,
-                    )
-                    if m in V_H1:
-                        nc.vector.tensor_scalar(
-                            out=r[:, t, :], in0=hp[:], scalar1=b1f[:, m:m + 1], scalar2=0.0,
-                            op0=ALU.add, op1=ALU.max,
-                        )
-                    else:
-                        nc.scalar.activation(out=r[:, t, :], in_=hp[:], func=ACT.Relu, bias=b1f[:, m:m + 1], scale=1.0)
-                hb = hpool.tile([P, CH, 4], BF16, name="hb", tag="hb", align_bytes=64)
-                nc.scalar.activation(
-                    out=hb[:].rearrange("p (c i) t -> p c t i", i=4),
-                    in_=r[:].rearrange("p t (c i) -> p c t i", i=4),
-                    func=ACT.Square,
-                )
-                nc.vector.quantize_mx(
-                    out=hcod[:, g, :].bitcast(FP8X4),
-                    scales=hscl[:, g, :],
-                    in_=hb[:].rearrange("p w t -> p (w t)"),
-                )
-            hq[c] = (hcod, hscl)
-
-        def stage_m2(c):
-            hcod, hscl = hq[c]
-            y = ypool.tile([P, BT, D], F32, name="y", tag="y")
-            o = opool.tile([P, BT, D], F32, name="o", tag="o")
-            sums = spool.tile([P, BT], F32, name="sums", tag="sums")
-            negmu = spool.tile([P, BT], F32, name="negmu", tag="negmu")
-            ssq = spool.tile([P, BT], F32, name="ssq", tag="ssq")
-            std = spool.tile([P, BT], F32, name="std", tag="std")
-            rstd = spool.tile([P, BT], F32, name="rstd", tag="rstd")
+        for c in range(NCH + 1):
+            if c > 0:
+                op_h1(c, 4)
+                op_mm1(c, 7)
+                op_h1(c, 5)
+                op_mm1(c + 1, 0)
+            op_t(c + 2, 0)
+            if c > 0:
+                op_h1(c, 6)
+                op_mm1(c + 1, 1)
+                op_h1(c, 7)
+                op_mm1(c + 1, 2)
+                op_h2(c, 1)
+            op_a(c + 2, 0)
+            op_t(c + 2, 1)
+            if c > 0:
+                op_h2(c, 2)
+            op_a(c + 2, 1)
+            for m in range(4):
+                op_h1(c + 1, m)
+                if m < 3:
+                    op_mm1(c + 1, m + 3)
             for t in range(BT):
-                yp = py.tile([P, D], F32, name="yp", tag="y")
-                for g in range(2):
-                    nc.tensor.matmul_mx(
-                        out=yp[:],
-                        lhsT=hcod[:, g, t * P:(t + 1) * P].bitcast(FP8X4),
-                        lhsT_scale=hscl[:, g, t * P:(t + 1) * P],
-                        rhs=w2c[:, g, :].bitcast(FP8X4),
-                        rhs_scale=w2s[:, g, :],
-                        start=(g == 0),
-                        stop=(g == 1),
-                    )
-                nc.vector.scalar_tensor_tensor(
-                    out=y[:, t, :], in0=yp[:], scalar=0.0, in1=bc[:, 0, :],
-                    op0=ALU.add, op1=ALU.add, accum_out=sums[:, t:t + 1],
-                )
-            nc.vector.tensor_scalar(out=negmu[:], in0=sums[:], scalar1=-1.0 / D, scalar2=None, op0=ALU.mult)
+                op_l2(c - 1, t)
+            op_sq(c - 1)
+            op_qh(c)
+            op_qt(c + 2)
+            op_h2(c + 1, 0)
+            op_mm2(c, 0)
+            op_mm1(c + 1, 6)
+            op_mm2(c, 1)
+            op_l3(c - 1, 0)
+            op_l3(c - 1, 1)
+            op_l1(c, 0)
+            op_mm2(c, 2)
+            op_l1(c, 1)
+            op_mm2(c, 3)
+            op_l3(c - 1, 2)
+            op_l3(c - 1, 3)
+            op_l1(c, 2)
+            op_l1(c, 3)
+            op_nm(c)
+            op_rc(c - 1)
             for t in range(BT):
-                junk = spool.tile([P, D], BF16, name="junk", tag="junk")
-                nc.scalar.activation(
-                    out=junk[:], in_=y[:, t, :], func=ACT.Square, bias=negmu[:, t:t + 1], scale=1.0,
-                    accum_out=ssq[:, t:t + 1],
-                )
-            for t in range(BT):
-                nc.vector.scalar_tensor_tensor(
-                    out=o[:, t, :], in0=y[:, t, :], scalar=negmu[:, t:t + 1], in1=bc[:, 1, :],
-                    op0=ALU.add, op1=ALU.mult,
-                )
-            nc.scalar.activation(out=std[:], in_=ssq[:], func=ACT.Sqrt, bias=epst[:, 0:1], scale=1.0 / D)
-            nc.vector.reciprocal(out=rstd[:], in_=std[:])
-            for t in range(BT):
-                nc.vector.scalar_tensor_tensor(
-                    out=o[:, t, :], in0=o[:, t, :], scalar=rstd[:, t:t + 1], in1=bc[:, 2, :],
-                    op0=ALU.mult, op1=ALU.add,
-                )
-            nc.sync.dma_start(
-                out=out[c * CH:(c + 1) * CH, :].rearrange("(p t) d -> p t d", t=BT),
-                in_=o[:],
-            )
-
-        prep_w1()
-        for s in range(NCH + 2):
-            if s < NCH:
-                stage_t(s)
-            if s == 1:
-                prep_w2()
-            if 0 <= s - 1 < NCH:
-                stage_m1(s - 1)
-            if 0 <= s - 2 < NCH:
-                stage_m2(s - 2)
+                op_l4(c - 1, t)
+            op_st(c - 1)

@@ -13,14 +13,492 @@ ALU = mybir.AluOpType
 
 P = 128
 B, K1, H, D = 4096, 512, 1024, 512
-CH = 512
-NCH = B // CH
-BT = CH // P
 LN_EPS = 1e-5
+NBS = (4, 4, 4, 4, 4, 4, 4, 2, 2)
+OFF = (0, 4, 8, 12, 16, 20, 24, 28, 30)
+CHM = 512
 
 FLOPS = 2 * B * K1 * H + 2 * B * H * D
 
-GX = 256
+PROG = (
+    ("ld_tri", 0,),
+    ("ld_w1", 0,),
+    ("ld_w1", 1,),
+    ("ld_w2",),
+    ("ld_tri", 1,),
+    ("ld_tri", 2,),
+    ("ld_tri", 3,),
+    ("ld_tri", 4,),
+    ("ld_tri", 5,),
+    ("ld_tri", 6,),
+    ("ld_tri", 7,),
+    ("ld_tri", 8,),
+    ("start",),
+    ("t", 0, 0, "h",),
+    ("t", 0, 1, "h",),
+    ("rw1", 0, "S",),
+    ("a", 0, 0, "V",),
+    ("rw1", 1, "V",),
+    ("a", 0, 1, "S",),
+    ("b1",),
+    ("qw1", 0,),
+    ("rw2", 0, "S",),
+    ("qt", 0,),
+    ("rw2", 1, "V",),
+    ("mm1", 0, 3,),
+    ("t", 1, 0, "h",),
+    ("qw1", 1,),
+    ("t", 1, 1, "h",),
+    ("a", 1, 0, "S",),
+    ("h1", 0, 3, "V",),
+    ("mm1", 0, 0,),
+    ("qw2",),
+    ("a", 1, 1, "S",),
+    ("mm1", 0, 2,),
+    ("mm1", 0, 1,),
+    ("h1", 0, 0, "S",),
+    ("mm1", 0, 4,),
+    ("t", 2, 0, "tr",),
+    ("h1", 0, 1, "S",),
+    ("h1", 0, 2, "V",),
+    ("h1", 0, 4, "S",),
+    ("qt", 1,),
+    ("mm1", 0, 7,),
+    ("h2", 0, 0, 0, 256, "S",),
+    ("mm1", 0, 6,),
+    ("a", 2, 0, "V",),
+    ("mm1", 0, 5,),
+    ("h1", 0, 7, "V",),
+    ("mm1", 1, 1,),
+    ("t", 2, 1, "tr",),
+    ("h1", 0, 6, "S",),
+    ("h1", 0, 5, "V",),
+    ("h1", 1, 1, "S",),
+    ("h2", 0, 0, 256, 512, "V",),
+    ("mm1", 1, 0,),
+    ("mm1", 1, 7,),
+    ("a", 2, 1, "S",),
+    ("mm1", 1, 5,),
+    ("mm1", 1, 6,),
+    ("h1", 1, 0, "S",),
+    ("h2", 0, 1, 256, 512, "V",),
+    ("t", 3, 0, "tr",),
+    ("h2", 0, 1, 0, 256, "S",),
+    ("pb",),
+    ("qh", 0, 0, 0, 512,),
+    ("h1", 1, 7, "S",),
+    ("qh", 0, 1, 0, 512,),
+    ("mm1", 1, 2,),
+    ("h1", 1, 5, "S",),
+    ("mm1", 1, 3,),
+    ("cb2", "V",),
+    ("h1", 1, 6, "S",),
+    ("mm2", 0, 0,),
+    ("qt", 2,),
+    ("h1", 1, 3, "S",),
+    ("mm1", 1, 4,),
+    ("mm2", 0, 1,),
+    ("l1", 0, 0,),
+    ("h1", 1, 2, "S",),
+    ("mm1", 2, 0,),
+    ("h1", 1, 4, "S",),
+    ("l1", 0, 1,),
+    ("mm2", 0, 3,),
+    ("h2", 1, 0, 0, 512, "G",),
+    ("l2", 0, 0,),
+    ("a", 3, 0, "V",),
+    ("mm2", 0, 2,),
+    ("l2", 0, 1,),
+    ("l1", 0, 3,),
+    ("mm1", 2, 1,),
+    ("h2", 1, 1, 256, 512, "S",),
+    ("mm1", 2, 2,),
+    ("nm", 0, 0, 2,),
+    ("l1", 0, 2,),
+    ("t", 3, 1, "tr",),
+    ("l3", 0, 0,),
+    ("sq", 0, 0, 2,),
+    ("l2", 0, 2,),
+    ("mm1", 2, 3,),
+    ("nm", 0, 2, 4,),
+    ("rc", 0, 0, 2,),
+    ("l3", 0, 1,),
+    ("l2", 0, 3,),
+    ("l3", 0, 3,),
+    ("h2", 1, 1, 0, 256, "S",),
+    ("l4", 0, 0,),
+    ("l4", 0, 1,),
+    ("sq", 0, 2, 4,),
+    ("a", 3, 1, "S",),
+    ("l3", 0, 2,),
+    ("st", 0, 0, 2,),
+    ("h1", 2, 0, "S",),
+    ("rc", 0, 2, 4,),
+    ("t", 4, 0, "tr",),
+    ("qt", 3,),
+    ("h1", 2, 1, "S",),
+    ("qh", 1, 1, 0, 512,),
+    ("h1", 2, 2, "S",),
+    ("mm1", 2, 4,),
+    ("mm1", 2, 5,),
+    ("qh", 1, 0, 0, 512,),
+    ("h1", 2, 3, "S",),
+    ("mm1", 2, 6,),
+    ("l4", 0, 2,),
+    ("h1", 2, 4, "S",),
+    ("h2", 2, 0, 0, 512, "G",),
+    ("mm1", 2, 7,),
+    ("l4", 0, 3,),
+    ("mm2", 1, 0,),
+    ("h1", 2, 5, "S",),
+    ("h1", 2, 6, "S",),
+    ("mm2", 1, 1,),
+    ("st", 0, 2, 4,),
+    ("l1", 1, 0,),
+    ("h1", 2, 7, "S",),
+    ("mm1", 3, 0,),
+    ("l1", 1, 1,),
+    ("l2", 1, 0,),
+    ("mm2", 1, 2,),
+    ("mm1", 3, 1,),
+    ("nm", 1, 0, 2,),
+    ("l2", 1, 1,),
+    ("a", 4, 0, "V",),
+    ("mm2", 1, 3,),
+    ("h2", 2, 1, 0, 256, "S",),
+    ("l1", 1, 2,),
+    ("mm1", 3, 2,),
+    ("mm1", 3, 3,),
+    ("l1", 1, 3,),
+    ("t", 4, 1, "tr",),
+    ("sq", 1, 0, 2,),
+    ("l2", 1, 2,),
+    ("l3", 1, 0,),
+    ("nm", 1, 2, 4,),
+    ("l2", 1, 3,),
+    ("l3", 1, 1,),
+    ("h2", 2, 1, 256, 512, "S",),
+    ("rc", 1, 0, 2,),
+    ("l3", 1, 2,),
+    ("l3", 1, 3,),
+    ("sq", 1, 2, 4,),
+    ("a", 4, 1, "S",),
+    ("l4", 1, 0,),
+    ("h1", 3, 0, "S",),
+    ("l4", 1, 1,),
+    ("t", 5, 0, "tr",),
+    ("h1", 3, 1, "S",),
+    ("rc", 1, 2, 4,),
+    ("qt", 4,),
+    ("st", 1, 0, 2,),
+    ("h1", 3, 2, "S",),
+    ("mm1", 3, 4,),
+    ("qh", 2, 1, 0, 512,),
+    ("mm1", 3, 5,),
+    ("h1", 3, 3, "S",),
+    ("qh", 2, 0, 0, 512,),
+    ("mm1", 3, 6,),
+    ("h1", 3, 4, "S",),
+    ("mm1", 3, 7,),
+    ("l4", 1, 2,),
+    ("h2", 3, 0, 0, 512, "G",),
+    ("mm2", 2, 0,),
+    ("h1", 3, 5, "S",),
+    ("l4", 1, 3,),
+    ("h1", 3, 6, "S",),
+    ("mm2", 2, 1,),
+    ("l1", 2, 0,),
+    ("h1", 3, 7, "S",),
+    ("st", 1, 2, 4,),
+    ("mm1", 4, 0,),
+    ("l1", 2, 1,),
+    ("l2", 2, 0,),
+    ("mm2", 2, 2,),
+    ("mm1", 4, 1,),
+    ("nm", 2, 0, 2,),
+    ("l2", 2, 1,),
+    ("a", 5, 0, "V",),
+    ("mm2", 2, 3,),
+    ("h2", 3, 1, 0, 256, "S",),
+    ("l1", 2, 2,),
+    ("mm1", 4, 2,),
+    ("mm1", 4, 3,),
+    ("l1", 2, 3,),
+    ("t", 5, 1, "tr",),
+    ("sq", 2, 0, 2,),
+    ("l2", 2, 2,),
+    ("l3", 2, 0,),
+    ("nm", 2, 2, 4,),
+    ("l2", 2, 3,),
+    ("l3", 2, 1,),
+    ("h2", 3, 1, 256, 512, "S",),
+    ("rc", 2, 0, 2,),
+    ("l3", 2, 2,),
+    ("l3", 2, 3,),
+    ("sq", 2, 2, 4,),
+    ("a", 5, 1, "S",),
+    ("l4", 2, 0,),
+    ("h1", 4, 0, "S",),
+    ("l4", 2, 1,),
+    ("t", 6, 0, "tr",),
+    ("h1", 4, 1, "S",),
+    ("rc", 2, 2, 4,),
+    ("qt", 5,),
+    ("st", 2, 0, 2,),
+    ("h1", 4, 2, "S",),
+    ("mm1", 4, 4,),
+    ("qh", 3, 1, 0, 512,),
+    ("mm1", 4, 5,),
+    ("h1", 4, 3, "S",),
+    ("qh", 3, 0, 0, 512,),
+    ("mm1", 4, 6,),
+    ("h1", 4, 4, "S",),
+    ("mm1", 4, 7,),
+    ("l4", 2, 2,),
+    ("h2", 4, 0, 0, 512, "G",),
+    ("mm2", 3, 0,),
+    ("h1", 4, 5, "S",),
+    ("l4", 2, 3,),
+    ("h1", 4, 6, "S",),
+    ("mm2", 3, 1,),
+    ("l1", 3, 0,),
+    ("h1", 4, 7, "S",),
+    ("st", 2, 2, 4,),
+    ("mm1", 5, 0,),
+    ("l1", 3, 1,),
+    ("l2", 3, 0,),
+    ("mm2", 3, 2,),
+    ("mm1", 5, 1,),
+    ("nm", 3, 0, 2,),
+    ("l2", 3, 1,),
+    ("a", 6, 0, "V",),
+    ("mm2", 3, 3,),
+    ("h2", 4, 1, 0, 256, "S",),
+    ("l1", 3, 2,),
+    ("mm1", 5, 2,),
+    ("mm1", 5, 3,),
+    ("l1", 3, 3,),
+    ("t", 6, 1, "tr",),
+    ("sq", 3, 0, 2,),
+    ("l2", 3, 2,),
+    ("l3", 3, 0,),
+    ("nm", 3, 2, 4,),
+    ("l2", 3, 3,),
+    ("l3", 3, 1,),
+    ("h2", 4, 1, 256, 512, "S",),
+    ("rc", 3, 0, 2,),
+    ("l3", 3, 2,),
+    ("l3", 3, 3,),
+    ("sq", 3, 2, 4,),
+    ("a", 6, 1, "S",),
+    ("l4", 3, 0,),
+    ("h1", 5, 0, "S",),
+    ("l4", 3, 1,),
+    ("t", 7, 0, "tr",),
+    ("h1", 5, 1, "S",),
+    ("rc", 3, 2, 4,),
+    ("qt", 6,),
+    ("st", 3, 0, 2,),
+    ("h1", 5, 2, "S",),
+    ("mm1", 5, 4,),
+    ("qh", 4, 1, 0, 512,),
+    ("mm1", 5, 5,),
+    ("h1", 5, 3, "S",),
+    ("qh", 4, 0, 0, 512,),
+    ("mm1", 5, 6,),
+    ("h1", 5, 4, "S",),
+    ("mm1", 5, 7,),
+    ("l4", 3, 2,),
+    ("h2", 5, 0, 0, 512, "G",),
+    ("mm2", 4, 0,),
+    ("h1", 5, 5, "S",),
+    ("l4", 3, 3,),
+    ("h1", 5, 6, "S",),
+    ("mm2", 4, 1,),
+    ("l1", 4, 0,),
+    ("h1", 5, 7, "S",),
+    ("st", 3, 2, 4,),
+    ("mm1", 6, 0,),
+    ("l1", 4, 1,),
+    ("l2", 4, 0,),
+    ("mm2", 4, 2,),
+    ("mm1", 6, 1,),
+    ("nm", 4, 0, 2,),
+    ("l2", 4, 1,),
+    ("a", 7, 0, "V",),
+    ("mm2", 4, 3,),
+    ("h2", 5, 1, 0, 256, "S",),
+    ("l1", 4, 2,),
+    ("mm1", 6, 2,),
+    ("mm1", 6, 3,),
+    ("l1", 4, 3,),
+    ("t", 8, 0, "tr",),
+    ("sq", 4, 0, 2,),
+    ("l2", 4, 2,),
+    ("l3", 4, 0,),
+    ("nm", 4, 2, 4,),
+    ("l2", 4, 3,),
+    ("l3", 4, 1,),
+    ("h2", 5, 1, 256, 512, "S",),
+    ("rc", 4, 0, 2,),
+    ("l3", 4, 2,),
+    ("l3", 4, 3,),
+    ("sq", 4, 2, 4,),
+    ("h1", 6, 0, "S",),
+    ("l4", 4, 0,),
+    ("h1", 6, 1, "S",),
+    ("l4", 4, 1,),
+    ("mm1", 6, 4,),
+    ("h1", 6, 2, "S",),
+    ("rc", 4, 2, 4,),
+    ("qt", 7,),
+    ("mm1", 6, 5,),
+    ("st", 4, 0, 2,),
+    ("qh", 5, 1, 0, 512,),
+    ("h1", 6, 3, "S",),
+    ("mm1", 6, 6,),
+    ("qh", 5, 0, 0, 512,),
+    ("h1", 6, 4, "S",),
+    ("mm1", 6, 7,),
+    ("l4", 4, 2,),
+    ("h1", 6, 5, "S",),
+    ("h2", 6, 0, 0, 512, "G",),
+    ("mm2", 5, 0,),
+    ("h1", 6, 6, "S",),
+    ("l4", 4, 3,),
+    ("mm2", 5, 1,),
+    ("h1", 6, 7, "S",),
+    ("l1", 5, 0,),
+    ("st", 4, 2, 4,),
+    ("mm1", 7, 0,),
+    ("mm1", 7, 7,),
+    ("l1", 5, 1,),
+    ("mm1", 7, 4,),
+    ("h1", 7, 0, "S",),
+    ("mm2", 5, 2,),
+    ("l2", 5, 0,),
+    ("mm1", 7, 1,),
+    ("nm", 5, 0, 2,),
+    ("a", 8, 0, "V",),
+    ("mm2", 5, 3,),
+    ("l2", 5, 1,),
+    ("l1", 5, 2,),
+    ("mm1", 7, 2,),
+    ("h2", 6, 1, 0, 256, "S",),
+    ("l1", 5, 3,),
+    ("l3", 5, 0,),
+    ("sq", 5, 0, 2,),
+    ("h1", 7, 4, "S",),
+    ("h2", 6, 1, 256, 512, "S",),
+    ("nm", 5, 2, 4,),
+    ("l3", 5, 1,),
+    ("rc", 5, 0, 2,),
+    ("l3", 5, 2,),
+    ("l2", 5, 2,),
+    ("qt", 8,),
+    ("h1", 7, 2, "S",),
+    ("qh", 6, 1, 0, 512,),
+    ("h1", 7, 7, "S",),
+    ("h1", 7, 1, "S",),
+    ("qh", 6, 0, 0, 512,),
+    ("mm1", 7, 6,),
+    ("l2", 5, 3,),
+    ("mm1", 7, 5,),
+    ("mm1", 8, 7,),
+    ("l4", 5, 0,),
+    ("mm1", 7, 3,),
+    ("mm2", 6, 0,),
+    ("h1", 8, 7, "S",),
+    ("sq", 5, 2, 4,),
+    ("l3", 5, 3,),
+    ("h1", 7, 5, "S",),
+    ("mm2", 6, 1,),
+    ("h1", 7, 3, "S",),
+    ("l1", 6, 0,),
+    ("h1", 7, 6, "S",),
+    ("h2", 7, 0, 0, 256, "G",),
+    ("rc", 5, 2, 4,),
+    ("mm1", 8, 0,),
+    ("l1", 6, 1,),
+    ("mm1", 8, 1,),
+    ("l2", 6, 0,),
+    ("mm2", 6, 2,),
+    ("l4", 5, 1,),
+    ("h2", 7, 1, 0, 256, "S",),
+    ("mm2", 6, 3,),
+    ("nm", 6, 0, 2,),
+    ("l1", 6, 2,),
+    ("st", 5, 0, 2,),
+    ("mm1", 8, 5,),
+    ("mm1", 8, 6,),
+    ("l4", 5, 2,),
+    ("l2", 6, 1,),
+    ("l1", 6, 3,),
+    ("h1", 8, 5, "S",),
+    ("sq", 6, 0, 2,),
+    ("h1", 8, 0, "S",),
+    ("qh", 7, 1, 0, 256,),
+    ("h1", 8, 1, "S",),
+    ("qh", 7, 0, 0, 256,),
+    ("mm1", 8, 2,),
+    ("l2", 6, 3,),
+    ("l3", 6, 1,),
+    ("mm1", 8, 4,),
+    ("mm2", 7, 0,),
+    ("h1", 8, 6, "S",),
+    ("nm", 6, 2, 4,),
+    ("l3", 6, 0,),
+    ("l2", 6, 2,),
+    ("mm2", 7, 1,),
+    ("l3", 6, 2,),
+    ("h1", 8, 4, "S",),
+    ("mm1", 8, 3,),
+    ("sq", 6, 2, 4,),
+    ("h1", 8, 2, "S",),
+    ("rc", 6, 0, 2,),
+    ("l1", 7, 0,),
+    ("h1", 8, 3, "S",),
+    ("h2", 8, 1, 0, 256, "S",),
+    ("l4", 5, 3,),
+    ("l3", 6, 3,),
+    ("st", 5, 2, 4,),
+    ("h2", 8, 0, 0, 256, "S",),
+    ("l1", 7, 1,),
+    ("rc", 6, 2, 4,),
+    ("l4", 6, 1,),
+    ("l2", 7, 0,),
+    ("l4", 6, 0,),
+    ("l2", 7, 1,),
+    ("nm", 7, 0, 2,),
+    ("qh", 8, 0, 0, 256,),
+    ("st", 6, 0, 2,),
+    ("qh", 8, 1, 0, 256,),
+    ("sq", 7, 0, 2,),
+    ("l3", 7, 0,),
+    ("mm2", 8, 0,),
+    ("l4", 6, 3,),
+    ("mm2", 8, 1,),
+    ("rc", 7, 0, 2,),
+    ("l1", 8, 0,),
+    ("l1", 8, 1,),
+    ("l2", 8, 0,),
+    ("l4", 7, 0,),
+    ("l2", 8, 1,),
+    ("nm", 8, 0, 2,),
+    ("l3", 7, 1,),
+    ("sq", 8, 0, 2,),
+    ("l4", 6, 2,),
+    ("rc", 8, 0, 2,),
+    ("l4", 7, 1,),
+    ("st", 6, 2, 4,),
+    ("l3", 8, 0,),
+    ("l3", 8, 1,),
+    ("st", 7, 0, 2,),
+    ("l4", 8, 0,),
+    ("l4", 8, 1,),
+    ("st", 8, 0, 1,),
+    ("st", 8, 1, 2,),
+)
 
 
 def tile_patchwork_t_kernel(tc, tri, W1, b1, W2, b2, gamma, beta, out):
@@ -29,18 +507,19 @@ def tile_patchwork_t_kernel(tc, tri, W1, b1, W2, b2, gamma, beta, out):
         keep = ctx.enter_context(tc.tile_pool(name="keep", bufs=1))
         tgpool = ctx.enter_context(tc.tile_pool(name="tgpool", bufs=2))
         tcpool = ctx.enter_context(tc.tile_pool(name="tcpool", bufs=3))
-        rpool = ctx.enter_context(tc.tile_pool(name="rpool", bufs=3))
-        hpool = ctx.enter_context(tc.tile_pool(name="hpool", bufs=1))
+        rpool = ctx.enter_context(tc.tile_pool(name="rpool", bufs=4))
+        hpool0 = ctx.enter_context(tc.tile_pool(name="hpool0", bufs=1))
+        hpool1 = ctx.enter_context(tc.tile_pool(name="hpool1", bufs=2))
         cpool = ctx.enter_context(tc.tile_pool(name="cpool", bufs=2))
-        ypool = ctx.enter_context(tc.tile_pool(name="ypool", bufs=2))
+        ypool = ctx.enter_context(tc.tile_pool(name="ypool", bufs=3))
         opool = ctx.enter_context(tc.tile_pool(name="opool", bufs=3))
         spool = ctx.enter_context(tc.tile_pool(name="spool", bufs=3))
         pgb = ctx.enter_context(tc.psum_pool(name="pgb", bufs=1))
         ptr = ctx.enter_context(tc.psum_pool(name="ptr", bufs=1))
-        ph = ctx.enter_context(tc.psum_pool(name="ph", bufs=3))
+        ph = ctx.enter_context(tc.psum_pool(name="ph", bufs=4))
         py = ctx.enter_context(tc.psum_pool(name="py", bufs=2))
 
-        traw = keep.tile([P, NCH, BT * K1], BF16, name="traw")
+        traw = keep.tile([P, (B // P) * K1], BF16, name="traw")
         w1raw = keep.tile([P, 4, H], BF16, name="w1raw")
         w2raw = keep.tile([P, 2, 4, D], BF16, name="w2raw")
         b1raw = keep.tile([P, 2, 4], BF16, name="b1raw")
@@ -58,71 +537,87 @@ def tile_patchwork_t_kernel(tc, tri, W1, b1, W2, b2, gamma, beta, out):
         w2g = keep.tile([P, 2, D, 4], BF16, name="w2g", align_bytes=64)
         w2c = keep.tile([P, 2 * D], U32, name="w2c", align_bytes=64)
         w2s = keep.tile([P, 2 * D], U8, name="w2s", align_bytes=64)
-        gam = pgb.tile([P, D], F32, name="gam")
-        bet = pgb.tile([P, D], F32, name="bet")
+        gb = pgb.tile([P, 2 * D], BF16, name="gb")
+        gam = gb[:, 0:D]
+        bet = gb[:, D:2 * D]
 
         make_identity(nc, ident[:])
         ctx.enter_context(tc.manual_schedule())
 
         w1v = W1.rearrange("o k h -> (o k) h")
         w2v = W2.rearrange("o k d -> (o k) d")
+        live = {}
 
-        def load_tri(c):
+        def copy_on(eng, dst, src):
+            if eng == "V":
+                nc.vector.tensor_copy(out=dst, in_=src)
+            elif eng == "S":
+                nc.scalar.copy(out=dst, in_=src)
+            else:
+                nc.gpsimd.tensor_scalar(out=dst, in0=src, scalar1=1.0, scalar2=0.0, op0=ALU.mult, op1=ALU.add)
+
+        def rows(c):
+            return slice(OFF[c] * P, (OFF[c] + NBS[c]) * P)
+
+        def ld_tri(c):
             nc.sync.dma_start(
-                out=traw[:, c, :],
-                in_=tri[c * CH:(c + 1) * CH, :].rearrange("(p t) k -> p (t k)", t=BT),
+                out=traw[:, OFF[c] * K1:(OFF[c] + NBS[c]) * K1],
+                in_=tri[rows(c), :].rearrange("(p t) k -> p (t k)", t=NBS[c]),
             )
 
-        def load_w1(g):
+        def ld_w1(g):
             for u in range(2):
                 nc.sync.dma_start(
                     out=w1raw[:, 2 * u:2 * u + 2, g * 512:(g + 1) * 512],
                     in_=w1v[256 * u:256 * (u + 1), g * 512:(g + 1) * 512].rearrange("(q e) h -> q e h", e=2),
                 )
 
-        def regroup_w1(g):
-            nc.vector.tensor_copy(
-                out=w1g[:, g * 2048:(g + 1) * 2048].rearrange("p (t q j) -> p t q j", t=4, q=P, j=4),
-                in_=w1raw[:, :, g * 512:(g + 1) * 512].rearrange("p j (q t) -> p t q j", t=4),
+        def ld_w2():
+            nc.sync.dma_start(out=w2raw[:], in_=w2v.rearrange("(g p t) d -> p g t d", g=2, t=4))
+
+        def rw1(g, eng):
+            copy_on(
+                eng,
+                w1g[:, g * 2048:(g + 1) * 2048].rearrange("p (t q j) -> p t q j", t=4, q=P, j=4),
+                w1raw[:, :, g * 512:(g + 1) * 512].rearrange("p j (q t) -> p t q j", t=4),
             )
 
-        def quant_w1(g):
+        def qw1(g):
             nc.vector.quantize_mx(
                 out=w1c[:, g * 512:(g + 1) * 512].bitcast(FP8X4),
                 scales=w1s[:, g * 512:(g + 1) * 512],
                 in_=w1g[:, g * 2048:(g + 1) * 2048],
             )
 
-        def regroup_w2(g):
-            nc.gpsimd.tensor_scalar(
-                out=w2g[:, g, :, :], in0=w2raw[:, g, :, :].rearrange("p t d -> p d t"),
-                scalar1=1.0, scalar2=0.0, op0=ALU.mult, op1=ALU.add,
-            )
+        def rw2(g, eng):
+            copy_on(eng, w2g[:, g, :, :], w2raw[:, g, :, :].rearrange("p t d -> p d t"))
 
-        def quant_w2():
+        def qw2():
             nc.vector.quantize_mx(
                 out=w2c[:].bitcast(FP8X4), scales=w2s[:], in_=w2g[:].rearrange("p g d t -> p (g d t)"),
             )
 
-        def spread_vectors():
-            pb = py.tile([P, D], F32, name="pb", tag="y")
-            nc.tensor.matmul(out=pb[:], lhsT=ones[:], rhs=vec[:, 0:D], start=True, stop=True)
-            nc.tensor.matmul(out=gam[:], lhsT=ones[:], rhs=vec[:, D:2 * D], start=True, stop=True)
-            nc.tensor.matmul(out=bet[:], lhsT=ones[:], rhs=vec[:, 2 * D:3 * D], start=True, stop=True)
-            nc.scalar.copy(out=b2b[:], in_=pb[:])
+        def b1cast():
+            nc.vector.tensor_copy(out=b1f[:], in_=b1raw[:].rearrange("p g t -> p (g t)"))
 
-        live = {}
+        def pb():
+            t = py.tile([P, D], F32, name="pbt", tag="y")
+            nc.tensor.matmul(out=t[:], lhsT=ones[:], rhs=vec[:, 0:D], start=True, stop=True)
+            nc.tensor.matmul(out=gam, lhsT=ones[:], rhs=vec[:, D:2 * D], start=True, stop=True)
+            nc.tensor.matmul(out=bet, lhsT=ones[:], rhs=vec[:, 2 * D:3 * D], start=True, stop=True)
+            live["pb"] = t
 
-        def ok(c):
-            return 0 <= c < NCH
+        def cb2(eng):
+            copy_on(eng, b2b[:], live["pb"][:])
 
-        def op_t(c, hf):
-            if not ok(c):
-                return
-            words = traw[:, c, :].bitcast(F32)
-            trp = ptr.tile([P, 2, 256], F32, name="trp", tag="tr")
+        def op_t(c, hf, tag):
+            words = traw[:, OFF[c] * K1:(OFF[c] + NBS[c]) * K1].bitcast(F32)
+            if tag == "h":
+                trp = ph.tile([P, 2, 256], F32, name="trp", tag="h")
+            else:
+                trp = ptr.tile([P, 2, 256], F32, name="trp", tag="tr")
             live["trp", c, hf] = trp
-            for j in range(2):
+            for j in range(min(2, NBS[c] - 2 * hf)):
                 t = 2 * hf + j
                 for u in range(2):
                     nc.tensor.transpose(
@@ -131,269 +626,165 @@ def tile_patchwork_t_kernel(tc, tri, W1, b1, W2, b2, gamma, beta, out):
                         ident[:],
                     )
 
-        def op_a(c, hf):
-            if not ok(c):
-                return
+        def op_a(c, hf, eng):
             if hf == 0:
-                live["tg", c] = tgpool.tile([P, 2 * CH], F32, name="tg", tag="tg", align_bytes=64)
-            dst = live["tg", c][:, hf * 512:(hf + 1) * 512].rearrange("p (w u) -> p w u", u=2)
-            src = live["trp", c, hf][:].rearrange("p u w -> p w u")
-            if c == 1:
-                nc.vector.tensor_copy(out=dst, in_=src)
-            else:
-                nc.scalar.copy(out=dst, in_=src)
+                live["tg", c] = tgpool.tile([P, 2 * CHM], F32, name="tg", tag="tg", align_bytes=64)
+            w = P * min(2, NBS[c] - 2 * hf)
+            dst = live["tg", c][:, hf * 512:hf * 512 + 2 * w].rearrange("p (w u) -> p w u", u=2)
+            src = live["trp", c, hf][:, :, 0:w].rearrange("p u w -> p w u")
+            copy_on(eng, dst, src)
 
         def op_qt(c):
-            if not ok(c):
-                return
-            tcod = tcpool.tile([P, CH], U32, name="tcod", tag="tcod", align_bytes=64)
-            tscl = tcpool.tile([P, CH], U8, name="tscl", tag="tscl", align_bytes=64)
-            nc.vector.quantize_mx(out=tcod[:].bitcast(FP8X4), scales=tscl[:], in_=live["tg", c][:].bitcast(BF16))
+            n = NBS[c] * P
+            tcod = tcpool.tile([P, CHM], U32, name="tcod", tag="tcod", align_bytes=64)
+            tscl = tcpool.tile([P, CHM], U8, name="tscl", tag="tscl", align_bytes=64)
+            nc.vector.quantize_mx(
+                out=tcod[:, 0:n].bitcast(FP8X4), scales=tscl[:, 0:n], in_=live["tg", c][:, 0:2 * n].bitcast(BF16),
+            )
             live["tq", c] = (tcod, tscl)
 
         def op_mm1(c, m):
-            if not ok(c):
-                return
+            n = NBS[c] * P
             tcod, tscl = live["tq", c]
-            hp = ph.tile([P, CH], F32, name="hp", tag="h")
+            hp = ph.tile([P, CHM], F32, name="hp", tag="h")
             live["hp", c, m] = hp
             nc.tensor.matmul_mx(
-                out=hp[:],
+                out=hp[:, 0:n],
                 lhsT=w1c[:, m * P:(m + 1) * P].bitcast(FP8X4),
                 lhsT_scale=w1s[:, m * P:(m + 1) * P],
-                rhs=tcod[:].bitcast(FP8X4),
-                rhs_scale=tscl[:],
+                rhs=tcod[:, 0:n].bitcast(FP8X4),
+                rhs_scale=tscl[:, 0:n],
                 start=True,
                 stop=True,
             )
 
-        def op_h1(c, m):
-            if not ok(c):
-                return
+        def op_h1(c, m, eng):
+            n = NBS[c] * P
             g, t = divmod(m, 4)
-            if t == 0:
-                live["r", c, g] = rpool.tile([P, 4, CH], F32, name="r", tag="r")
+            if ("r", c, g) not in live:
+                live["r", c, g] = rpool.tile([P, 4, CHM], F32, name="r", tag="r")
             r = live["r", c, g]
             hp = live["hp", c, m]
-            if c == 0 and g == 1:
+            if eng == "V":
                 nc.vector.tensor_scalar(
-                    out=r[:, t, :], in0=hp[:], scalar1=b1f[:, m:m + 1], scalar2=0.0, op0=ALU.add, op1=ALU.max,
+                    out=r[:, t, 0:n], in0=hp[:, 0:n], scalar1=b1f[:, m:m + 1], scalar2=0.0, op0=ALU.add, op1=ALU.max,
                 )
             else:
-                nc.scalar.activation(out=r[:, t, :], in_=hp[:], func=ACT.Relu, bias=b1f[:, m:m + 1], scale=1.0)
+                nc.scalar.activation(out=r[:, t, 0:n], in_=hp[:, 0:n], func=ACT.Relu, bias=b1f[:, m:m + 1], scale=1.0)
 
-        def square_s(c, g, w0, w1):
-            nc.scalar.activation(
-                out=live["hb", c][:, g, w0:w1, :].rearrange("p (c i) t -> p c t i", i=4),
-                in_=live["r", c, g][:, :, w0:w1].rearrange("p t (c i) -> p c t i", i=4),
-                func=ACT.Square,
-            )
-
-        def square_g(c, g, w0, w1):
-            src = live["r", c, g][:, :, w0:w1].rearrange("p t w -> p w t")
-            nc.gpsimd.tensor_tensor(out=live["hb", c][:, g, w0:w1, :], in0=src, in1=src, op=ALU.mult)
-
-        def op_h2(c, piece):
-            if not ok(c):
-                return
-            if piece == 0:
-                live["hb", c] = hpool.tile([P, 2, CH, 4], BF16, name="hb", tag="hb", align_bytes=64)
-            if c == 0:
-                if piece < 2:
-                    square_s(c, piece, 0, CH)
-            elif piece == 0:
-                square_g(c, 0, 0, CH)
-            elif piece == 1:
-                square_g(c, 1, 0, GX)
+        def op_h2(c, g, w0, w1, eng):
+            if ("hb", c, g) not in live:
+                pool = hpool0 if g == 0 else hpool1
+                live["hb", c, g] = pool.tile([P, CHM, 4], BF16, name="hb%d" % g, tag="hb%d" % g, align_bytes=64)
+            hb = live["hb", c, g]
+            r = live["r", c, g]
+            if eng == "S":
+                nc.scalar.activation(
+                    out=hb[:, w0:w1, :].rearrange("p (c i) t -> p c t i", i=4),
+                    in_=r[:, :, w0:w1].rearrange("p t (c i) -> p c t i", i=4),
+                    func=ACT.Square,
+                )
             else:
-                square_s(c, 1, GX, CH)
+                src = r[:, :, w0:w1].rearrange("p t w -> p w t")
+                if eng == "V":
+                    nc.vector.tensor_tensor(out=hb[:, w0:w1, :], in0=src, in1=src, op=ALU.mult)
+                else:
+                    nc.gpsimd.tensor_tensor(out=hb[:, w0:w1, :], in0=src, in1=src, op=ALU.mult)
 
-        def op_qh(c):
-            if not ok(c):
-                return
-            hcod = cpool.tile([P, 2 * CH], U32, name="hcod", tag="hcod", align_bytes=64)
-            hscl = cpool.tile([P, 2 * CH], U8, name="hscl", tag="hscl", align_bytes=64)
+        def op_qh(c, g, w0, w1):
+            if ("hq", c, g) not in live:
+                hcod = cpool.tile([P, CHM], U32, name="hcod%d" % g, tag="hcod%d" % g, align_bytes=64)
+                hscl = cpool.tile([P, CHM], U8, name="hscl%d" % g, tag="hscl%d" % g, align_bytes=64)
+                live["hq", c, g] = (hcod, hscl)
+            hcod, hscl = live["hq", c, g]
             nc.vector.quantize_mx(
-                out=hcod[:].bitcast(FP8X4), scales=hscl[:], in_=live["hb", c][:].rearrange("p g w t -> p (g w t)"),
+                out=hcod[:, w0:w1].bitcast(FP8X4), scales=hscl[:, w0:w1],
+                in_=live["hb", c, g][:, w0:w1, :].rearrange("p w t -> p (w t)"),
             )
-            live["hq", c] = (hcod, hscl)
 
         def op_mm2(c, t):
-            if not ok(c):
-                return
-            hcod, hscl = live["hq", c]
             yp = py.tile([P, D], F32, name="yp", tag="y")
             live["yp", c, t] = yp
             for g in range(2):
-                col = g * CH + t * P
+                hcod, hscl = live["hq", c, g]
                 nc.tensor.matmul_mx(
                     out=yp[:],
-                    lhsT=hcod[:, col:col + P].bitcast(FP8X4),
-                    lhsT_scale=hscl[:, col:col + P],
+                    lhsT=hcod[:, t * P:(t + 1) * P].bitcast(FP8X4),
+                    lhsT_scale=hscl[:, t * P:(t + 1) * P],
                     rhs=w2c[:, g * D:(g + 1) * D].bitcast(FP8X4),
                     rhs_scale=w2s[:, g * D:(g + 1) * D],
                     start=(g == 0),
                     stop=(g == 1),
                 )
 
+        def stat(name, c):
+            if (name, c) not in live:
+                live[name, c] = spool.tile([P, 4], F32, name=name, tag=name)
+            return live[name, c]
+
         def op_l1(c, t):
-            if not ok(c):
-                return
-            if t == 0:
-                live["y", c] = ypool.tile([P, BT, D], F32, name="y", tag="y")
-                live["sums", c] = spool.tile([P, BT], F32, name="sums", tag="sums")
+            if ("y", c) not in live:
+                live["y", c] = ypool.tile([P, 4, D], F32, name="y", tag="y")
             nc.vector.scalar_tensor_tensor(
                 out=live["y", c][:, t, :], in0=live["yp", c, t][:], scalar=0.0, in1=b2b[:],
-                op0=ALU.add, op1=ALU.add, accum_out=live["sums", c][:, t:t + 1],
+                op0=ALU.add, op1=ALU.add, accum_out=stat("sums", c)[:, t:t + 1],
             )
 
-        def op_nm(c):
-            if not ok(c):
-                return
-            live["negmu", c] = spool.tile([P, BT], F32, name="negmu", tag="negmu")
+        def op_nm(c, t0, t1):
             nc.vector.tensor_scalar(
-                out=live["negmu", c][:], in0=live["sums", c][:], scalar1=-1.0 / D, scalar2=None, op0=ALU.mult,
+                out=stat("negmu", c)[:, t0:t1], in0=stat("sums", c)[:, t0:t1], scalar1=-1.0 / D, scalar2=None, op0=ALU.mult,
             )
 
         def op_l2(c, t):
-            if not ok(c):
-                return
-            if t == 0:
-                live["ssq", c] = spool.tile([P, BT], F32, name="ssq", tag="ssq")
             nc.scalar.activation(
-                out=junk[:], in_=live["y", c][:, t, :], func=ACT.Square, bias=live["negmu", c][:, t:t + 1], scale=1.0,
-                accum_out=live["ssq", c][:, t:t + 1],
+                out=junk[:], in_=live["y", c][:, t, :], func=ACT.Square, bias=stat("sums", c)[:, t:t + 1], scale=-float(D),
+                accum_out=stat("ssq", c)[:, t:t + 1],
             )
 
-        def op_sq(c):
-            if not ok(c):
-                return
-            live["std", c] = spool.tile([P, BT], F32, name="std", tag="std")
+        def op_sq(c, t0, t1):
             nc.scalar.activation(
-                out=live["std", c][:], in_=live["ssq", c][:], func=ACT.Sqrt, bias=epst[:, 0:1], scale=1.0 / D,
+                out=stat("std", c)[:, t0:t1], in_=stat("ssq", c)[:, t0:t1], func=ACT.Sqrt, bias=epst[:, 0:1],
+                scale=1.0 / (D * D * D),
             )
+
+        def op_rc(c, t0, t1):
+            nc.vector.reciprocal(out=stat("rstd", c)[:, t0:t1], in_=stat("std", c)[:, t0:t1])
 
         def op_l3(c, t):
-            if not ok(c):
-                return
-            if t == 0:
-                live["o", c] = opool.tile([P, BT, D], F32, name="o", tag="o")
+            if ("o", c) not in live:
+                live["o", c] = opool.tile([P, 4, D], F32, name="o", tag="o")
             nc.vector.scalar_tensor_tensor(
-                out=live["o", c][:, t, :], in0=live["y", c][:, t, :], scalar=live["negmu", c][:, t:t + 1], in1=gam[:],
+                out=live["o", c][:, t, :], in0=live["y", c][:, t, :], scalar=stat("negmu", c)[:, t:t + 1], in1=gam,
                 op0=ALU.add, op1=ALU.mult,
             )
 
-        def op_rc(c):
-            if not ok(c):
-                return
-            live["rstd", c] = spool.tile([P, BT], F32, name="rstd", tag="rstd")
-            nc.vector.reciprocal(out=live["rstd", c][:], in_=live["std", c][:])
-
         def op_l4(c, t):
-            if not ok(c):
-                return
             o = live["o", c]
             nc.vector.scalar_tensor_tensor(
-                out=o[:, t, :], in0=o[:, t, :], scalar=live["rstd", c][:, t:t + 1], in1=bet[:],
+                out=o[:, t, :], in0=o[:, t, :], scalar=stat("rstd", c)[:, t:t + 1], in1=bet,
                 op0=ALU.mult, op1=ALU.add,
             )
 
-        def op_st(c):
-            if not ok(c):
-                return
+        def op_st(c, t0, t1):
             nc.sync.dma_start(
-                out=out[c * CH:(c + 1) * CH, :].rearrange("(p t) d -> p t d", t=BT),
-                in_=live["o", c][:],
+                out=out[rows(c), :].rearrange("(p t) d -> p t d", t=NBS[c])[:, t0:t1, :],
+                in_=live["o", c][:, t0:t1, :],
             )
 
-        load_w1(0)
-        load_tri(0)
-        load_w1(1)
-        nc.sync.dma_start(out=w2raw[:], in_=w2v.rearrange("(g p t) d -> p g t d", g=2, t=4))
-        for c in range(1, NCH):
-            load_tri(c)
-        nc.vector.memset(vec[:], 0.0)
-        nc.scalar.dma_start(out=b1raw[:], in_=b1.rearrange("o (g p t) -> p (o g) t", g=2, t=4))
-        for j, v in enumerate((b2, gamma, beta)):
-            nc.scalar.dma_start(out=vec[0:1, j * D:(j + 1) * D], in_=v)
-        nc.vector.memset(epst[:], LN_EPS)
-        nc.vector.memset(ones[:], 1.0)
-        nc.scalar.activation(out=warm[:], in_=epst[:], func=ACT.Sqrt)
+        def start():
+            nc.vector.memset(vec[:], 0.0)
+            nc.scalar.dma_start(out=b1raw[:], in_=b1.rearrange("o (g p t) -> p (o g) t", g=2, t=4))
+            for j, v in enumerate((b2, gamma, beta)):
+                nc.scalar.dma_start(out=vec[0:1, j * D:(j + 1) * D], in_=v)
+            nc.vector.memset(epst[:], LN_EPS)
+            nc.vector.memset(ones[:], 1.0)
+            nc.scalar.activation(out=warm[:], in_=epst[:], func=ACT.Sqrt)
 
-        regroup_w1(0)
-        quant_w1(0)
-        nc.vector.tensor_copy(out=b1f[:], in_=b1raw[:].rearrange("p g t -> p (g t)"))
-        op_t(0, 0)
-        op_a(0, 0)
-        op_t(0, 1)
-        op_a(0, 1)
-        regroup_w1(1)
-        op_qt(0)
-        quant_w1(1)
-        regroup_w2(0)
-        regroup_w2(1)
-        for m in range(3):
-            op_mm1(0, m)
-        for m in range(5):
-            op_h1(0, m)
-            op_mm1(0, m + 3)
-        for m in range(5, 8):
-            op_h1(0, m)
-        op_h2(0, 0)
-        op_t(1, 0)
-        op_a(1, 0)
-        op_t(1, 1)
-        op_a(1, 1)
-        op_h2(0, 1)
-        op_qt(1)
-        spread_vectors()
-        quant_w2()
-        for m in range(3):
-            op_mm1(1, m)
-
-        for c in range(NCH + 1):
-            if c > 0:
-                op_h1(c, 4)
-                op_mm1(c, 7)
-                op_h1(c, 5)
-                op_mm1(c + 1, 0)
-            op_t(c + 2, 0)
-            if c > 0:
-                op_h1(c, 6)
-                op_mm1(c + 1, 1)
-                op_h1(c, 7)
-                op_mm1(c + 1, 2)
-                op_h2(c, 1)
-            op_a(c + 2, 0)
-            op_t(c + 2, 1)
-            if c > 0:
-                op_h2(c, 2)
-            op_a(c + 2, 1)
-            for m in range(4):
-                op_h1(c + 1, m)
-                if m < 3:
-                    op_mm1(c + 1, m + 3)
-            for t in range(BT):
-                op_l2(c - 1, t)
-            op_sq(c - 1)
-            op_qh(c)
-            op_qt(c + 2)
-            op_h2(c + 1, 0)
-            op_mm2(c, 0)
-            op_mm1(c + 1, 6)
-            op_mm2(c, 1)
-            op_l3(c - 1, 0)
-            op_l3(c - 1, 1)
-            op_l1(c, 0)
-            op_mm2(c, 2)
-            op_l1(c, 1)
-            op_mm2(c, 3)
-            op_l3(c - 1, 2)
-            op_l3(c - 1, 3)
-            op_l1(c, 2)
-            op_l1(c, 3)
-            op_nm(c)
-            op_rc(c - 1)
-            for t in range(BT):
-                op_l4(c - 1, t)
-            op_st(c - 1)
+        table = {
+            "ld_tri": ld_tri, "ld_w1": ld_w1, "ld_w2": ld_w2, "start": start, "rw1": rw1, "qw1": qw1, "rw2": rw2,
+            "qw2": qw2, "b1": b1cast, "pb": pb, "cb2": cb2, "t": op_t, "a": op_a, "qt": op_qt, "mm1": op_mm1,
+            "h1": op_h1, "h2": op_h2, "qh": op_qh, "mm2": op_mm2, "l1": op_l1, "nm": op_nm, "l2": op_l2, "sq": op_sq,
+            "rc": op_rc, "l3": op_l3, "l4": op_l4, "st": op_st,
+        }
+        for step in PROG:
+            table[step[0]](*step[1:])

@@ -14,8 +14,8 @@ ALU = mybir.AluOpType
 P = 128
 B, K1, H, D = 4096, 512, 1024, 512
 LN_EPS = 1e-5
-NBS = (4, 4, 4, 4, 4, 4, 4, 2, 2)
-OFF = (0, 4, 8, 12, 16, 20, 24, 28, 30)
+NBS = (4, 4, 4, 4, 4, 4, 4, 4)
+OFF = (0, 4, 8, 12, 16, 20, 24, 28)
 CHM = 512
 
 FLOPS = 2 * B * K1 * H + 2 * B * H * D
@@ -32,472 +32,459 @@ PROG = (
     ("ld_tri", 5,),
     ("ld_tri", 6,),
     ("ld_tri", 7,),
-    ("ld_tri", 8,),
     ("start",),
-    ("t", 0, 0, "h",),
+    ("pb",),
     ("t", 0, 1, "h",),
-    ("rw1", 0, "S",),
-    ("a", 0, 0, "V",),
-    ("rw1", 1, "V",),
-    ("a", 0, 1, "S",),
+    ("cb2", "V",),
     ("b1",),
+    ("t", 0, 0, "h",),
+    ("rw1", 0, "V",),
+    ("a", 0, 1, "S",),
+    ("rw1", 1, "S",),
+    ("a", 0, 0, "V",),
     ("qw1", 0,),
-    ("rw2", 0, "S",),
     ("qt", 0,),
-    ("rw2", 1, "V",),
-    ("mm1", 0, 3,),
-    ("t", 1, 0, "h",),
+    ("rw2", 1, "S",),
     ("qw1", 1,),
+    ("t", 1, 0, "h",),
+    ("rw2", 0, "V",),
     ("t", 1, 1, "h",),
     ("a", 1, 0, "S",),
-    ("h1", 0, 3, "V",),
     ("mm1", 0, 0,),
     ("qw2",),
-    ("a", 1, 1, "S",),
-    ("mm1", 0, 2,),
     ("mm1", 0, 1,),
-    ("h1", 0, 0, "S",),
-    ("mm1", 0, 4,),
+    ("a", 1, 1, "S",),
     ("t", 2, 0, "tr",),
-    ("h1", 0, 1, "S",),
-    ("h1", 0, 2, "V",),
-    ("h1", 0, 4, "S",),
+    ("h1", 0, 0, "S",),
     ("qt", 1,),
-    ("mm1", 0, 7,),
-    ("h2", 0, 0, 0, 256, "S",),
-    ("mm1", 0, 6,),
-    ("a", 2, 0, "V",),
+    ("mm1", 0, 2,),
+    ("h1", 0, 1, "S",),
+    ("mm1", 0, 3,),
     ("mm1", 0, 5,),
-    ("h1", 0, 7, "V",),
-    ("mm1", 1, 1,),
-    ("t", 2, 1, "tr",),
-    ("h1", 0, 6, "S",),
+    ("h1", 0, 2, "V",),
+    ("mm1", 0, 6,),
+    ("h1", 0, 3, "S",),
     ("h1", 0, 5, "V",),
-    ("h1", 1, 1, "S",),
+    ("mm1", 0, 7,),
+    ("a", 2, 0, "S",),
+    ("mm1", 0, 4,),
     ("h2", 0, 0, 256, 512, "V",),
+    ("h1", 0, 6, "S",),
     ("mm1", 1, 0,),
-    ("mm1", 1, 7,),
-    ("a", 2, 1, "S",),
-    ("mm1", 1, 5,),
-    ("mm1", 1, 6,),
+    ("t", 2, 1, "tr",),
+    ("h1", 0, 7, "S",),
+    ("h1", 0, 4, "V",),
     ("h1", 1, 0, "S",),
-    ("h2", 0, 1, 256, 512, "V",),
-    ("t", 3, 0, "tr",),
-    ("h2", 0, 1, 0, 256, "S",),
-    ("pb",),
-    ("qh", 0, 0, 0, 512,),
-    ("h1", 1, 7, "S",),
-    ("qh", 0, 1, 0, 512,),
+    ("mm1", 1, 1,),
+    ("h2", 0, 0, 0, 256, "V",),
     ("mm1", 1, 2,),
-    ("h1", 1, 5, "S",),
+    ("h2", 0, 1, 0, 256, "S",),
+    ("mm1", 1, 4,),
     ("mm1", 1, 3,),
-    ("cb2", "V",),
-    ("h1", 1, 6, "S",),
-    ("mm2", 0, 0,),
+    ("h2", 0, 1, 256, 512, "V",),
+    ("a", 2, 1, "S",),
+    ("h1", 1, 1, "S",),
+    ("t", 3, 0, "tr",),
+    ("qh", 0, 0, 0, 512,),
+    ("h1", 1, 2, "S",),
+    ("qh", 0, 1, 0, 512,),
+    ("h1", 1, 4, "S",),
+    ("mm1", 1, 7,),
+    ("mm1", 1, 5,),
     ("qt", 2,),
     ("h1", 1, 3, "S",),
-    ("mm1", 1, 4,),
+    ("mm2", 0, 0,),
+    ("a", 3, 0, "V",),
+    ("h1", 1, 7, "S",),
+    ("mm1", 1, 6,),
+    ("h2", 1, 0, 0, 512, "G",),
     ("mm2", 0, 1,),
+    ("h1", 1, 5, "S",),
     ("l1", 0, 0,),
-    ("h1", 1, 2, "S",),
-    ("mm1", 2, 0,),
-    ("h1", 1, 4, "S",),
+    ("mm1", 2, 1,),
+    ("h1", 1, 6, "S",),
+    ("mm1", 2, 2,),
     ("l1", 0, 1,),
     ("mm2", 0, 3,),
-    ("h2", 1, 0, 0, 512, "G",),
     ("l2", 0, 0,),
-    ("a", 3, 0, "V",),
-    ("mm2", 0, 2,),
-    ("l2", 0, 1,),
-    ("l1", 0, 3,),
-    ("mm1", 2, 1,),
-    ("h2", 1, 1, 256, 512, "S",),
-    ("mm1", 2, 2,),
-    ("nm", 0, 0, 2,),
-    ("l1", 0, 2,),
-    ("t", 3, 1, "tr",),
-    ("l3", 0, 0,),
-    ("sq", 0, 0, 2,),
-    ("l2", 0, 2,),
-    ("mm1", 2, 3,),
-    ("nm", 0, 2, 4,),
-    ("rc", 0, 0, 2,),
-    ("l3", 0, 1,),
-    ("l2", 0, 3,),
-    ("l3", 0, 3,),
-    ("h2", 1, 1, 0, 256, "S",),
-    ("l4", 0, 0,),
-    ("l4", 0, 1,),
-    ("sq", 0, 2, 4,),
-    ("a", 3, 1, "S",),
-    ("l3", 0, 2,),
-    ("st", 0, 0, 2,),
-    ("h1", 2, 0, "S",),
-    ("rc", 0, 2, 4,),
-    ("t", 4, 0, "tr",),
-    ("qt", 3,),
     ("h1", 2, 1, "S",),
-    ("qh", 1, 1, 0, 512,),
+    ("mm2", 0, 2,),
+    ("l1", 0, 3,),
+    ("h2", 1, 1, 0, 256, "S",),
+    ("mm1", 2, 0,),
+    ("t", 3, 1, "tr",),
+    ("l1", 0, 2,),
     ("h1", 2, 2, "S",),
+    ("mm1", 2, 3,),
+    ("nm", 0, 0, 2,),
     ("mm1", 2, 4,),
-    ("mm1", 2, 5,),
-    ("qh", 1, 0, 0, 512,),
-    ("h1", 2, 3, "S",),
+    ("h1", 2, 0, "S",),
     ("mm1", 2, 6,),
-    ("l4", 0, 2,),
+    ("l3", 0, 0,),
+    ("l2", 0, 2,),
+    ("l3", 0, 1,),
+    ("nm", 0, 2, 4,),
+    ("a", 3, 1, "S",),
+    ("h2", 1, 1, 448, 512, "G",),
+    ("l3", 0, 2,),
+    ("h2", 1, 1, 256, 448, "S",),
+    ("t", 4, 0, "tr",),
+    ("l3", 0, 3,),
+    ("l2", 0, 1,),
+    ("qh", 1, 0, 0, 512,),
+    ("mm1", 2, 5,),
+    ("qh", 1, 1, 0, 512,),
+    ("l2", 0, 3,),
+    ("a", 4, 0, "V",),
+    ("h1", 2, 3, "S",),
+    ("sq", 0, 0, 2,),
+    ("qt", 3,),
+    ("sq", 0, 2, 4,),
     ("h1", 2, 4, "S",),
-    ("h2", 2, 0, 0, 512, "G",),
     ("mm1", 2, 7,),
-    ("l4", 0, 3,),
     ("mm2", 1, 0,),
+    ("rc", 0, 0, 2,),
+    ("rc", 0, 2, 4,),
     ("h1", 2, 5, "S",),
+    ("h2", 2, 0, 0, 512, "G",),
+    ("l4", 0, 0,),
+    ("mm1", 3, 0,),
     ("h1", 2, 6, "S",),
     ("mm2", 1, 1,),
-    ("st", 0, 2, 4,),
-    ("l1", 1, 0,),
+    ("l4", 0, 1,),
     ("h1", 2, 7, "S",),
-    ("mm1", 3, 0,),
-    ("l1", 1, 1,),
-    ("l2", 1, 0,),
-    ("mm2", 1, 2,),
+    ("l1", 1, 0,),
     ("mm1", 3, 1,),
-    ("nm", 1, 0, 2,),
-    ("l2", 1, 1,),
-    ("a", 4, 0, "V",),
-    ("mm2", 1, 3,),
+    ("st", 0, 0, 2,),
+    ("h1", 3, 0, "S",),
+    ("l1", 1, 1,),
+    ("mm2", 1, 2,),
     ("h2", 2, 1, 0, 256, "S",),
-    ("l1", 1, 2,),
+    ("l4", 0, 2,),
     ("mm1", 3, 2,),
+    ("mm2", 1, 3,),
+    ("l4", 0, 3,),
+    ("l2", 1, 0,),
+    ("l1", 1, 2,),
     ("mm1", 3, 3,),
-    ("l1", 1, 3,),
+    ("st", 0, 2, 4,),
+    ("nm", 1, 0, 2,),
     ("t", 4, 1, "tr",),
-    ("sq", 1, 0, 2,),
+    ("l2", 1, 1,),
+    ("l1", 1, 3,),
     ("l2", 1, 2,),
+    ("mm1", 3, 4,),
     ("l3", 1, 0,),
     ("nm", 1, 2, 4,),
     ("l2", 1, 3,),
     ("l3", 1, 1,),
-    ("h2", 2, 1, 256, 512, "S",),
-    ("rc", 1, 0, 2,),
+    ("h2", 2, 1, 448, 512, "G",),
+    ("h2", 2, 1, 256, 448, "S",),
     ("l3", 1, 2,),
     ("l3", 1, 3,),
-    ("sq", 1, 2, 4,),
     ("a", 4, 1, "S",),
-    ("l4", 1, 0,),
-    ("h1", 3, 0, "S",),
-    ("l4", 1, 1,),
-    ("t", 5, 0, "tr",),
+    ("sq", 1, 0, 2,),
+    ("sq", 1, 2, 4,),
     ("h1", 3, 1, "S",),
-    ("rc", 1, 2, 4,),
     ("qt", 4,),
-    ("st", 1, 0, 2,),
+    ("t", 5, 0, "tr",),
     ("h1", 3, 2, "S",),
-    ("mm1", 3, 4,),
+    ("rc", 1, 0, 2,),
+    ("rc", 1, 2, 4,),
     ("qh", 2, 1, 0, 512,),
     ("mm1", 3, 5,),
     ("h1", 3, 3, "S",),
-    ("qh", 2, 0, 0, 512,),
     ("mm1", 3, 6,),
+    ("qh", 2, 0, 0, 512,),
     ("h1", 3, 4, "S",),
     ("mm1", 3, 7,),
-    ("l4", 1, 2,),
+    ("a", 5, 0, "V",),
+    ("h1", 3, 5, "S",),
     ("h2", 3, 0, 0, 512, "G",),
     ("mm2", 2, 0,),
-    ("h1", 3, 5, "S",),
-    ("l4", 1, 3,),
+    ("l4", 1, 0,),
     ("h1", 3, 6, "S",),
-    ("mm2", 2, 1,),
-    ("l1", 2, 0,),
-    ("h1", 3, 7, "S",),
-    ("st", 1, 2, 4,),
     ("mm1", 4, 0,),
-    ("l1", 2, 1,),
-    ("l2", 2, 0,),
-    ("mm2", 2, 2,),
+    ("l4", 1, 1,),
+    ("mm2", 2, 1,),
+    ("h1", 3, 7, "S",),
+    ("l1", 2, 0,),
     ("mm1", 4, 1,),
+    ("h1", 4, 0, "S",),
+    ("st", 1, 0, 2,),
+    ("l1", 2, 1,),
+    ("h2", 3, 1, 0, 256, "S",),
+    ("mm2", 2, 2,),
+    ("l4", 1, 2,),
+    ("mm1", 4, 2,),
+    ("mm2", 2, 3,),
+    ("l4", 1, 3,),
+    ("l2", 2, 0,),
+    ("mm1", 4, 3,),
+    ("l1", 2, 2,),
     ("nm", 2, 0, 2,),
     ("l2", 2, 1,),
-    ("a", 5, 0, "V",),
-    ("mm2", 2, 3,),
-    ("h2", 3, 1, 0, 256, "S",),
-    ("l1", 2, 2,),
-    ("mm1", 4, 2,),
-    ("mm1", 4, 3,),
-    ("l1", 2, 3,),
+    ("st", 1, 2, 4,),
     ("t", 5, 1, "tr",),
-    ("sq", 2, 0, 2,),
+    ("l1", 2, 3,),
     ("l2", 2, 2,),
+    ("mm1", 4, 4,),
     ("l3", 2, 0,),
     ("nm", 2, 2, 4,),
     ("l2", 2, 3,),
     ("l3", 2, 1,),
-    ("h2", 3, 1, 256, 512, "S",),
-    ("rc", 2, 0, 2,),
+    ("h2", 3, 1, 448, 512, "G",),
+    ("h2", 3, 1, 256, 448, "S",),
     ("l3", 2, 2,),
     ("l3", 2, 3,),
-    ("sq", 2, 2, 4,),
     ("a", 5, 1, "S",),
-    ("l4", 2, 0,),
-    ("h1", 4, 0, "S",),
-    ("l4", 2, 1,),
-    ("t", 6, 0, "tr",),
+    ("sq", 2, 0, 2,),
+    ("sq", 2, 2, 4,),
     ("h1", 4, 1, "S",),
-    ("rc", 2, 2, 4,),
     ("qt", 5,),
-    ("st", 2, 0, 2,),
+    ("t", 6, 0, "tr",),
     ("h1", 4, 2, "S",),
-    ("mm1", 4, 4,),
+    ("rc", 2, 0, 2,),
+    ("rc", 2, 2, 4,),
     ("qh", 3, 1, 0, 512,),
     ("mm1", 4, 5,),
     ("h1", 4, 3, "S",),
-    ("qh", 3, 0, 0, 512,),
     ("mm1", 4, 6,),
+    ("qh", 3, 0, 0, 512,),
     ("h1", 4, 4, "S",),
     ("mm1", 4, 7,),
-    ("l4", 2, 2,),
+    ("a", 6, 0, "V",),
+    ("h1", 4, 5, "S",),
     ("h2", 4, 0, 0, 512, "G",),
     ("mm2", 3, 0,),
-    ("h1", 4, 5, "S",),
-    ("l4", 2, 3,),
+    ("l4", 2, 0,),
     ("h1", 4, 6, "S",),
-    ("mm2", 3, 1,),
-    ("l1", 3, 0,),
-    ("h1", 4, 7, "S",),
-    ("st", 2, 2, 4,),
     ("mm1", 5, 0,),
-    ("l1", 3, 1,),
-    ("l2", 3, 0,),
-    ("mm2", 3, 2,),
+    ("l4", 2, 1,),
+    ("mm2", 3, 1,),
+    ("h1", 4, 7, "S",),
+    ("l1", 3, 0,),
     ("mm1", 5, 1,),
+    ("h1", 5, 0, "S",),
+    ("st", 2, 0, 2,),
+    ("l1", 3, 1,),
+    ("h2", 4, 1, 0, 256, "S",),
+    ("mm2", 3, 2,),
+    ("l4", 2, 2,),
+    ("mm1", 5, 2,),
+    ("mm2", 3, 3,),
+    ("l4", 2, 3,),
+    ("l2", 3, 0,),
+    ("mm1", 5, 3,),
+    ("l1", 3, 2,),
     ("nm", 3, 0, 2,),
     ("l2", 3, 1,),
-    ("a", 6, 0, "V",),
-    ("mm2", 3, 3,),
-    ("h2", 4, 1, 0, 256, "S",),
-    ("l1", 3, 2,),
-    ("mm1", 5, 2,),
-    ("mm1", 5, 3,),
-    ("l1", 3, 3,),
+    ("st", 2, 2, 4,),
     ("t", 6, 1, "tr",),
-    ("sq", 3, 0, 2,),
+    ("l1", 3, 3,),
     ("l2", 3, 2,),
+    ("mm1", 5, 4,),
     ("l3", 3, 0,),
     ("nm", 3, 2, 4,),
     ("l2", 3, 3,),
     ("l3", 3, 1,),
-    ("h2", 4, 1, 256, 512, "S",),
-    ("rc", 3, 0, 2,),
+    ("h2", 4, 1, 448, 512, "G",),
+    ("h2", 4, 1, 256, 448, "S",),
     ("l3", 3, 2,),
     ("l3", 3, 3,),
-    ("sq", 3, 2, 4,),
     ("a", 6, 1, "S",),
-    ("l4", 3, 0,),
-    ("h1", 5, 0, "S",),
-    ("l4", 3, 1,),
-    ("t", 7, 0, "tr",),
+    ("sq", 3, 0, 2,),
+    ("sq", 3, 2, 4,),
     ("h1", 5, 1, "S",),
-    ("rc", 3, 2, 4,),
     ("qt", 6,),
-    ("st", 3, 0, 2,),
+    ("t", 7, 0, "tr",),
     ("h1", 5, 2, "S",),
-    ("mm1", 5, 4,),
+    ("rc", 3, 0, 2,),
+    ("rc", 3, 2, 4,),
     ("qh", 4, 1, 0, 512,),
     ("mm1", 5, 5,),
     ("h1", 5, 3, "S",),
-    ("qh", 4, 0, 0, 512,),
     ("mm1", 5, 6,),
+    ("qh", 4, 0, 0, 512,),
     ("h1", 5, 4, "S",),
     ("mm1", 5, 7,),
-    ("l4", 3, 2,),
+    ("a", 7, 0, "V",),
+    ("h1", 5, 5, "S",),
     ("h2", 5, 0, 0, 512, "G",),
     ("mm2", 4, 0,),
-    ("h1", 5, 5, "S",),
-    ("l4", 3, 3,),
+    ("l4", 3, 0,),
     ("h1", 5, 6, "S",),
-    ("mm2", 4, 1,),
-    ("l1", 4, 0,),
-    ("h1", 5, 7, "S",),
-    ("st", 3, 2, 4,),
     ("mm1", 6, 0,),
-    ("l1", 4, 1,),
-    ("l2", 4, 0,),
-    ("mm2", 4, 2,),
+    ("l4", 3, 1,),
+    ("mm2", 4, 1,),
+    ("h1", 5, 7, "S",),
+    ("l1", 4, 0,),
     ("mm1", 6, 1,),
+    ("h1", 6, 0, "S",),
+    ("st", 3, 0, 2,),
+    ("l1", 4, 1,),
+    ("h2", 5, 1, 0, 256, "S",),
+    ("mm2", 4, 2,),
+    ("l4", 3, 2,),
+    ("mm1", 6, 2,),
+    ("mm2", 4, 3,),
+    ("l4", 3, 3,),
+    ("l2", 4, 0,),
+    ("mm1", 6, 3,),
+    ("l1", 4, 2,),
     ("nm", 4, 0, 2,),
     ("l2", 4, 1,),
-    ("a", 7, 0, "V",),
-    ("mm2", 4, 3,),
-    ("h2", 5, 1, 0, 256, "S",),
-    ("l1", 4, 2,),
-    ("mm1", 6, 2,),
-    ("mm1", 6, 3,),
+    ("st", 3, 2, 4,),
+    ("t", 7, 1, "tr",),
     ("l1", 4, 3,),
-    ("t", 8, 0, "tr",),
-    ("sq", 4, 0, 2,),
     ("l2", 4, 2,),
+    ("mm1", 6, 4,),
     ("l3", 4, 0,),
     ("nm", 4, 2, 4,),
     ("l2", 4, 3,),
     ("l3", 4, 1,),
-    ("h2", 5, 1, 256, 512, "S",),
-    ("rc", 4, 0, 2,),
+    ("h2", 5, 1, 448, 512, "G",),
+    ("h2", 5, 1, 256, 448, "S",),
     ("l3", 4, 2,),
     ("l3", 4, 3,),
+    ("a", 7, 1, "S",),
+    ("sq", 4, 0, 2,),
     ("sq", 4, 2, 4,),
-    ("h1", 6, 0, "S",),
-    ("l4", 4, 0,),
     ("h1", 6, 1, "S",),
-    ("l4", 4, 1,),
-    ("mm1", 6, 4,),
-    ("h1", 6, 2, "S",),
-    ("rc", 4, 2, 4,),
     ("qt", 7,),
+    ("h1", 6, 2, "S",),
+    ("rc", 4, 0, 2,),
+    ("rc", 4, 2, 4,),
     ("mm1", 6, 5,),
-    ("st", 4, 0, 2,),
     ("qh", 5, 1, 0, 512,),
     ("h1", 6, 3, "S",),
     ("mm1", 6, 6,),
     ("qh", 5, 0, 0, 512,),
     ("h1", 6, 4, "S",),
     ("mm1", 6, 7,),
-    ("l4", 4, 2,),
+    ("l4", 4, 0,),
     ("h1", 6, 5, "S",),
     ("h2", 6, 0, 0, 512, "G",),
     ("mm2", 5, 0,),
+    ("l4", 4, 1,),
     ("h1", 6, 6, "S",),
-    ("l4", 4, 3,),
+    ("mm1", 7, 0,),
     ("mm2", 5, 1,),
     ("h1", 6, 7, "S",),
+    ("st", 4, 0, 2,),
     ("l1", 5, 0,),
-    ("st", 4, 2, 4,),
-    ("mm1", 7, 0,),
-    ("mm1", 7, 7,),
-    ("l1", 5, 1,),
-    ("mm1", 7, 4,),
+    ("mm1", 7, 1,),
     ("h1", 7, 0, "S",),
     ("mm2", 5, 2,),
-    ("l2", 5, 0,),
-    ("mm1", 7, 1,),
-    ("nm", 5, 0, 2,),
-    ("a", 8, 0, "V",),
-    ("mm2", 5, 3,),
-    ("l2", 5, 1,),
-    ("l1", 5, 2,),
-    ("mm1", 7, 2,),
+    ("l1", 5, 1,),
     ("h2", 6, 1, 0, 256, "S",),
-    ("l1", 5, 3,),
-    ("l3", 5, 0,),
-    ("sq", 5, 0, 2,),
-    ("h1", 7, 4, "S",),
-    ("h2", 6, 1, 256, 512, "S",),
-    ("nm", 5, 2, 4,),
-    ("l3", 5, 1,),
-    ("rc", 5, 0, 2,),
-    ("l3", 5, 2,),
-    ("l2", 5, 2,),
-    ("qt", 8,),
-    ("h1", 7, 2, "S",),
-    ("qh", 6, 1, 0, 512,),
-    ("h1", 7, 7, "S",),
-    ("h1", 7, 1, "S",),
-    ("qh", 6, 0, 0, 512,),
-    ("mm1", 7, 6,),
-    ("l2", 5, 3,),
-    ("mm1", 7, 5,),
-    ("mm1", 8, 7,),
-    ("l4", 5, 0,),
+    ("mm1", 7, 2,),
+    ("l4", 4, 2,),
+    ("mm2", 5, 3,),
+    ("l4", 4, 3,),
+    ("l2", 5, 0,),
     ("mm1", 7, 3,),
-    ("mm2", 6, 0,),
-    ("h1", 8, 7, "S",),
-    ("sq", 5, 2, 4,),
+    ("l1", 5, 2,),
+    ("mm1", 7, 4,),
+    ("nm", 5, 0, 2,),
+    ("l2", 5, 1,),
+    ("st", 4, 2, 4,),
+    ("l1", 5, 3,),
+    ("l2", 5, 2,),
+    ("l3", 5, 0,),
+    ("nm", 5, 2, 4,),
+    ("l2", 5, 3,),
+    ("l3", 5, 1,),
+    ("h2", 6, 1, 448, 512, "G",),
+    ("h2", 6, 1, 256, 448, "S",),
+    ("l3", 5, 2,),
     ("l3", 5, 3,),
-    ("h1", 7, 5, "S",),
-    ("mm2", 6, 1,),
-    ("h1", 7, 3, "S",),
-    ("l1", 6, 0,),
-    ("h1", 7, 6, "S",),
-    ("h2", 7, 0, 0, 256, "G",),
+    ("sq", 5, 0, 2,),
+    ("sq", 5, 2, 4,),
+    ("h1", 7, 1, "S",),
+    ("rc", 5, 0, 2,),
     ("rc", 5, 2, 4,),
-    ("mm1", 8, 0,),
-    ("l1", 6, 1,),
-    ("mm1", 8, 1,),
-    ("l2", 6, 0,),
-    ("mm2", 6, 2,),
+    ("qh", 6, 1, 0, 512,),
+    ("h1", 7, 2, "S",),
+    ("mm1", 7, 5,),
+    ("qh", 6, 0, 0, 512,),
+    ("h1", 7, 3, "S",),
+    ("mm1", 7, 6,),
+    ("l4", 5, 0,),
+    ("h1", 7, 4, "S",),
+    ("h2", 7, 0, 0, 512, "G",),
+    ("mm1", 7, 7,),
+    ("mm2", 6, 0,),
+    ("h1", 7, 5, "S",),
     ("l4", 5, 1,),
-    ("h2", 7, 1, 0, 256, "S",),
-    ("mm2", 6, 3,),
-    ("nm", 6, 0, 2,),
-    ("l1", 6, 2,),
+    ("h1", 7, 6, "S",),
+    ("mm2", 6, 1,),
     ("st", 5, 0, 2,),
-    ("mm1", 8, 5,),
-    ("mm1", 8, 6,),
+    ("h1", 7, 7, "S",),
+    ("l1", 6, 0,),
+    ("l1", 6, 1,),
+    ("h2", 7, 1, 0, 256, "S",),
+    ("mm2", 6, 2,),
     ("l4", 5, 2,),
+    ("mm2", 6, 3,),
+    ("l4", 5, 3,),
+    ("l2", 6, 0,),
+    ("l1", 6, 2,),
+    ("nm", 6, 0, 2,),
     ("l2", 6, 1,),
+    ("st", 5, 2, 4,),
     ("l1", 6, 3,),
-    ("h1", 8, 5, "S",),
-    ("sq", 6, 0, 2,),
-    ("h1", 8, 0, "S",),
-    ("qh", 7, 1, 0, 256,),
-    ("h1", 8, 1, "S",),
-    ("qh", 7, 0, 0, 256,),
-    ("mm1", 8, 2,),
+    ("l2", 6, 2,),
+    ("l3", 6, 0,),
+    ("nm", 6, 2, 4,),
     ("l2", 6, 3,),
     ("l3", 6, 1,),
-    ("mm1", 8, 4,),
-    ("mm2", 7, 0,),
-    ("h1", 8, 6, "S",),
-    ("nm", 6, 2, 4,),
-    ("l3", 6, 0,),
-    ("l2", 6, 2,),
-    ("mm2", 7, 1,),
+    ("h2", 7, 1, 448, 512, "G",),
+    ("h2", 7, 1, 256, 448, "S",),
     ("l3", 6, 2,),
-    ("h1", 8, 4, "S",),
-    ("mm1", 8, 3,),
-    ("sq", 6, 2, 4,),
-    ("h1", 8, 2, "S",),
-    ("rc", 6, 0, 2,),
-    ("l1", 7, 0,),
-    ("h1", 8, 3, "S",),
-    ("h2", 8, 1, 0, 256, "S",),
-    ("l4", 5, 3,),
     ("l3", 6, 3,),
-    ("st", 5, 2, 4,),
-    ("h2", 8, 0, 0, 256, "S",),
-    ("l1", 7, 1,),
+    ("sq", 6, 0, 2,),
+    ("sq", 6, 2, 4,),
+    ("rc", 6, 0, 2,),
     ("rc", 6, 2, 4,),
-    ("l4", 6, 1,),
-    ("l2", 7, 0,),
+    ("qh", 7, 1, 0, 512,),
+    ("qh", 7, 0, 0, 512,),
     ("l4", 6, 0,),
-    ("l2", 7, 1,),
-    ("nm", 7, 0, 2,),
-    ("qh", 8, 0, 0, 256,),
+    ("mm2", 7, 0,),
+    ("l4", 6, 1,),
+    ("mm2", 7, 1,),
     ("st", 6, 0, 2,),
-    ("qh", 8, 1, 0, 256,),
-    ("sq", 7, 0, 2,),
-    ("l3", 7, 0,),
-    ("mm2", 8, 0,),
-    ("l4", 6, 3,),
-    ("mm2", 8, 1,),
-    ("rc", 7, 0, 2,),
-    ("l1", 8, 0,),
-    ("l1", 8, 1,),
-    ("l2", 8, 0,),
-    ("l4", 7, 0,),
-    ("l2", 8, 1,),
-    ("nm", 8, 0, 2,),
-    ("l3", 7, 1,),
-    ("sq", 8, 0, 2,),
+    ("l1", 7, 0,),
+    ("l1", 7, 1,),
+    ("l2", 7, 0,),
+    ("mm2", 7, 2,),
     ("l4", 6, 2,),
-    ("rc", 8, 0, 2,),
-    ("l4", 7, 1,),
+    ("mm2", 7, 3,),
+    ("nm", 7, 0, 2,),
+    ("l2", 7, 1,),
+    ("l4", 6, 3,),
+    ("l1", 7, 2,),
     ("st", 6, 2, 4,),
-    ("l3", 8, 0,),
-    ("l3", 8, 1,),
-    ("st", 7, 0, 2,),
-    ("l4", 8, 0,),
-    ("l4", 8, 1,),
-    ("st", 8, 0, 1,),
-    ("st", 8, 1, 2,),
+    ("l1", 7, 3,),
+    ("l2", 7, 2,),
+    ("l3", 7, 0,),
+    ("nm", 7, 2, 4,),
+    ("l2", 7, 3,),
+    ("l3", 7, 1,),
+    ("sq", 7, 0, 2,),
+    ("l3", 7, 2,),
+    ("sq", 7, 2, 4,),
+    ("l3", 7, 3,),
+    ("rc", 7, 0, 2,),
+    ("rc", 7, 2, 4,),
+    ("l4", 7, 0,),
+    ("l4", 7, 1,),
+    ("st", 7, 0, 1,),
+    ("l4", 7, 2,),
+    ("st", 7, 1, 2,),
+    ("l4", 7, 3,),
+    ("st", 7, 2, 3,),
+    ("st", 7, 3, 4,),
 )
 
 
@@ -627,7 +614,7 @@ def tile_patchwork_t_kernel(tc, tri, W1, b1, W2, b2, gamma, beta, out):
                     )
 
         def op_a(c, hf, eng):
-            if hf == 0:
+            if ("tg", c) not in live:
                 live["tg", c] = tgpool.tile([P, 2 * CHM], F32, name="tg", tag="tg", align_bytes=64)
             w = P * min(2, NBS[c] - 2 * hf)
             dst = live["tg", c][:, hf * 512:hf * 512 + 2 * w].rearrange("p (w u) -> p w u", u=2)
@@ -731,8 +718,8 @@ def tile_patchwork_t_kernel(tc, tri, W1, b1, W2, b2, gamma, beta, out):
             )
 
         def op_nm(c, t0, t1):
-            nc.vector.tensor_scalar(
-                out=stat("negmu", c)[:, t0:t1], in0=stat("sums", c)[:, t0:t1], scalar1=-1.0 / D, scalar2=None, op0=ALU.mult,
+            nc.scalar.activation(
+                out=stat("negmu", c)[:, t0:t1], in_=stat("sums", c)[:, t0:t1], func=ACT.Copy, scale=-1.0 / D,
             )
 
         def op_l2(c, t):

@@ -13,479 +13,13 @@ ALU = mybir.AluOpType
 
 P = 128
 B, K1, H, D = 4096, 512, 1024, 512
+CH = 512
+NCH = B // CH
+BT = CH // P
 LN_EPS = 1e-5
-NBS = (4, 4, 4, 4, 4, 4, 4, 4)
-OFF = (0, 4, 8, 12, 16, 20, 24, 28)
-CHM = 512
+GCOLS = 96
 
 FLOPS = 2 * B * K1 * H + 2 * B * H * D
-
-PROG = (
-    ("ld_tri", 0,),
-    ("ld_w1", 0,),
-    ("ld_w1", 1,),
-    ("ld_w2",),
-    ("ld_tri", 1,),
-    ("ld_tri", 2,),
-    ("ld_tri", 3,),
-    ("ld_tri", 4,),
-    ("ld_tri", 5,),
-    ("ld_tri", 6,),
-    ("ld_tri", 7,),
-    ("start",),
-    ("pb",),
-    ("t", 0, 1, "h",),
-    ("cb2", "V",),
-    ("b1",),
-    ("t", 0, 0, "h",),
-    ("rw1", 0, "V",),
-    ("a", 0, 1, "S",),
-    ("rw1", 1, "S",),
-    ("a", 0, 0, "V",),
-    ("qw1", 0,),
-    ("qt", 0,),
-    ("rw2", 1, "S",),
-    ("qw1", 1,),
-    ("t", 1, 0, "h",),
-    ("rw2", 0, "V",),
-    ("t", 1, 1, "h",),
-    ("a", 1, 0, "S",),
-    ("mm1", 0, 0,),
-    ("qw2",),
-    ("mm1", 0, 1,),
-    ("a", 1, 1, "S",),
-    ("t", 2, 0, "tr",),
-    ("h1", 0, 0, "S",),
-    ("qt", 1,),
-    ("mm1", 0, 2,),
-    ("h1", 0, 1, "S",),
-    ("mm1", 0, 3,),
-    ("mm1", 0, 5,),
-    ("h1", 0, 2, "V",),
-    ("mm1", 0, 6,),
-    ("h1", 0, 3, "S",),
-    ("h1", 0, 5, "V",),
-    ("mm1", 0, 7,),
-    ("a", 2, 0, "S",),
-    ("mm1", 0, 4,),
-    ("h2", 0, 0, 256, 512, "V",),
-    ("h1", 0, 6, "S",),
-    ("mm1", 1, 0,),
-    ("t", 2, 1, "tr",),
-    ("h1", 0, 7, "S",),
-    ("h1", 0, 4, "V",),
-    ("h1", 1, 0, "S",),
-    ("mm1", 1, 1,),
-    ("h2", 0, 0, 0, 256, "V",),
-    ("mm1", 1, 2,),
-    ("h2", 0, 1, 0, 256, "S",),
-    ("mm1", 1, 4,),
-    ("mm1", 1, 3,),
-    ("h2", 0, 1, 256, 512, "V",),
-    ("a", 2, 1, "S",),
-    ("h1", 1, 1, "S",),
-    ("t", 3, 0, "tr",),
-    ("qh", 0, 0, 0, 512,),
-    ("h1", 1, 2, "S",),
-    ("qh", 0, 1, 0, 512,),
-    ("h1", 1, 4, "S",),
-    ("mm1", 1, 7,),
-    ("mm1", 1, 5,),
-    ("qt", 2,),
-    ("h1", 1, 3, "S",),
-    ("mm2", 0, 0,),
-    ("a", 3, 0, "V",),
-    ("h1", 1, 7, "S",),
-    ("mm1", 1, 6,),
-    ("h2", 1, 0, 0, 512, "G",),
-    ("mm2", 0, 1,),
-    ("h1", 1, 5, "S",),
-    ("l1", 0, 0,),
-    ("mm1", 2, 1,),
-    ("h1", 1, 6, "S",),
-    ("mm1", 2, 2,),
-    ("l1", 0, 1,),
-    ("mm2", 0, 3,),
-    ("l2", 0, 0,),
-    ("h1", 2, 1, "S",),
-    ("mm2", 0, 2,),
-    ("l1", 0, 3,),
-    ("h2", 1, 1, 0, 256, "S",),
-    ("mm1", 2, 0,),
-    ("t", 3, 1, "tr",),
-    ("l1", 0, 2,),
-    ("h1", 2, 2, "S",),
-    ("mm1", 2, 3,),
-    ("nm", 0, 0, 2,),
-    ("mm1", 2, 4,),
-    ("h1", 2, 0, "S",),
-    ("mm1", 2, 6,),
-    ("l3", 0, 0,),
-    ("l2", 0, 2,),
-    ("l3", 0, 1,),
-    ("nm", 0, 2, 4,),
-    ("a", 3, 1, "S",),
-    ("h2", 1, 1, 448, 512, "G",),
-    ("l3", 0, 2,),
-    ("h2", 1, 1, 256, 448, "S",),
-    ("t", 4, 0, "tr",),
-    ("l3", 0, 3,),
-    ("l2", 0, 1,),
-    ("qh", 1, 0, 0, 512,),
-    ("mm1", 2, 5,),
-    ("qh", 1, 1, 0, 512,),
-    ("l2", 0, 3,),
-    ("a", 4, 0, "V",),
-    ("h1", 2, 3, "S",),
-    ("sq", 0, 0, 2,),
-    ("qt", 3,),
-    ("sq", 0, 2, 4,),
-    ("h1", 2, 4, "S",),
-    ("mm1", 2, 7,),
-    ("mm2", 1, 0,),
-    ("rc", 0, 0, 2,),
-    ("rc", 0, 2, 4,),
-    ("h1", 2, 5, "S",),
-    ("h2", 2, 0, 0, 512, "G",),
-    ("l4", 0, 0,),
-    ("mm1", 3, 0,),
-    ("h1", 2, 6, "S",),
-    ("mm2", 1, 1,),
-    ("l4", 0, 1,),
-    ("h1", 2, 7, "S",),
-    ("l1", 1, 0,),
-    ("mm1", 3, 1,),
-    ("st", 0, 0, 2,),
-    ("h1", 3, 0, "S",),
-    ("l1", 1, 1,),
-    ("mm2", 1, 2,),
-    ("h2", 2, 1, 0, 256, "S",),
-    ("l4", 0, 2,),
-    ("mm1", 3, 2,),
-    ("mm2", 1, 3,),
-    ("l4", 0, 3,),
-    ("l2", 1, 0,),
-    ("l1", 1, 2,),
-    ("mm1", 3, 3,),
-    ("st", 0, 2, 4,),
-    ("nm", 1, 0, 2,),
-    ("t", 4, 1, "tr",),
-    ("l2", 1, 1,),
-    ("l1", 1, 3,),
-    ("l2", 1, 2,),
-    ("mm1", 3, 4,),
-    ("l3", 1, 0,),
-    ("nm", 1, 2, 4,),
-    ("l2", 1, 3,),
-    ("l3", 1, 1,),
-    ("h2", 2, 1, 448, 512, "G",),
-    ("h2", 2, 1, 256, 448, "S",),
-    ("l3", 1, 2,),
-    ("l3", 1, 3,),
-    ("a", 4, 1, "S",),
-    ("sq", 1, 0, 2,),
-    ("sq", 1, 2, 4,),
-    ("h1", 3, 1, "S",),
-    ("qt", 4,),
-    ("t", 5, 0, "tr",),
-    ("h1", 3, 2, "S",),
-    ("rc", 1, 0, 2,),
-    ("rc", 1, 2, 4,),
-    ("qh", 2, 1, 0, 512,),
-    ("mm1", 3, 5,),
-    ("h1", 3, 3, "S",),
-    ("mm1", 3, 6,),
-    ("qh", 2, 0, 0, 512,),
-    ("h1", 3, 4, "S",),
-    ("mm1", 3, 7,),
-    ("a", 5, 0, "V",),
-    ("h1", 3, 5, "S",),
-    ("h2", 3, 0, 0, 512, "G",),
-    ("mm2", 2, 0,),
-    ("l4", 1, 0,),
-    ("h1", 3, 6, "S",),
-    ("mm1", 4, 0,),
-    ("l4", 1, 1,),
-    ("mm2", 2, 1,),
-    ("h1", 3, 7, "S",),
-    ("l1", 2, 0,),
-    ("mm1", 4, 1,),
-    ("h1", 4, 0, "S",),
-    ("st", 1, 0, 2,),
-    ("l1", 2, 1,),
-    ("h2", 3, 1, 0, 256, "S",),
-    ("mm2", 2, 2,),
-    ("l4", 1, 2,),
-    ("mm1", 4, 2,),
-    ("mm2", 2, 3,),
-    ("l4", 1, 3,),
-    ("l2", 2, 0,),
-    ("mm1", 4, 3,),
-    ("l1", 2, 2,),
-    ("nm", 2, 0, 2,),
-    ("l2", 2, 1,),
-    ("st", 1, 2, 4,),
-    ("t", 5, 1, "tr",),
-    ("l1", 2, 3,),
-    ("l2", 2, 2,),
-    ("mm1", 4, 4,),
-    ("l3", 2, 0,),
-    ("nm", 2, 2, 4,),
-    ("l2", 2, 3,),
-    ("l3", 2, 1,),
-    ("h2", 3, 1, 448, 512, "G",),
-    ("h2", 3, 1, 256, 448, "S",),
-    ("l3", 2, 2,),
-    ("l3", 2, 3,),
-    ("a", 5, 1, "S",),
-    ("sq", 2, 0, 2,),
-    ("sq", 2, 2, 4,),
-    ("h1", 4, 1, "S",),
-    ("qt", 5,),
-    ("t", 6, 0, "tr",),
-    ("h1", 4, 2, "S",),
-    ("rc", 2, 0, 2,),
-    ("rc", 2, 2, 4,),
-    ("qh", 3, 1, 0, 512,),
-    ("mm1", 4, 5,),
-    ("h1", 4, 3, "S",),
-    ("mm1", 4, 6,),
-    ("qh", 3, 0, 0, 512,),
-    ("h1", 4, 4, "S",),
-    ("mm1", 4, 7,),
-    ("a", 6, 0, "V",),
-    ("h1", 4, 5, "S",),
-    ("h2", 4, 0, 0, 512, "G",),
-    ("mm2", 3, 0,),
-    ("l4", 2, 0,),
-    ("h1", 4, 6, "S",),
-    ("mm1", 5, 0,),
-    ("l4", 2, 1,),
-    ("mm2", 3, 1,),
-    ("h1", 4, 7, "S",),
-    ("l1", 3, 0,),
-    ("mm1", 5, 1,),
-    ("h1", 5, 0, "S",),
-    ("st", 2, 0, 2,),
-    ("l1", 3, 1,),
-    ("h2", 4, 1, 0, 256, "S",),
-    ("mm2", 3, 2,),
-    ("l4", 2, 2,),
-    ("mm1", 5, 2,),
-    ("mm2", 3, 3,),
-    ("l4", 2, 3,),
-    ("l2", 3, 0,),
-    ("mm1", 5, 3,),
-    ("l1", 3, 2,),
-    ("nm", 3, 0, 2,),
-    ("l2", 3, 1,),
-    ("st", 2, 2, 4,),
-    ("t", 6, 1, "tr",),
-    ("l1", 3, 3,),
-    ("l2", 3, 2,),
-    ("mm1", 5, 4,),
-    ("l3", 3, 0,),
-    ("nm", 3, 2, 4,),
-    ("l2", 3, 3,),
-    ("l3", 3, 1,),
-    ("h2", 4, 1, 448, 512, "G",),
-    ("h2", 4, 1, 256, 448, "S",),
-    ("l3", 3, 2,),
-    ("l3", 3, 3,),
-    ("a", 6, 1, "S",),
-    ("sq", 3, 0, 2,),
-    ("sq", 3, 2, 4,),
-    ("h1", 5, 1, "S",),
-    ("qt", 6,),
-    ("t", 7, 0, "tr",),
-    ("h1", 5, 2, "S",),
-    ("rc", 3, 0, 2,),
-    ("rc", 3, 2, 4,),
-    ("qh", 4, 1, 0, 512,),
-    ("mm1", 5, 5,),
-    ("h1", 5, 3, "S",),
-    ("mm1", 5, 6,),
-    ("qh", 4, 0, 0, 512,),
-    ("h1", 5, 4, "S",),
-    ("mm1", 5, 7,),
-    ("a", 7, 0, "V",),
-    ("h1", 5, 5, "S",),
-    ("h2", 5, 0, 0, 512, "G",),
-    ("mm2", 4, 0,),
-    ("l4", 3, 0,),
-    ("h1", 5, 6, "S",),
-    ("mm1", 6, 0,),
-    ("l4", 3, 1,),
-    ("mm2", 4, 1,),
-    ("h1", 5, 7, "S",),
-    ("l1", 4, 0,),
-    ("mm1", 6, 1,),
-    ("h1", 6, 0, "S",),
-    ("st", 3, 0, 2,),
-    ("l1", 4, 1,),
-    ("h2", 5, 1, 0, 256, "S",),
-    ("mm2", 4, 2,),
-    ("l4", 3, 2,),
-    ("mm1", 6, 2,),
-    ("mm2", 4, 3,),
-    ("l4", 3, 3,),
-    ("l2", 4, 0,),
-    ("mm1", 6, 3,),
-    ("l1", 4, 2,),
-    ("nm", 4, 0, 2,),
-    ("l2", 4, 1,),
-    ("st", 3, 2, 4,),
-    ("t", 7, 1, "tr",),
-    ("l1", 4, 3,),
-    ("l2", 4, 2,),
-    ("mm1", 6, 4,),
-    ("l3", 4, 0,),
-    ("nm", 4, 2, 4,),
-    ("l2", 4, 3,),
-    ("l3", 4, 1,),
-    ("h2", 5, 1, 448, 512, "G",),
-    ("h2", 5, 1, 256, 448, "S",),
-    ("l3", 4, 2,),
-    ("l3", 4, 3,),
-    ("a", 7, 1, "S",),
-    ("sq", 4, 0, 2,),
-    ("sq", 4, 2, 4,),
-    ("h1", 6, 1, "S",),
-    ("qt", 7,),
-    ("h1", 6, 2, "S",),
-    ("rc", 4, 0, 2,),
-    ("rc", 4, 2, 4,),
-    ("mm1", 6, 5,),
-    ("qh", 5, 1, 0, 512,),
-    ("h1", 6, 3, "S",),
-    ("mm1", 6, 6,),
-    ("qh", 5, 0, 0, 512,),
-    ("h1", 6, 4, "S",),
-    ("mm1", 6, 7,),
-    ("l4", 4, 0,),
-    ("h1", 6, 5, "S",),
-    ("h2", 6, 0, 0, 512, "G",),
-    ("mm2", 5, 0,),
-    ("l4", 4, 1,),
-    ("h1", 6, 6, "S",),
-    ("mm1", 7, 0,),
-    ("mm2", 5, 1,),
-    ("h1", 6, 7, "S",),
-    ("st", 4, 0, 2,),
-    ("l1", 5, 0,),
-    ("mm1", 7, 1,),
-    ("h1", 7, 0, "S",),
-    ("mm2", 5, 2,),
-    ("l1", 5, 1,),
-    ("h2", 6, 1, 0, 256, "S",),
-    ("mm1", 7, 2,),
-    ("l4", 4, 2,),
-    ("mm2", 5, 3,),
-    ("l4", 4, 3,),
-    ("l2", 5, 0,),
-    ("mm1", 7, 3,),
-    ("l1", 5, 2,),
-    ("mm1", 7, 4,),
-    ("nm", 5, 0, 2,),
-    ("l2", 5, 1,),
-    ("st", 4, 2, 4,),
-    ("l1", 5, 3,),
-    ("l2", 5, 2,),
-    ("l3", 5, 0,),
-    ("nm", 5, 2, 4,),
-    ("l2", 5, 3,),
-    ("l3", 5, 1,),
-    ("h2", 6, 1, 448, 512, "G",),
-    ("h2", 6, 1, 256, 448, "S",),
-    ("l3", 5, 2,),
-    ("l3", 5, 3,),
-    ("sq", 5, 0, 2,),
-    ("sq", 5, 2, 4,),
-    ("h1", 7, 1, "S",),
-    ("rc", 5, 0, 2,),
-    ("rc", 5, 2, 4,),
-    ("qh", 6, 1, 0, 512,),
-    ("h1", 7, 2, "S",),
-    ("mm1", 7, 5,),
-    ("qh", 6, 0, 0, 512,),
-    ("h1", 7, 3, "S",),
-    ("mm1", 7, 6,),
-    ("l4", 5, 0,),
-    ("h1", 7, 4, "S",),
-    ("h2", 7, 0, 0, 512, "G",),
-    ("mm1", 7, 7,),
-    ("mm2", 6, 0,),
-    ("h1", 7, 5, "S",),
-    ("l4", 5, 1,),
-    ("h1", 7, 6, "S",),
-    ("mm2", 6, 1,),
-    ("st", 5, 0, 2,),
-    ("h1", 7, 7, "S",),
-    ("l1", 6, 0,),
-    ("l1", 6, 1,),
-    ("h2", 7, 1, 0, 256, "S",),
-    ("mm2", 6, 2,),
-    ("l4", 5, 2,),
-    ("mm2", 6, 3,),
-    ("l4", 5, 3,),
-    ("l2", 6, 0,),
-    ("l1", 6, 2,),
-    ("nm", 6, 0, 2,),
-    ("l2", 6, 1,),
-    ("st", 5, 2, 4,),
-    ("l1", 6, 3,),
-    ("l2", 6, 2,),
-    ("l3", 6, 0,),
-    ("nm", 6, 2, 4,),
-    ("l2", 6, 3,),
-    ("l3", 6, 1,),
-    ("h2", 7, 1, 448, 512, "G",),
-    ("h2", 7, 1, 256, 448, "S",),
-    ("l3", 6, 2,),
-    ("l3", 6, 3,),
-    ("sq", 6, 0, 2,),
-    ("sq", 6, 2, 4,),
-    ("rc", 6, 0, 2,),
-    ("rc", 6, 2, 4,),
-    ("qh", 7, 1, 0, 512,),
-    ("qh", 7, 0, 0, 512,),
-    ("l4", 6, 0,),
-    ("mm2", 7, 0,),
-    ("l4", 6, 1,),
-    ("mm2", 7, 1,),
-    ("st", 6, 0, 2,),
-    ("l1", 7, 0,),
-    ("l1", 7, 1,),
-    ("l2", 7, 0,),
-    ("mm2", 7, 2,),
-    ("l4", 6, 2,),
-    ("mm2", 7, 3,),
-    ("nm", 7, 0, 2,),
-    ("l2", 7, 1,),
-    ("l4", 6, 3,),
-    ("l1", 7, 2,),
-    ("st", 6, 2, 4,),
-    ("l1", 7, 3,),
-    ("l2", 7, 2,),
-    ("l3", 7, 0,),
-    ("nm", 7, 2, 4,),
-    ("l2", 7, 3,),
-    ("l3", 7, 1,),
-    ("sq", 7, 0, 2,),
-    ("l3", 7, 2,),
-    ("sq", 7, 2, 4,),
-    ("l3", 7, 3,),
-    ("rc", 7, 0, 2,),
-    ("rc", 7, 2, 4,),
-    ("l4", 7, 0,),
-    ("l4", 7, 1,),
-    ("st", 7, 0, 1,),
-    ("l4", 7, 2,),
-    ("st", 7, 1, 2,),
-    ("l4", 7, 3,),
-    ("st", 7, 2, 3,),
-    ("st", 7, 3, 4,),
-)
 
 
 def tile_patchwork_t_kernel(tc, tri, W1, b1, W2, b2, gamma, beta, out):
@@ -505,8 +39,9 @@ def tile_patchwork_t_kernel(tc, tri, W1, b1, W2, b2, gamma, beta, out):
         ptr = ctx.enter_context(tc.psum_pool(name="ptr", bufs=1))
         ph = ctx.enter_context(tc.psum_pool(name="ph", bufs=4))
         py = ctx.enter_context(tc.psum_pool(name="py", bufs=2))
+        banks = {"tr": ptr, "h": ph, "y": py}
 
-        traw = keep.tile([P, (B // P) * K1], BF16, name="traw")
+        traw = keep.tile([P, NCH * BT * K1], BF16, name="traw")
         w1raw = keep.tile([P, 4, H], BF16, name="w1raw")
         w2raw = keep.tile([P, 2, 4, D], BF16, name="w2raw")
         b1raw = keep.tile([P, 2, 4], BF16, name="b1raw")
@@ -517,6 +52,7 @@ def tile_patchwork_t_kernel(tc, tri, W1, b1, W2, b2, gamma, beta, out):
         epst = keep.tile([P, 1], F32, name="epst")
         warm = keep.tile([P, 1], F32, name="warm")
         b2b = keep.tile([P, D], F32, name="b2b")
+        betf = keep.tile([P, D], F32, name="betf")
         junk = keep.tile([P, D], BF16, name="junk")
         w1g = keep.tile([P, 4 * H], BF16, name="w1g", align_bytes=64)
         w1c = keep.tile([P, H], U32, name="w1c", align_bytes=64)
@@ -535,21 +71,19 @@ def tile_patchwork_t_kernel(tc, tri, W1, b1, W2, b2, gamma, beta, out):
         w2v = W2.rearrange("o k d -> (o k) d")
         live = {}
 
+        def ok(c):
+            return 0 <= c < NCH
+
         def copy_on(eng, dst, src):
             if eng == "V":
                 nc.vector.tensor_copy(out=dst, in_=src)
-            elif eng == "S":
-                nc.scalar.copy(out=dst, in_=src)
             else:
-                nc.gpsimd.tensor_scalar(out=dst, in0=src, scalar1=1.0, scalar2=0.0, op0=ALU.mult, op1=ALU.add)
-
-        def rows(c):
-            return slice(OFF[c] * P, (OFF[c] + NBS[c]) * P)
+                nc.scalar.copy(out=dst, in_=src)
 
         def ld_tri(c):
             nc.sync.dma_start(
-                out=traw[:, OFF[c] * K1:(OFF[c] + NBS[c]) * K1],
-                in_=tri[rows(c), :].rearrange("(p t) k -> p (t k)", t=NBS[c]),
+                out=traw[:, c * BT * K1:(c + 1) * BT * K1],
+                in_=tri[c * CH:(c + 1) * CH, :].rearrange("(p t) k -> p (t k)", t=BT),
             )
 
         def ld_w1(g):
@@ -558,9 +92,6 @@ def tile_patchwork_t_kernel(tc, tri, W1, b1, W2, b2, gamma, beta, out):
                     out=w1raw[:, 2 * u:2 * u + 2, g * 512:(g + 1) * 512],
                     in_=w1v[256 * u:256 * (u + 1), g * 512:(g + 1) * 512].rearrange("(q e) h -> q e h", e=2),
                 )
-
-        def ld_w2():
-            nc.sync.dma_start(out=w2raw[:], in_=w2v.rearrange("(g p t) d -> p g t d", g=2, t=4))
 
         def rw1(g, eng):
             copy_on(
@@ -576,35 +107,28 @@ def tile_patchwork_t_kernel(tc, tri, W1, b1, W2, b2, gamma, beta, out):
                 in_=w1g[:, g * 2048:(g + 1) * 2048],
             )
 
-        def rw2(g, eng):
-            copy_on(eng, w2g[:, g, :, :], w2raw[:, g, :, :].rearrange("p t d -> p d t"))
+        def rw2(g):
+            nc.vector.tensor_copy(out=w2g[:, g, :, :], in_=w2raw[:, g, :, :].rearrange("p t d -> p d t"))
 
         def qw2():
             nc.vector.quantize_mx(
                 out=w2c[:].bitcast(FP8X4), scales=w2s[:], in_=w2g[:].rearrange("p g d t -> p (g d t)"),
             )
 
-        def b1cast():
-            nc.vector.tensor_copy(out=b1f[:], in_=b1raw[:].rearrange("p g t -> p (g t)"))
-
-        def pb():
-            t = py.tile([P, D], F32, name="pbt", tag="y")
-            nc.tensor.matmul(out=t[:], lhsT=ones[:], rhs=vec[:, 0:D], start=True, stop=True)
+        def spread():
+            pbt = py.tile([P, D], F32, name="pbt", tag="y")
+            nc.tensor.matmul(out=pbt[:], lhsT=ones[:], rhs=vec[:, 0:D], start=True, stop=True)
             nc.tensor.matmul(out=gam, lhsT=ones[:], rhs=vec[:, D:2 * D], start=True, stop=True)
             nc.tensor.matmul(out=bet, lhsT=ones[:], rhs=vec[:, 2 * D:3 * D], start=True, stop=True)
-            live["pb"] = t
+            live["pb"] = pbt
 
-        def cb2(eng):
-            copy_on(eng, b2b[:], live["pb"][:])
-
-        def op_t(c, hf, tag):
-            words = traw[:, OFF[c] * K1:(OFF[c] + NBS[c]) * K1].bitcast(F32)
-            if tag == "h":
-                trp = ph.tile([P, 2, 256], F32, name="trp", tag="h")
-            else:
-                trp = ptr.tile([P, 2, 256], F32, name="trp", tag="tr")
+        def op_t(c, hf, bank="tr"):
+            if not ok(c):
+                return
+            words = traw[:, c * BT * K1:(c + 1) * BT * K1].bitcast(F32)
+            trp = banks[bank].tile([P, 2, 256], F32, name="trp", tag=bank)
             live["trp", c, hf] = trp
-            for j in range(min(2, NBS[c] - 2 * hf)):
+            for j in range(2):
                 t = 2 * hf + j
                 for u in range(2):
                     nc.tensor.transpose(
@@ -614,55 +138,53 @@ def tile_patchwork_t_kernel(tc, tri, W1, b1, W2, b2, gamma, beta, out):
                     )
 
         def op_a(c, hf, eng):
-            if ("tg", c) not in live:
-                live["tg", c] = tgpool.tile([P, 2 * CHM], F32, name="tg", tag="tg", align_bytes=64)
-            w = P * min(2, NBS[c] - 2 * hf)
-            dst = live["tg", c][:, hf * 512:hf * 512 + 2 * w].rearrange("p (w u) -> p w u", u=2)
-            src = live["trp", c, hf][:, :, 0:w].rearrange("p u w -> p w u")
-            copy_on(eng, dst, src)
+            if not ok(c):
+                return
+            if hf == 0:
+                live["tg", c] = tgpool.tile([P, 2 * CH], F32, name="tg", tag="tg", align_bytes=64)
+            dst = live["tg", c][:, hf * 512:(hf + 1) * 512].rearrange("p (w u) -> p w u", u=2)
+            copy_on(eng, dst, live["trp", c, hf][:].rearrange("p u w -> p w u"))
 
         def op_qt(c):
-            n = NBS[c] * P
-            tcod = tcpool.tile([P, CHM], U32, name="tcod", tag="tcod", align_bytes=64)
-            tscl = tcpool.tile([P, CHM], U8, name="tscl", tag="tscl", align_bytes=64)
-            nc.vector.quantize_mx(
-                out=tcod[:, 0:n].bitcast(FP8X4), scales=tscl[:, 0:n], in_=live["tg", c][:, 0:2 * n].bitcast(BF16),
-            )
+            if not ok(c):
+                return
+            tcod = tcpool.tile([P, CH], U32, name="tcod", tag="tcod", align_bytes=64)
+            tscl = tcpool.tile([P, CH], U8, name="tscl", tag="tscl", align_bytes=64)
+            nc.vector.quantize_mx(out=tcod[:].bitcast(FP8X4), scales=tscl[:], in_=live["tg", c][:].bitcast(BF16))
             live["tq", c] = (tcod, tscl)
 
         def op_mm1(c, m):
-            n = NBS[c] * P
+            if not ok(c):
+                return
             tcod, tscl = live["tq", c]
-            hp = ph.tile([P, CHM], F32, name="hp", tag="h")
+            hp = ph.tile([P, CH], F32, name="hp", tag="h")
             live["hp", c, m] = hp
             nc.tensor.matmul_mx(
-                out=hp[:, 0:n],
+                out=hp[:],
                 lhsT=w1c[:, m * P:(m + 1) * P].bitcast(FP8X4),
                 lhsT_scale=w1s[:, m * P:(m + 1) * P],
-                rhs=tcod[:, 0:n].bitcast(FP8X4),
-                rhs_scale=tscl[:, 0:n],
+                rhs=tcod[:].bitcast(FP8X4),
+                rhs_scale=tscl[:],
                 start=True,
                 stop=True,
             )
 
-        def op_h1(c, m, eng):
-            n = NBS[c] * P
+        def op_h1(c, m):
+            if not ok(c):
+                return
             g, t = divmod(m, 4)
-            if ("r", c, g) not in live:
-                live["r", c, g] = rpool.tile([P, 4, CHM], F32, name="r", tag="r")
-            r = live["r", c, g]
-            hp = live["hp", c, m]
-            if eng == "V":
-                nc.vector.tensor_scalar(
-                    out=r[:, t, 0:n], in0=hp[:, 0:n], scalar1=b1f[:, m:m + 1], scalar2=0.0, op0=ALU.add, op1=ALU.max,
-                )
-            else:
-                nc.scalar.activation(out=r[:, t, 0:n], in_=hp[:, 0:n], func=ACT.Relu, bias=b1f[:, m:m + 1], scale=1.0)
+            if t == 0:
+                live["r", c, g] = rpool.tile([P, 4, CH], F32, name="r", tag="r")
+            nc.scalar.activation(
+                out=live["r", c, g][:, t, :], in_=live["hp", c, m][:], func=ACT.Relu, bias=b1f[:, m:m + 1], scale=1.0,
+            )
 
         def op_h2(c, g, w0, w1, eng):
+            if not ok(c):
+                return
             if ("hb", c, g) not in live:
                 pool = hpool0 if g == 0 else hpool1
-                live["hb", c, g] = pool.tile([P, CHM, 4], BF16, name="hb%d" % g, tag="hb%d" % g, align_bytes=64)
+                live["hb", c, g] = pool.tile([P, CH, 4], BF16, name="hb%d" % g, tag="hb%d" % g, align_bytes=64)
             hb = live["hb", c, g]
             r = live["r", c, g]
             if eng == "S":
@@ -678,19 +200,20 @@ def tile_patchwork_t_kernel(tc, tri, W1, b1, W2, b2, gamma, beta, out):
                 else:
                     nc.gpsimd.tensor_tensor(out=hb[:, w0:w1, :], in0=src, in1=src, op=ALU.mult)
 
-        def op_qh(c, g, w0, w1):
-            if ("hq", c, g) not in live:
-                hcod = cpool.tile([P, CHM], U32, name="hcod%d" % g, tag="hcod%d" % g, align_bytes=64)
-                hscl = cpool.tile([P, CHM], U8, name="hscl%d" % g, tag="hscl%d" % g, align_bytes=64)
-                live["hq", c, g] = (hcod, hscl)
-            hcod, hscl = live["hq", c, g]
+        def op_qh(c, g):
+            if not ok(c):
+                return
+            hcod = cpool.tile([P, CH], U32, name="hcod%d" % g, tag="hcod%d" % g, align_bytes=64)
+            hscl = cpool.tile([P, CH], U8, name="hscl%d" % g, tag="hscl%d" % g, align_bytes=64)
+            live["hq", c, g] = (hcod, hscl)
             nc.vector.quantize_mx(
-                out=hcod[:, w0:w1].bitcast(FP8X4), scales=hscl[:, w0:w1],
-                in_=live["hb", c, g][:, w0:w1, :].rearrange("p w t -> p (w t)"),
+                out=hcod[:].bitcast(FP8X4), scales=hscl[:], in_=live["hb", c, g][:].rearrange("p w t -> p (w t)"),
             )
 
-        def op_mm2(c, t):
-            yp = py.tile([P, D], F32, name="yp", tag="y")
+        def op_mm2(c, t, bank="y"):
+            if not ok(c):
+                return
+            yp = banks[bank].tile([P, D], F32, name="yp", tag=bank)
             live["yp", c, t] = yp
             for g in range(2):
                 hcod, hscl = live["hq", c, g]
@@ -706,72 +229,198 @@ def tile_patchwork_t_kernel(tc, tri, W1, b1, W2, b2, gamma, beta, out):
 
         def stat(name, c):
             if (name, c) not in live:
-                live[name, c] = spool.tile([P, 4], F32, name=name, tag=name)
+                live[name, c] = spool.tile([P, BT], F32, name=name, tag=name)
             return live[name, c]
 
         def op_l1(c, t):
-            if ("y", c) not in live:
-                live["y", c] = ypool.tile([P, 4, D], F32, name="y", tag="y")
+            if not ok(c):
+                return
+            if t == 0:
+                live["y", c] = ypool.tile([P, BT, D], F32, name="y", tag="y")
             nc.vector.scalar_tensor_tensor(
                 out=live["y", c][:, t, :], in0=live["yp", c, t][:], scalar=0.0, in1=b2b[:],
                 op0=ALU.add, op1=ALU.add, accum_out=stat("sums", c)[:, t:t + 1],
             )
 
-        def op_nm(c, t0, t1):
+        def op_nm(c, t0):
+            if not ok(c):
+                return
             nc.scalar.activation(
-                out=stat("negmu", c)[:, t0:t1], in_=stat("sums", c)[:, t0:t1], func=ACT.Copy, scale=-1.0 / D,
+                out=stat("negmu", c)[:, t0:t0 + 2], in_=stat("sums", c)[:, t0:t0 + 2], func=ACT.Copy, scale=-1.0 / D,
             )
 
         def op_l2(c, t):
+            if not ok(c):
+                return
             nc.scalar.activation(
                 out=junk[:], in_=live["y", c][:, t, :], func=ACT.Square, bias=stat("sums", c)[:, t:t + 1], scale=-float(D),
                 accum_out=stat("ssq", c)[:, t:t + 1],
             )
 
-        def op_sq(c, t0, t1):
+        def op_sq(c):
+            if not ok(c):
+                return
             nc.scalar.activation(
-                out=stat("std", c)[:, t0:t1], in_=stat("ssq", c)[:, t0:t1], func=ACT.Sqrt, bias=epst[:, 0:1],
-                scale=1.0 / (D * D * D),
+                out=stat("std", c)[:], in_=stat("ssq", c)[:], func=ACT.Sqrt, bias=epst[:, 0:1], scale=1.0 / (D * D * D),
             )
 
-        def op_rc(c, t0, t1):
-            nc.vector.reciprocal(out=stat("rstd", c)[:, t0:t1], in_=stat("std", c)[:, t0:t1])
+        def op_rc(c):
+            if not ok(c):
+                return
+            nc.vector.reciprocal(out=stat("rstd", c)[:], in_=stat("std", c)[:])
 
         def op_l3(c, t):
+            if not ok(c):
+                return
             if ("o", c) not in live:
-                live["o", c] = opool.tile([P, 4, D], F32, name="o", tag="o")
+                live["o", c] = opool.tile([P, BT, D], F32, name="o", tag="o")
             nc.vector.scalar_tensor_tensor(
                 out=live["o", c][:, t, :], in0=live["y", c][:, t, :], scalar=stat("negmu", c)[:, t:t + 1], in1=gam,
                 op0=ALU.add, op1=ALU.mult,
             )
 
         def op_l4(c, t):
+            if not ok(c):
+                return
             o = live["o", c]
             nc.vector.scalar_tensor_tensor(
                 out=o[:, t, :], in0=o[:, t, :], scalar=stat("rstd", c)[:, t:t + 1], in1=bet,
                 op0=ALU.mult, op1=ALU.add,
             )
 
+        def op_l4_sg(c, t):
+            o = live["o", c]
+            nc.scalar.activation(out=o[:, t, :], in_=o[:, t, :], func=ACT.Copy, scale=stat("rstd", c)[:, t:t + 1])
+            nc.gpsimd.tensor_tensor(out=o[:, t, :], in0=o[:, t, :], in1=betf[:], op=ALU.add)
+
         def op_st(c, t0, t1):
+            if not ok(c):
+                return
             nc.sync.dma_start(
-                out=out[rows(c), :].rearrange("(p t) d -> p t d", t=NBS[c])[:, t0:t1, :],
+                out=out[c * CH:(c + 1) * CH, :].rearrange("(p t) d -> p t d", t=BT)[:, t0:t1, :],
                 in_=live["o", c][:, t0:t1, :],
             )
 
-        def start():
-            nc.vector.memset(vec[:], 0.0)
-            nc.scalar.dma_start(out=b1raw[:], in_=b1.rearrange("o (g p t) -> p (o g) t", g=2, t=4))
-            for j, v in enumerate((b2, gamma, beta)):
-                nc.scalar.dma_start(out=vec[0:1, j * D:(j + 1) * D], in_=v)
-            nc.vector.memset(epst[:], LN_EPS)
-            nc.vector.memset(ones[:], 1.0)
-            nc.scalar.activation(out=warm[:], in_=epst[:], func=ACT.Sqrt)
+        ld_tri(0)
+        ld_w1(0)
+        ld_w1(1)
+        nc.sync.dma_start(out=w2raw[:], in_=w2v.rearrange("(g p t) d -> p g t d", g=2, t=4))
+        for c in range(1, NCH):
+            ld_tri(c)
+        nc.vector.memset(vec[:], 0.0)
+        nc.scalar.dma_start(out=b1raw[:], in_=b1.rearrange("o (g p t) -> p (o g) t", g=2, t=4))
+        for j, v in enumerate((b2, gamma, beta)):
+            nc.scalar.dma_start(out=vec[0:1, j * D:(j + 1) * D], in_=v)
+        nc.vector.memset(epst[:], LN_EPS)
+        nc.vector.memset(ones[:], 1.0)
+        nc.scalar.activation(out=warm[:], in_=epst[:], func=ACT.Sqrt)
 
-        table = {
-            "ld_tri": ld_tri, "ld_w1": ld_w1, "ld_w2": ld_w2, "start": start, "rw1": rw1, "qw1": qw1, "rw2": rw2,
-            "qw2": qw2, "b1": b1cast, "pb": pb, "cb2": cb2, "t": op_t, "a": op_a, "qt": op_qt, "mm1": op_mm1,
-            "h1": op_h1, "h2": op_h2, "qh": op_qh, "mm2": op_mm2, "l1": op_l1, "nm": op_nm, "l2": op_l2, "sq": op_sq,
-            "rc": op_rc, "l3": op_l3, "l4": op_l4, "st": op_st,
-        }
-        for step in PROG:
-            table[step[0]](*step[1:])
+        op_t(0, 0, "h")
+        op_t(0, 1, "h")
+        rw1(0, "V")
+        op_a(0, 0, "S")
+        op_a(0, 1, "S")
+        nc.vector.tensor_copy(out=b1f[:], in_=b1raw[:].rearrange("p g t -> p (g t)"))
+        qw1(0)
+        op_qt(0)
+        for m in range(4):
+            op_mm1(0, m)
+        rw1(1, "S")
+        rw2(0)
+        qw1(1)
+        rw2(1)
+        qw2()
+        op_t(1, 0)
+        op_t(1, 1, "y")
+        spread()
+        for m in range(4):
+            op_h1(0, m)
+            op_mm1(0, 4 + m)
+        op_a(1, 0, "S")
+        op_a(1, 1, "S")
+        op_qt(1)
+        op_t(2, 0)
+        for m in range(4):
+            op_h1(0, 4 + m)
+            op_mm1(1, m)
+        nc.vector.tensor_copy(out=b2b[:], in_=live["pb"][:])
+        op_h2(0, 0, 0, 256, "V")
+        op_a(2, 0, "V")
+        op_t(2, 1)
+        op_h2(0, 0, 256, CH, "V")
+        op_h2(0, 1, 0, 256, "S")
+        op_h2(0, 1, 256, CH, "V")
+        op_h1(1, 0)
+        op_mm1(1, 4)
+        op_a(2, 1, "S")
+        op_t(3, 0)
+
+        for c in range(1, NCH + 1):
+            last = c == NCH
+            op_qt(c + 1)
+            op_rc(c - 2)
+            op_qh(c - 1, 1)
+            op_qh(c - 1, 0)
+            for m in range(1, 4):
+                op_h1(c, m)
+                op_mm1(c, 4 + m)
+            op_h2(c, 0, 0, CH, "G")
+            for j in range(2):
+                op_h1(c, 4 + j)
+                op_mm2(c - 1, j)
+                op_mm1(c + 1, j)
+            if last:
+                op_mm2(c - 1, 2, "h")
+                op_mm2(c - 1, 3, "h")
+            op_a(c + 2, 0, "V")
+            op_l4(c - 2, 0)
+            op_l4(c - 2, 1)
+            op_st(c - 2, 0, 2)
+            if last:
+                nc.scalar.copy(out=betf[:], in_=bet)
+                op_l4_sg(c - 2, 2)
+                op_l4_sg(c - 2, 3)
+                op_st(c - 2, 2, 4)
+            for j in range(2):
+                op_l1(c - 1, j)
+                if not last:
+                    op_mm2(c - 1, 2 + j)
+            for j in range(2):
+                op_h1(c, 6 + j)
+                op_mm1(c + 1, 2 + j)
+            op_h1(c + 1, 0)
+            op_t(c + 2, 1)
+            op_mm1(c + 1, 4)
+            op_h2(c, 1, CH - GCOLS, CH, "G")
+            op_h2(c, 1, 0, 256, "S")
+            if not last:
+                op_l4(c - 2, 2)
+                op_l4(c - 2, 3)
+                op_st(c - 2, 2, 4)
+            op_l1(c - 1, 2)
+            op_l1(c - 1, 3)
+            op_l2(c - 1, 0)
+            op_nm(c - 1, 0)
+            op_l2(c - 1, 1)
+            op_l2(c - 1, 2)
+            op_nm(c - 1, 2)
+            op_l2(c - 1, 3)
+            op_h2(c, 1, 256, CH - GCOLS, "S")
+            op_a(c + 2, 1, "S")
+            op_sq(c - 1)
+            op_t(c + 3, 0)
+            if not last:
+                for t in range(BT):
+                    op_l3(c - 1, t)
+
+        e = NCH - 1
+        op_l3(e, 0)
+        op_l3(e, 1)
+        op_l3(e, 3)
+        op_rc(e)
+        op_l3(e, 2)
+        op_l4_sg(e, 3)
+        for t in range(3):
+            op_l4(e, t)
+            op_st(e, t, t + 1)
+        op_st(e, 3, 4)

@@ -17,7 +17,7 @@ CH = 512
 NCH = B // CH
 BT = CH // P
 LN_EPS = 1e-5
-GCOLS = 96
+GCOLS = 128
 
 FLOPS = 2 * B * K1 * H + 2 * B * H * D
 
@@ -392,7 +392,7 @@ def tile_patchwork_t_kernel(tc, tri, W1, b1, W2, b2, gamma, beta, out):
             op_t(c + 2, 1)
             op_mm1(c + 1, 4)
             op_h2(c, 1, CH - GCOLS, CH, "G")
-            op_h2(c, 1, 0, 256, "S")
+            op_h2(c, 1, 0, CH - GCOLS, "S")
             if not last:
                 op_l4(c - 2, 2)
                 op_l4(c - 2, 3)
@@ -405,7 +405,6 @@ def tile_patchwork_t_kernel(tc, tri, W1, b1, W2, b2, gamma, beta, out):
             op_l2(c - 1, 2)
             op_nm(c - 1, 2)
             op_l2(c - 1, 3)
-            op_h2(c, 1, 256, CH - GCOLS, "S")
             op_a(c + 2, 1, "S")
             op_sq(c - 1)
             op_t(c + 3, 0)

@@ -26,6 +26,7 @@ def tile_patchwork_t_kernel(tc, tri, W1, b1, W2, b2, gamma, beta, out):
     nc = tc.nc
     with ExitStack() as ctx:
         keep = ctx.enter_context(tc.tile_pool(name="keep", bufs=1))
+        wgpool = ctx.enter_context(tc.tile_pool(name="wgpool", bufs=1))
         tgpool = ctx.enter_context(tc.tile_pool(name="tgpool", bufs=2))
         tcpool = ctx.enter_context(tc.tile_pool(name="tcpool", bufs=3))
         rpool = ctx.enter_context(tc.tile_pool(name="rpool", bufs=4))
@@ -54,10 +55,9 @@ def tile_patchwork_t_kernel(tc, tri, W1, b1, W2, b2, gamma, beta, out):
         b2b = keep.tile([P, D], F32, name="b2b")
         betf = keep.tile([P, D], F32, name="betf")
         junk = keep.tile([P, D], BF16, name="junk")
-        w1g = keep.tile([P, 4 * H], BF16, name="w1g", align_bytes=64)
+        w1g = wgpool.tile([P, 4 * H], BF16, name="w1g", tag="wg", align_bytes=64)
         w1c = keep.tile([P, H], U32, name="w1c", align_bytes=64)
         w1s = keep.tile([P, H], U8, name="w1s", align_bytes=64)
-        w2g = keep.tile([P, 2, D, 4], BF16, name="w2g", align_bytes=64)
         w2c = keep.tile([P, 2 * D], U32, name="w2c", align_bytes=64)
         w2s = keep.tile([P, 2 * D], U8, name="w2s", align_bytes=64)
         gb = pgb.tile([P, 2 * D], BF16, name="gb")
@@ -107,12 +107,18 @@ def tile_patchwork_t_kernel(tc, tri, W1, b1, W2, b2, gamma, beta, out):
                 in_=w1g[:, g * 2048:(g + 1) * 2048],
             )
 
-        def rw2(g):
-            nc.vector.tensor_copy(out=w2g[:, g, :, :], in_=w2raw[:, g, :, :].rearrange("p t d -> p d t"))
+        def rw2():
+            w2g = wgpool.tile([P, 2, D, 4], BF16, name="w2g", tag="wg", align_bytes=64)
+            live["w2g"] = w2g
+            for g in range(2):
+                nc.gpsimd.tensor_scalar(
+                    out=w2g[:, g, :, :], in0=w2raw[:, g, :, :].rearrange("p t d -> p d t"),
+                    scalar1=1.0, scalar2=0.0, op0=ALU.mult, op1=ALU.add,
+                )
 
         def qw2():
             nc.vector.quantize_mx(
-                out=w2c[:].bitcast(FP8X4), scales=w2s[:], in_=w2g[:].rearrange("p g d t -> p (g d t)"),
+                out=w2c[:].bitcast(FP8X4), scales=w2s[:], in_=live["w2g"][:].rearrange("p g d t -> p (g d t)"),
             )
 
         def spread():
@@ -169,15 +175,21 @@ def tile_patchwork_t_kernel(tc, tri, W1, b1, W2, b2, gamma, beta, out):
                 stop=True,
             )
 
-        def op_h1(c, m):
+        def op_h1(c, m, eng="S"):
             if not ok(c):
                 return
             g, t = divmod(m, 4)
             if t == 0:
                 live["r", c, g] = rpool.tile([P, 4, CH], F32, name="r", tag="r")
-            nc.scalar.activation(
-                out=live["r", c, g][:, t, :], in_=live["hp", c, m][:], func=ACT.Relu, bias=b1f[:, m:m + 1], scale=1.0,
-            )
+            if eng == "V":
+                nc.vector.tensor_scalar(
+                    out=live["r", c, g][:, t, :], in0=live["hp", c, m][:], scalar1=b1f[:, m:m + 1], scalar2=0.0,
+                    op0=ALU.add, op1=ALU.max,
+                )
+            else:
+                nc.scalar.activation(
+                    out=live["r", c, g][:, t, :], in_=live["hp", c, m][:], func=ACT.Relu, bias=b1f[:, m:m + 1], scale=1.0,
+                )
 
         def op_h2(c, g, w0, w1, eng):
             if not ok(c):
@@ -303,9 +315,10 @@ def tile_patchwork_t_kernel(tc, tri, W1, b1, W2, b2, gamma, beta, out):
 
         ld_tri(0)
         ld_w1(0)
+        ld_tri(1)
         ld_w1(1)
         nc.sync.dma_start(out=w2raw[:], in_=w2v.rearrange("(g p t) d -> p g t d", g=2, t=4))
-        for c in range(1, NCH):
+        for c in range(2, NCH):
             ld_tri(c)
         nc.vector.memset(vec[:], 0.0)
         nc.scalar.dma_start(out=b1raw[:], in_=b1.rearrange("o (g p t) -> p (o g) t", g=2, t=4))
@@ -323,37 +336,39 @@ def tile_patchwork_t_kernel(tc, tri, W1, b1, W2, b2, gamma, beta, out):
         nc.vector.tensor_copy(out=b1f[:], in_=b1raw[:].rearrange("p g t -> p (g t)"))
         qw1(0)
         op_qt(0)
-        for m in range(4):
-            op_mm1(0, m)
-        rw1(1, "S")
-        rw2(0)
-        qw1(1)
-        rw2(1)
-        qw2()
         op_t(1, 0)
         op_t(1, 1, "y")
-        spread()
         for m in range(4):
-            op_h1(0, m)
-            op_mm1(0, 4 + m)
+            op_mm1(0, m)
         op_a(1, 0, "S")
         op_a(1, 1, "S")
+        rw1(1, "V")
         op_qt(1)
+        qw1(1)
+        rw2()
+        spread()
+        op_h1(0, 0)
+        op_mm1(0, 4)
         op_t(2, 0)
-        for m in range(4):
-            op_h1(0, 4 + m)
-            op_mm1(1, m)
+        for m in range(1, 4):
+            op_h1(0, m)
+            op_mm1(0, 4 + m)
         nc.vector.tensor_copy(out=b2b[:], in_=live["pb"][:])
-        op_h2(0, 0, 0, 256, "V")
+        op_t(2, 1, "y")
+        op_h2(0, 0, 0, CH, "S")
+        for m in range(2):
+            op_h1(0, 4 + m, "V")
+            op_mm1(1, m)
         op_a(2, 0, "V")
-        op_t(2, 1)
-        op_h2(0, 0, 256, CH, "V")
-        op_h2(0, 1, 0, 256, "S")
-        op_h2(0, 1, 256, CH, "V")
-        op_h1(1, 0)
-        op_mm1(1, 4)
-        op_a(2, 1, "S")
         op_t(3, 0)
+        for m in range(2, 4):
+            op_h1(0, 4 + m, "V")
+            op_mm1(1, m)
+        op_a(2, 1, "V")
+        op_h2(0, 1, 0, CH, "S")
+        op_h1(1, 0, "V")
+        op_mm1(1, 4)
+        qw2()
 
         for c in range(1, NCH + 1):
             last = c == NCH

@@ -17,7 +17,7 @@ CH = 512
 NCH = B // CH
 BT = CH // P
 LN_EPS = 1e-5
-GCOLS = 128
+GCOLS = 112
 
 FLOPS = 2 * B * K1 * H + 2 * B * H * D
 
@@ -26,7 +26,6 @@ def tile_patchwork_t_kernel(tc, tri, W1, b1, W2, b2, gamma, beta, out):
     nc = tc.nc
     with ExitStack() as ctx:
         keep = ctx.enter_context(tc.tile_pool(name="keep", bufs=1))
-        wgpool = ctx.enter_context(tc.tile_pool(name="wgpool", bufs=1))
         tgpool = ctx.enter_context(tc.tile_pool(name="tgpool", bufs=2))
         tcpool = ctx.enter_context(tc.tile_pool(name="tcpool", bufs=3))
         rpool = ctx.enter_context(tc.tile_pool(name="rpool", bufs=4))
@@ -55,9 +54,10 @@ def tile_patchwork_t_kernel(tc, tri, W1, b1, W2, b2, gamma, beta, out):
         b2b = keep.tile([P, D], F32, name="b2b")
         betf = keep.tile([P, D], F32, name="betf")
         junk = keep.tile([P, D], BF16, name="junk")
-        w1g = wgpool.tile([P, 4 * H], BF16, name="w1g", tag="wg", align_bytes=64)
+        w1g = keep.tile([P, 4 * H], BF16, name="w1g", align_bytes=64)
         w1c = keep.tile([P, H], U32, name="w1c", align_bytes=64)
         w1s = keep.tile([P, H], U8, name="w1s", align_bytes=64)
+        w2g = keep.tile([P, 2, D, 4], BF16, name="w2g", align_bytes=64)
         w2c = keep.tile([P, 2 * D], U32, name="w2c", align_bytes=64)
         w2s = keep.tile([P, 2 * D], U8, name="w2s", align_bytes=64)
         gb = pgb.tile([P, 2 * D], BF16, name="gb")
@@ -71,71 +71,65 @@ def tile_patchwork_t_kernel(tc, tri, W1, b1, W2, b2, gamma, beta, out):
         w2v = W2.rearrange("o k d -> (o k) d")
         live = {}
 
-        def ok(c):
+        def in_range(c):
             return 0 <= c < NCH
 
-        def copy_on(eng, dst, src):
-            if eng == "V":
+        def copy_on(engine, dst, src):
+            if engine == "V":
                 nc.vector.tensor_copy(out=dst, in_=src)
             else:
                 nc.scalar.copy(out=dst, in_=src)
 
-        def ld_tri(c):
+        def load_tri(c):
             nc.sync.dma_start(
                 out=traw[:, c * BT * K1:(c + 1) * BT * K1],
                 in_=tri[c * CH:(c + 1) * CH, :].rearrange("(p t) k -> p (t k)", t=BT),
             )
 
-        def ld_w1(g):
+        def load_w1(g):
             for u in range(2):
                 nc.sync.dma_start(
                     out=w1raw[:, 2 * u:2 * u + 2, g * 512:(g + 1) * 512],
                     in_=w1v[256 * u:256 * (u + 1), g * 512:(g + 1) * 512].rearrange("(q e) h -> q e h", e=2),
                 )
 
-        def rw1(g, eng):
+        def regroup_w1(g, engine):
             copy_on(
-                eng,
+                engine,
                 w1g[:, g * 2048:(g + 1) * 2048].rearrange("p (t q j) -> p t q j", t=4, q=P, j=4),
                 w1raw[:, :, g * 512:(g + 1) * 512].rearrange("p j (q t) -> p t q j", t=4),
             )
 
-        def qw1(g):
+        def quantise_w1(g):
             nc.vector.quantize_mx(
                 out=w1c[:, g * 512:(g + 1) * 512].bitcast(FP8X4),
                 scales=w1s[:, g * 512:(g + 1) * 512],
                 in_=w1g[:, g * 2048:(g + 1) * 2048],
             )
 
-        def rw2():
-            w2g = wgpool.tile([P, 2, D, 4], BF16, name="w2g", tag="wg", align_bytes=64)
-            live["w2g"] = w2g
-            for g in range(2):
-                nc.gpsimd.tensor_scalar(
-                    out=w2g[:, g, :, :], in0=w2raw[:, g, :, :].rearrange("p t d -> p d t"),
-                    scalar1=1.0, scalar2=0.0, op0=ALU.mult, op1=ALU.add,
-                )
+        def regroup_w2(g):
+            nc.vector.tensor_copy(out=w2g[:, g, :, :], in_=w2raw[:, g, :, :].rearrange("p t d -> p d t"))
 
-        def qw2():
+        def quantise_w2():
             nc.vector.quantize_mx(
-                out=w2c[:].bitcast(FP8X4), scales=w2s[:], in_=live["w2g"][:].rearrange("p g d t -> p (g d t)"),
+                out=w2c[:].bitcast(FP8X4), scales=w2s[:], in_=w2g[:].rearrange("p g d t -> p (g d t)"),
             )
 
-        def spread():
+        def spread_vectors():
             pbt = py.tile([P, D], F32, name="pbt", tag="y")
             nc.tensor.matmul(out=pbt[:], lhsT=ones[:], rhs=vec[:, 0:D], start=True, stop=True)
             nc.tensor.matmul(out=gam, lhsT=ones[:], rhs=vec[:, D:2 * D], start=True, stop=True)
             nc.tensor.matmul(out=bet, lhsT=ones[:], rhs=vec[:, 2 * D:3 * D], start=True, stop=True)
             live["pb"] = pbt
 
-        def op_t(c, hf, bank="tr"):
-            if not ok(c):
+        def transpose_tri(c, pair, bank="tr"):
+            if not in_range(c):
                 return
             words = traw[:, c * BT * K1:(c + 1) * BT * K1].bitcast(F32)
             trp = banks[bank].tile([P, 2, 256], F32, name="trp", tag=bank)
-            live["trp", c, hf] = trp
+            live["trp", c, pair] = trp
             for j in range(2):
-                t = 2 * hf + j
+                t = 2 * pair + j
                 for u in range(2):
                     nc.tensor.transpose(
                         trp[:, u, j * P:(j + 1) * P],
@@ -143,24 +137,24 @@ def tile_patchwork_t_kernel(tc, tri, W1, b1, W2, b2, gamma, beta, out):
                         ident[:],
                     )
 
-        def op_a(c, hf, eng):
-            if not ok(c):
+        def copy_tri(c, pair, engine):
+            if not in_range(c):
                 return
-            if hf == 0:
+            if pair == 0:
                 live["tg", c] = tgpool.tile([P, 2 * CH], F32, name="tg", tag="tg", align_bytes=64)
-            dst = live["tg", c][:, hf * 512:(hf + 1) * 512].rearrange("p (w u) -> p w u", u=2)
-            copy_on(eng, dst, live["trp", c, hf][:].rearrange("p u w -> p w u"))
+            dst = live["tg", c][:, pair * 512:(pair + 1) * 512].rearrange("p (w u) -> p w u", u=2)
+            copy_on(engine, dst, live["trp", c, pair][:].rearrange("p u w -> p w u"))
 
-        def op_qt(c):
-            if not ok(c):
+        def quantise_tri(c):
+            if not in_range(c):
                 return
             tcod = tcpool.tile([P, CH], U32, name="tcod", tag="tcod", align_bytes=64)
             tscl = tcpool.tile([P, CH], U8, name="tscl", tag="tscl", align_bytes=64)
             nc.vector.quantize_mx(out=tcod[:].bitcast(FP8X4), scales=tscl[:], in_=live["tg", c][:].bitcast(BF16))
             live["tq", c] = (tcod, tscl)
 
-        def op_mm1(c, m):
-            if not ok(c):
+        def layer1(c, m):
+            if not in_range(c):
                 return
             tcod, tscl = live["tq", c]
             hp = ph.tile([P, CH], F32, name="hp", tag="h")
@@ -175,31 +169,25 @@ def tile_patchwork_t_kernel(tc, tri, W1, b1, W2, b2, gamma, beta, out):
                 stop=True,
             )
 
-        def op_h1(c, m, eng="S"):
-            if not ok(c):
+        def relu(c, m):
+            if not in_range(c):
                 return
             g, t = divmod(m, 4)
             if t == 0:
                 live["r", c, g] = rpool.tile([P, 4, CH], F32, name="r", tag="r")
-            if eng == "V":
-                nc.vector.tensor_scalar(
-                    out=live["r", c, g][:, t, :], in0=live["hp", c, m][:], scalar1=b1f[:, m:m + 1], scalar2=0.0,
-                    op0=ALU.add, op1=ALU.max,
-                )
-            else:
-                nc.scalar.activation(
-                    out=live["r", c, g][:, t, :], in_=live["hp", c, m][:], func=ACT.Relu, bias=b1f[:, m:m + 1], scale=1.0,
-                )
+            nc.scalar.activation(
+                out=live["r", c, g][:, t, :], in_=live["hp", c, m][:], func=ACT.Relu, bias=b1f[:, m:m + 1], scale=1.0,
+            )
 
-        def op_h2(c, g, w0, w1, eng):
-            if not ok(c):
+        def square(c, g, w0, w1, engine):
+            if not in_range(c):
                 return
             if ("hb", c, g) not in live:
                 pool = hpool0 if g == 0 else hpool1
                 live["hb", c, g] = pool.tile([P, CH, 4], BF16, name="hb%d" % g, tag="hb%d" % g, align_bytes=64)
             hb = live["hb", c, g]
             r = live["r", c, g]
-            if eng == "S":
+            if engine == "S":
                 nc.scalar.activation(
                     out=hb[:, w0:w1, :].rearrange("p (c i) t -> p c t i", i=4),
                     in_=r[:, :, w0:w1].rearrange("p t (c i) -> p c t i", i=4),
@@ -207,13 +195,13 @@ def tile_patchwork_t_kernel(tc, tri, W1, b1, W2, b2, gamma, beta, out):
                 )
             else:
                 src = r[:, :, w0:w1].rearrange("p t w -> p w t")
-                if eng == "V":
+                if engine == "V":
                     nc.vector.tensor_tensor(out=hb[:, w0:w1, :], in0=src, in1=src, op=ALU.mult)
                 else:
                     nc.gpsimd.tensor_tensor(out=hb[:, w0:w1, :], in0=src, in1=src, op=ALU.mult)
 
-        def op_qh(c, g):
-            if not ok(c):
+        def quantise_h(c, g):
+            if not in_range(c):
                 return
             hcod = cpool.tile([P, CH], U32, name="hcod%d" % g, tag="hcod%d" % g, align_bytes=64)
             hscl = cpool.tile([P, CH], U8, name="hscl%d" % g, tag="hscl%d" % g, align_bytes=64)
@@ -222,8 +210,8 @@ def tile_patchwork_t_kernel(tc, tri, W1, b1, W2, b2, gamma, beta, out):
                 out=hcod[:].bitcast(FP8X4), scales=hscl[:], in_=live["hb", c, g][:].rearrange("p w t -> p (w t)"),
             )
 
-        def op_mm2(c, t, bank="y"):
-            if not ok(c):
+        def layer2(c, t, bank="y"):
+            if not in_range(c):
                 return
             yp = banks[bank].tile([P, D], F32, name="yp", tag=bank)
             live["yp", c, t] = yp
@@ -244,8 +232,8 @@ def tile_patchwork_t_kernel(tc, tri, W1, b1, W2, b2, gamma, beta, out):
                 live[name, c] = spool.tile([P, BT], F32, name=name, tag=name)
             return live[name, c]
 
-        def op_l1(c, t):
-            if not ok(c):
+        def add_b2(c, t):
+            if not in_range(c):
                 return
             if t == 0:
                 live["y", c] = ypool.tile([P, BT, D], F32, name="y", tag="y")
@@ -254,35 +242,35 @@ def tile_patchwork_t_kernel(tc, tri, W1, b1, W2, b2, gamma, beta, out):
                 op0=ALU.add, op1=ALU.add, accum_out=stat("sums", c)[:, t:t + 1],
             )
 
-        def op_nm(c, t0):
-            if not ok(c):
+        def neg_mean(c, t0):
+            if not in_range(c):
                 return
             nc.scalar.activation(
                 out=stat("negmu", c)[:, t0:t0 + 2], in_=stat("sums", c)[:, t0:t0 + 2], func=ACT.Copy, scale=-1.0 / D,
             )
 
-        def op_l2(c, t):
-            if not ok(c):
+        def sum_squares(c, t):
+            if not in_range(c):
                 return
             nc.scalar.activation(
                 out=junk[:], in_=live["y", c][:, t, :], func=ACT.Square, bias=stat("sums", c)[:, t:t + 1], scale=-float(D),
                 accum_out=stat("ssq", c)[:, t:t + 1],
             )
 
-        def op_sq(c):
-            if not ok(c):
+        def std_dev(c):
+            if not in_range(c):
                 return
             nc.scalar.activation(
                 out=stat("std", c)[:], in_=stat("ssq", c)[:], func=ACT.Sqrt, bias=epst[:, 0:1], scale=1.0 / (D * D * D),
             )
 
-        def op_rc(c):
-            if not ok(c):
+        def inv_std(c):
+            if not in_range(c):
                 return
             nc.vector.reciprocal(out=stat("rstd", c)[:], in_=stat("std", c)[:])
 
-        def op_l3(c, t):
-            if not ok(c):
+        def centre_gamma(c, t):
+            if not in_range(c):
                 return
             if ("o", c) not in live:
                 live["o", c] = opool.tile([P, BT, D], F32, name="o", tag="o")
@@ -291,8 +279,8 @@ def tile_patchwork_t_kernel(tc, tri, W1, b1, W2, b2, gamma, beta, out):
                 op0=ALU.add, op1=ALU.mult,
             )
 
-        def op_l4(c, t):
-            if not ok(c):
+        def scale_beta(c, t):
+            if not in_range(c):
                 return
             o = live["o", c]
             nc.vector.scalar_tensor_tensor(
@@ -300,26 +288,25 @@ def tile_patchwork_t_kernel(tc, tri, W1, b1, W2, b2, gamma, beta, out):
                 op0=ALU.mult, op1=ALU.add,
             )
 
-        def op_l4_sg(c, t):
+        def scale_beta_without_vector(c, t):
             o = live["o", c]
             nc.scalar.activation(out=o[:, t, :], in_=o[:, t, :], func=ACT.Copy, scale=stat("rstd", c)[:, t:t + 1])
             nc.gpsimd.tensor_tensor(out=o[:, t, :], in0=o[:, t, :], in1=betf[:], op=ALU.add)
 
-        def op_st(c, t0, t1):
-            if not ok(c):
+        def store(c, t0, t1):
+            if not in_range(c):
                 return
             nc.sync.dma_start(
                 out=out[c * CH:(c + 1) * CH, :].rearrange("(p t) d -> p t d", t=BT)[:, t0:t1, :],
                 in_=live["o", c][:, t0:t1, :],
             )
 
-        ld_tri(0)
-        ld_w1(0)
-        ld_tri(1)
-        ld_w1(1)
+        load_tri(0)
+        load_w1(0)
+        load_w1(1)
         nc.sync.dma_start(out=w2raw[:], in_=w2v.rearrange("(g p t) d -> p g t d", g=2, t=4))
-        for c in range(2, NCH):
-            ld_tri(c)
+        for c in range(1, NCH):
+            load_tri(c)
         nc.vector.memset(vec[:], 0.0)
         nc.scalar.dma_start(out=b1raw[:], in_=b1.rearrange("o (g p t) -> p (o g) t", g=2, t=4))
         for j, v in enumerate((b2, gamma, beta)):
@@ -328,113 +315,111 @@ def tile_patchwork_t_kernel(tc, tri, W1, b1, W2, b2, gamma, beta, out):
         nc.vector.memset(ones[:], 1.0)
         nc.scalar.activation(out=warm[:], in_=epst[:], func=ACT.Sqrt)
 
-        op_t(0, 0, "h")
-        op_t(0, 1, "h")
-        rw1(0, "V")
-        op_a(0, 0, "S")
-        op_a(0, 1, "S")
+        transpose_tri(0, 0, "h")
+        transpose_tri(0, 1, "h")
+        regroup_w1(0, "V")
+        copy_tri(0, 0, "S")
+        copy_tri(0, 1, "S")
         nc.vector.tensor_copy(out=b1f[:], in_=b1raw[:].rearrange("p g t -> p (g t)"))
-        qw1(0)
-        op_qt(0)
-        op_t(1, 0)
-        op_t(1, 1, "y")
+        quantise_w1(0)
+        quantise_tri(0)
         for m in range(4):
-            op_mm1(0, m)
-        op_a(1, 0, "S")
-        op_a(1, 1, "S")
-        rw1(1, "V")
-        op_qt(1)
-        qw1(1)
-        rw2()
-        spread()
-        op_h1(0, 0)
-        op_mm1(0, 4)
-        op_t(2, 0)
-        for m in range(1, 4):
-            op_h1(0, m)
-            op_mm1(0, 4 + m)
+            layer1(0, m)
+        regroup_w1(1, "S")
+        regroup_w2(0)
+        quantise_w1(1)
+        regroup_w2(1)
+        quantise_w2()
+        transpose_tri(1, 0)
+        transpose_tri(1, 1, "y")
+        spread_vectors()
+        for m in range(4):
+            relu(0, m)
+            layer1(0, 4 + m)
+        copy_tri(1, 0, "S")
+        copy_tri(1, 1, "S")
+        quantise_tri(1)
+        transpose_tri(2, 0)
+        for m in range(4):
+            relu(0, 4 + m)
+            layer1(1, m)
         nc.vector.tensor_copy(out=b2b[:], in_=live["pb"][:])
-        op_t(2, 1, "y")
-        op_h2(0, 0, 0, CH, "S")
-        for m in range(2):
-            op_h1(0, 4 + m, "V")
-            op_mm1(1, m)
-        op_a(2, 0, "V")
-        op_t(3, 0)
-        for m in range(2, 4):
-            op_h1(0, 4 + m, "V")
-            op_mm1(1, m)
-        op_a(2, 1, "V")
-        op_h2(0, 1, 0, CH, "S")
-        op_h1(1, 0, "V")
-        op_mm1(1, 4)
-        qw2()
+        square(0, 0, 0, 256, "V")
+        copy_tri(2, 0, "V")
+        transpose_tri(2, 1)
+        square(0, 0, 256, CH, "V")
+        square(0, 1, 0, 256, "S")
+        square(0, 1, 256, CH, "V")
+        relu(1, 0)
+        layer1(1, 4)
+        copy_tri(2, 1, "S")
+        transpose_tri(3, 0)
 
         for c in range(1, NCH + 1):
             last = c == NCH
-            op_qt(c + 1)
-            op_rc(c - 2)
-            op_qh(c - 1, 1)
-            op_qh(c - 1, 0)
+            quantise_tri(c + 1)
+            inv_std(c - 2)
+            quantise_h(c - 1, 1)
+            quantise_h(c - 1, 0)
             for m in range(1, 4):
-                op_h1(c, m)
-                op_mm1(c, 4 + m)
-            op_h2(c, 0, 0, CH, "G")
+                relu(c, m)
+                layer1(c, 4 + m)
+            square(c, 0, 0, CH, "G")
             for j in range(2):
-                op_h1(c, 4 + j)
-                op_mm2(c - 1, j)
-                op_mm1(c + 1, j)
+                relu(c, 4 + j)
+                layer2(c - 1, j)
+                layer1(c + 1, j)
             if last:
-                op_mm2(c - 1, 2, "h")
-                op_mm2(c - 1, 3, "h")
-            op_a(c + 2, 0, "V")
-            op_l4(c - 2, 0)
-            op_l4(c - 2, 1)
-            op_st(c - 2, 0, 2)
+                layer2(c - 1, 2, "h")
+                layer2(c - 1, 3, "h")
+            copy_tri(c + 2, 0, "V")
+            scale_beta(c - 2, 0)
+            scale_beta(c - 2, 1)
+            store(c - 2, 0, 2)
             if last:
                 nc.scalar.copy(out=betf[:], in_=bet)
-                op_l4_sg(c - 2, 2)
-                op_l4_sg(c - 2, 3)
-                op_st(c - 2, 2, 4)
+                scale_beta_without_vector(c - 2, 2)
+                scale_beta_without_vector(c - 2, 3)
+                store(c - 2, 2, 4)
             for j in range(2):
-                op_l1(c - 1, j)
+                add_b2(c - 1, j)
                 if not last:
-                    op_mm2(c - 1, 2 + j)
+                    layer2(c - 1, 2 + j)
             for j in range(2):
-                op_h1(c, 6 + j)
-                op_mm1(c + 1, 2 + j)
-            op_h1(c + 1, 0)
-            op_t(c + 2, 1)
-            op_mm1(c + 1, 4)
-            op_h2(c, 1, CH - GCOLS, CH, "G")
-            op_h2(c, 1, 0, CH - GCOLS, "S")
+                relu(c, 6 + j)
+                layer1(c + 1, 2 + j)
+            relu(c + 1, 0)
+            transpose_tri(c + 2, 1)
+            layer1(c + 1, 4)
+            square(c, 1, CH - GCOLS, CH, "G")
+            square(c, 1, 0, CH - GCOLS, "S")
             if not last:
-                op_l4(c - 2, 2)
-                op_l4(c - 2, 3)
-                op_st(c - 2, 2, 4)
-            op_l1(c - 1, 2)
-            op_l1(c - 1, 3)
-            op_l2(c - 1, 0)
-            op_nm(c - 1, 0)
-            op_l2(c - 1, 1)
-            op_l2(c - 1, 2)
-            op_nm(c - 1, 2)
-            op_l2(c - 1, 3)
-            op_a(c + 2, 1, "S")
-            op_sq(c - 1)
-            op_t(c + 3, 0)
+                scale_beta(c - 2, 2)
+                scale_beta(c - 2, 3)
+                store(c - 2, 2, 4)
+            add_b2(c - 1, 2)
+            add_b2(c - 1, 3)
+            sum_squares(c - 1, 0)
+            neg_mean(c - 1, 0)
+            sum_squares(c - 1, 1)
+            sum_squares(c - 1, 2)
+            neg_mean(c - 1, 2)
+            sum_squares(c - 1, 3)
+            copy_tri(c + 2, 1, "S")
+            std_dev(c - 1)
+            transpose_tri(c + 3, 0)
             if not last:
                 for t in range(BT):
-                    op_l3(c - 1, t)
+                    centre_gamma(c - 1, t)
 
         e = NCH - 1
-        op_l3(e, 0)
-        op_l3(e, 1)
-        op_l3(e, 3)
-        op_rc(e)
-        op_l3(e, 2)
-        op_l4_sg(e, 3)
+        centre_gamma(e, 0)
+        centre_gamma(e, 1)
+        centre_gamma(e, 3)
+        inv_std(e)
+        centre_gamma(e, 2)
+        scale_beta_without_vector(e, 3)
         for t in range(3):
-            op_l4(e, t)
-            op_st(e, t, t + 1)
-        op_st(e, 3, 4)
+            scale_beta(e, t)
+            store(e, t, t + 1)
+        store(e, 3, 4)

from contextlib import ExitStack

import concourse.mybir as mybir
from concourse.masks import make_identity

F32 = mybir.dt.float32
BF16 = mybir.dt.bfloat16
U32 = mybir.dt.uint32
U8 = mybir.dt.uint8
FP8X4 = mybir.dt.float8_e4m3fn_x4
ACT = mybir.ActivationFunctionType
ALU = mybir.AluOpType

P = 128
B, K1, H, D = 4096, 512, 1024, 512
CH = 512
NCH = B // CH
BT = CH // P
LN_EPS = 1e-5
GCOLS = 112

FLOPS = 2 * B * K1 * H + 2 * B * H * D


def tile_patchwork_t_kernel(tc, tri, W1, b1, W2, b2, gamma, beta, out):
    nc = tc.nc
    with ExitStack() as ctx:
        keep = ctx.enter_context(tc.tile_pool(name="keep", bufs=1))
        tgpool = ctx.enter_context(tc.tile_pool(name="tgpool", bufs=2))
        tcpool = ctx.enter_context(tc.tile_pool(name="tcpool", bufs=3))
        rpool = ctx.enter_context(tc.tile_pool(name="rpool", bufs=4))
        hpool0 = ctx.enter_context(tc.tile_pool(name="hpool0", bufs=1))
        hpool1 = ctx.enter_context(tc.tile_pool(name="hpool1", bufs=2))
        cpool = ctx.enter_context(tc.tile_pool(name="cpool", bufs=2))
        ypool = ctx.enter_context(tc.tile_pool(name="ypool", bufs=3))
        opool = ctx.enter_context(tc.tile_pool(name="opool", bufs=3))
        spool = ctx.enter_context(tc.tile_pool(name="spool", bufs=3))
        pgb = ctx.enter_context(tc.psum_pool(name="pgb", bufs=1))
        ptr = ctx.enter_context(tc.psum_pool(name="ptr", bufs=1))
        ph = ctx.enter_context(tc.psum_pool(name="ph", bufs=4))
        py = ctx.enter_context(tc.psum_pool(name="py", bufs=2))
        banks = {"tr": ptr, "h": ph, "y": py}

        traw = keep.tile([P, NCH * BT * K1], BF16, name="traw")
        w1raw = keep.tile([P, 4, H], BF16, name="w1raw")
        w2raw = keep.tile([P, 2, 4, D], BF16, name="w2raw")
        b1raw = keep.tile([P, 2, 4], BF16, name="b1raw")
        b1f = keep.tile([P, 8], F32, name="b1f")
        vec = keep.tile([P, 3 * D], BF16, name="vec")
        ones = keep.tile([P, P], BF16, name="ones")
        ident = keep.tile([P, P], F32, name="ident")
        epst = keep.tile([P, 1], F32, name="epst")
        warm = keep.tile([P, 1], F32, name="warm")
        b2b = keep.tile([P, D], F32, name="b2b")
        betf = keep.tile([P, D], F32, name="betf")
        junk = keep.tile([P, D], BF16, name="junk")
        w1g = keep.tile([P, 4 * H], BF16, name="w1g", align_bytes=64)
        w1c = keep.tile([P, H], U32, name="w1c", align_bytes=64)
        w1s = keep.tile([P, H], U8, name="w1s", align_bytes=64)
        w2g = keep.tile([P, 2, D, 4], BF16, name="w2g", align_bytes=64)
        w2c = keep.tile([P, 2 * D], U32, name="w2c", align_bytes=64)
        w2s = keep.tile([P, 2 * D], U8, name="w2s", align_bytes=64)
        gb = pgb.tile([P, 2 * D], BF16, name="gb")
        gam = gb[:, 0:D]
        bet = gb[:, D:2 * D]

        make_identity(nc, ident[:])
        ctx.enter_context(tc.manual_schedule())

        w1v = W1.rearrange("o k h -> (o k) h")
        w2v = W2.rearrange("o k d -> (o k) d")
        live = {}

        def in_range(c):
            return 0 <= c < NCH

        def copy_on(engine, dst, src):
            if engine == "V":
                nc.vector.tensor_copy(out=dst, in_=src)
            else:
                nc.scalar.copy(out=dst, in_=src)

        def load_tri(c):
            nc.sync.dma_start(
                out=traw[:, c * BT * K1:(c + 1) * BT * K1],
                in_=tri[c * CH:(c + 1) * CH, :].rearrange("(p t) k -> p (t k)", t=BT),
            )

        def load_w1(g):
            for u in range(2):
                nc.sync.dma_start(
                    out=w1raw[:, 2 * u:2 * u + 2, g * 512:(g + 1) * 512],
                    in_=w1v[256 * u:256 * (u + 1), g * 512:(g + 1) * 512].rearrange("(q e) h -> q e h", e=2),
                )

        def regroup_w1(g, engine):
            copy_on(
                engine,
                w1g[:, g * 2048:(g + 1) * 2048].rearrange("p (t q j) -> p t q j", t=4, q=P, j=4),
                w1raw[:, :, g * 512:(g + 1) * 512].rearrange("p j (q t) -> p t q j", t=4),
            )

        def quantise_w1(g):
            nc.vector.quantize_mx(
                out=w1c[:, g * 512:(g + 1) * 512].bitcast(FP8X4),
                scales=w1s[:, g * 512:(g + 1) * 512],
                in_=w1g[:, g * 2048:(g + 1) * 2048],
            )

        def regroup_w2(g):
            nc.vector.tensor_copy(out=w2g[:, g, :, :], in_=w2raw[:, g, :, :].rearrange("p t d -> p d t"))

        def quantise_w2():
            nc.vector.quantize_mx(
                out=w2c[:].bitcast(FP8X4), scales=w2s[:], in_=w2g[:].rearrange("p g d t -> p (g d t)"),
            )

        def spread_vectors():
            pbt = py.tile([P, D], F32, name="pbt", tag="y")
            nc.tensor.matmul(out=pbt[:], lhsT=ones[:], rhs=vec[:, 0:D], start=True, stop=True)
            nc.tensor.matmul(out=gam, lhsT=ones[:], rhs=vec[:, D:2 * D], start=True, stop=True)
            nc.tensor.matmul(out=bet, lhsT=ones[:], rhs=vec[:, 2 * D:3 * D], start=True, stop=True)
            live["pb"] = pbt

        def transpose_tri(c, pair, bank="tr"):
            if not in_range(c):
                return
            words = traw[:, c * BT * K1:(c + 1) * BT * K1].bitcast(F32)
            trp = banks[bank].tile([P, 2, 256], F32, name="trp", tag=bank)
            live["trp", c, pair] = trp
            for j in range(2):
                t = 2 * pair + j
                for u in range(2):
                    nc.tensor.transpose(
                        trp[:, u, j * P:(j + 1) * P],
                        words[:, t * 256 + u * P:t * 256 + (u + 1) * P],
                        ident[:],
                    )

        def copy_tri(c, pair, engine):
            if not in_range(c):
                return
            if pair == 0:
                live["tg", c] = tgpool.tile([P, 2 * CH], F32, name="tg", tag="tg", align_bytes=64)
            dst = live["tg", c][:, pair * 512:(pair + 1) * 512].rearrange("p (w u) -> p w u", u=2)
            copy_on(engine, dst, live["trp", c, pair][:].rearrange("p u w -> p w u"))

        def quantise_tri(c):
            if not in_range(c):
                return
            tcod = tcpool.tile([P, CH], U32, name="tcod", tag="tcod", align_bytes=64)
            tscl = tcpool.tile([P, CH], U8, name="tscl", tag="tscl", align_bytes=64)
            nc.vector.quantize_mx(out=tcod[:].bitcast(FP8X4), scales=tscl[:], in_=live["tg", c][:].bitcast(BF16))
            live["tq", c] = (tcod, tscl)

        def layer1(c, m):
            if not in_range(c):
                return
            tcod, tscl = live["tq", c]
            hp = ph.tile([P, CH], F32, name="hp", tag="h")
            live["hp", c, m] = hp
            nc.tensor.matmul_mx(
                out=hp[:],
                lhsT=w1c[:, m * P:(m + 1) * P].bitcast(FP8X4),
                lhsT_scale=w1s[:, m * P:(m + 1) * P],
                rhs=tcod[:].bitcast(FP8X4),
                rhs_scale=tscl[:],
                start=True,
                stop=True,
            )

        def relu(c, m):
            if not in_range(c):
                return
            g, t = divmod(m, 4)
            if t == 0:
                live["r", c, g] = rpool.tile([P, 4, CH], F32, name="r", tag="r")
            nc.scalar.activation(
                out=live["r", c, g][:, t, :], in_=live["hp", c, m][:], func=ACT.Relu, bias=b1f[:, m:m + 1], scale=1.0,
            )

        def square(c, g, w0, w1, engine):
            if not in_range(c):
                return
            if ("hb", c, g) not in live:
                pool = hpool0 if g == 0 else hpool1
                live["hb", c, g] = pool.tile([P, CH, 4], BF16, name="hb%d" % g, tag="hb%d" % g, align_bytes=64)
            hb = live["hb", c, g]
            r = live["r", c, g]
            if engine == "S":
                nc.scalar.activation(
                    out=hb[:, w0:w1, :].rearrange("p (c i) t -> p c t i", i=4),
                    in_=r[:, :, w0:w1].rearrange("p t (c i) -> p c t i", i=4),
                    func=ACT.Square,
                )
            else:
                src = r[:, :, w0:w1].rearrange("p t w -> p w t")
                if engine == "V":
                    nc.vector.tensor_tensor(out=hb[:, w0:w1, :], in0=src, in1=src, op=ALU.mult)
                else:
                    nc.gpsimd.tensor_tensor(out=hb[:, w0:w1, :], in0=src, in1=src, op=ALU.mult)

        def quantise_h(c, g):
            if not in_range(c):
                return
            hcod = cpool.tile([P, CH], U32, name="hcod%d" % g, tag="hcod%d" % g, align_bytes=64)
            hscl = cpool.tile([P, CH], U8, name="hscl%d" % g, tag="hscl%d" % g, align_bytes=64)
            live["hq", c, g] = (hcod, hscl)
            nc.vector.quantize_mx(
                out=hcod[:].bitcast(FP8X4), scales=hscl[:], in_=live["hb", c, g][:].rearrange("p w t -> p (w t)"),
            )

        def layer2(c, t, bank="y"):
            if not in_range(c):
                return
            yp = banks[bank].tile([P, D], F32, name="yp", tag=bank)
            live["yp", c, t] = yp
            for g in range(2):
                hcod, hscl = live["hq", c, g]
                nc.tensor.matmul_mx(
                    out=yp[:],
                    lhsT=hcod[:, t * P:(t + 1) * P].bitcast(FP8X4),
                    lhsT_scale=hscl[:, t * P:(t + 1) * P],
                    rhs=w2c[:, g * D:(g + 1) * D].bitcast(FP8X4),
                    rhs_scale=w2s[:, g * D:(g + 1) * D],
                    start=(g == 0),
                    stop=(g == 1),
                )

        def stat(name, c):
            if (name, c) not in live:
                live[name, c] = spool.tile([P, BT], F32, name=name, tag=name)
            return live[name, c]

        def add_b2(c, t):
            if not in_range(c):
                return
            if t == 0:
                live["y", c] = ypool.tile([P, BT, D], F32, name="y", tag="y")
            nc.vector.scalar_tensor_tensor(
                out=live["y", c][:, t, :], in0=live["yp", c, t][:], scalar=0.0, in1=b2b[:],
                op0=ALU.add, op1=ALU.add, accum_out=stat("sums", c)[:, t:t + 1],
            )

        def neg_mean(c, t0):
            if not in_range(c):
                return
            nc.scalar.activation(
                out=stat("negmu", c)[:, t0:t0 + 2], in_=stat("sums", c)[:, t0:t0 + 2], func=ACT.Copy, scale=-1.0 / D,
            )

        def sum_squares(c, t):
            if not in_range(c):
                return
            nc.scalar.activation(
                out=junk[:], in_=live["y", c][:, t, :], func=ACT.Square, bias=stat("sums", c)[:, t:t + 1], scale=-float(D),
                accum_out=stat("ssq", c)[:, t:t + 1],
            )

        def std_dev(c):
            if not in_range(c):
                return
            nc.scalar.activation(
                out=stat("std", c)[:], in_=stat("ssq", c)[:], func=ACT.Sqrt, bias=epst[:, 0:1], scale=1.0 / (D * D * D),
            )

        def inv_std(c):
            if not in_range(c):
                return
            nc.vector.reciprocal(out=stat("rstd", c)[:], in_=stat("std", c)[:])

        def centre_gamma(c, t):
            if not in_range(c):
                return
            if ("o", c) not in live:
                live["o", c] = opool.tile([P, BT, D], F32, name="o", tag="o")
            nc.vector.scalar_tensor_tensor(
                out=live["o", c][:, t, :], in0=live["y", c][:, t, :], scalar=stat("negmu", c)[:, t:t + 1], in1=gam,
                op0=ALU.add, op1=ALU.mult,
            )

        def scale_beta(c, t):
            if not in_range(c):
                return
            o = live["o", c]
            nc.vector.scalar_tensor_tensor(
                out=o[:, t, :], in0=o[:, t, :], scalar=stat("rstd", c)[:, t:t + 1], in1=bet,
                op0=ALU.mult, op1=ALU.add,
            )

        def scale_beta_without_vector(c, t):
            o = live["o", c]
            nc.scalar.activation(out=o[:, t, :], in_=o[:, t, :], func=ACT.Copy, scale=stat("rstd", c)[:, t:t + 1])
            nc.gpsimd.tensor_tensor(out=o[:, t, :], in0=o[:, t, :], in1=betf[:], op=ALU.add)

        def store(c, t0, t1):
            if not in_range(c):
                return
            nc.sync.dma_start(
                out=out[c * CH:(c + 1) * CH, :].rearrange("(p t) d -> p t d", t=BT)[:, t0:t1, :],
                in_=live["o", c][:, t0:t1, :],
            )

        load_tri(0)
        load_w1(0)
        load_w1(1)
        nc.sync.dma_start(out=w2raw[:], in_=w2v.rearrange("(g p t) d -> p g t d", g=2, t=4))
        for c in range(1, NCH):
            load_tri(c)
        nc.vector.memset(vec[:], 0.0)
        nc.scalar.dma_start(out=b1raw[:], in_=b1.rearrange("o (g p t) -> p (o g) t", g=2, t=4))
        for j, v in enumerate((b2, gamma, beta)):
            nc.scalar.dma_start(out=vec[0:1, j * D:(j + 1) * D], in_=v)
        nc.vector.memset(epst[:], LN_EPS)
        nc.vector.memset(ones[:], 1.0)
        nc.scalar.activation(out=warm[:], in_=epst[:], func=ACT.Sqrt)

        transpose_tri(0, 0, "h")
        transpose_tri(0, 1, "h")
        regroup_w1(0, "V")
        copy_tri(0, 0, "S")
        copy_tri(0, 1, "S")
        nc.vector.tensor_copy(out=b1f[:], in_=b1raw[:].rearrange("p g t -> p (g t)"))
        quantise_w1(0)
        quantise_tri(0)
        for m in range(4):
            layer1(0, m)
        regroup_w1(1, "S")
        regroup_w2(0)
        quantise_w1(1)
        regroup_w2(1)
        quantise_w2()
        transpose_tri(1, 0)
        transpose_tri(1, 1, "y")
        spread_vectors()
        for m in range(4):
            relu(0, m)
            layer1(0, 4 + m)
        copy_tri(1, 0, "S")
        copy_tri(1, 1, "S")
        quantise_tri(1)
        transpose_tri(2, 0)
        for m in range(4):
            relu(0, 4 + m)
            layer1(1, m)
        nc.vector.tensor_copy(out=b2b[:], in_=live["pb"][:])
        square(0, 0, 0, 256, "V")
        copy_tri(2, 0, "V")
        transpose_tri(2, 1)
        square(0, 0, 256, CH, "V")
        square(0, 1, 0, 256, "S")
        square(0, 1, 256, CH, "V")
        relu(1, 0)
        layer1(1, 4)
        copy_tri(2, 1, "S")
        transpose_tri(3, 0)

        for c in range(1, NCH + 1):
            last = c == NCH
            quantise_tri(c + 1)
            inv_std(c - 2)
            quantise_h(c - 1, 1)
            quantise_h(c - 1, 0)
            for m in range(1, 4):
                relu(c, m)
                layer1(c, 4 + m)
            square(c, 0, 0, CH, "G")
            for j in range(2):
                relu(c, 4 + j)
                layer2(c - 1, j)
                layer1(c + 1, j)
            if last:
                layer2(c - 1, 2, "h")
                layer2(c - 1, 3, "h")
            copy_tri(c + 2, 0, "V")
            scale_beta(c - 2, 0)
            scale_beta(c - 2, 1)
            store(c - 2, 0, 2)
            if last:
                nc.scalar.copy(out=betf[:], in_=bet)
                scale_beta_without_vector(c - 2, 2)
                scale_beta_without_vector(c - 2, 3)
                store(c - 2, 2, 4)
            for j in range(2):
                add_b2(c - 1, j)
                if not last:
                    layer2(c - 1, 2 + j)
            for j in range(2):
                relu(c, 6 + j)
                layer1(c + 1, 2 + j)
            relu(c + 1, 0)
            transpose_tri(c + 2, 1)
            layer1(c + 1, 4)
            square(c, 1, CH - GCOLS, CH, "G")
            square(c, 1, 0, CH - GCOLS, "S")
            if not last:
                scale_beta(c - 2, 2)
                scale_beta(c - 2, 3)
                store(c - 2, 2, 4)
            add_b2(c - 1, 2)
            add_b2(c - 1, 3)
            sum_squares(c - 1, 0)
            neg_mean(c - 1, 0)
            sum_squares(c - 1, 1)
            sum_squares(c - 1, 2)
            neg_mean(c - 1, 2)
            sum_squares(c - 1, 3)
            copy_tri(c + 2, 1, "S")
            std_dev(c - 1)
            transpose_tri(c + 3, 0)
            if not last:
                for t in range(BT):
                    centre_gamma(c - 1, t)

        e = NCH - 1
        centre_gamma(e, 0)
        centre_gamma(e, 1)
        centre_gamma(e, 3)
        inv_std(e)
        centre_gamma(e, 2)
        scale_beta_without_vector(e, 3)
        for t in range(3):
            scale_beta(e, t)
            store(e, t, t + 1)
        store(e, 3, 4)
